import numpy as np
import ml_dtypes


def mxq(x, axis, fmt="e4m3"):
    dtype, down = {"e4m3": (ml_dtypes.float8_e4m3fn, 7), "e5m2": (ml_dtypes.float8_e5m2, 14)}[fmt]
    v = np.moveaxis(np.asarray(x, np.float32).astype(ml_dtypes.bfloat16).astype(np.float64), axis, -1)
    blocks = v.reshape(v.shape[:-1] + (-1, 32))
    amax = np.abs(blocks).max(-1, keepdims=True)
    byte = np.maximum(np.where(amax > 0, np.frexp(amax)[1] - 1 + 127, 0) - down, 1)
    scale = np.exp2(byte - 127.0)
    codes = (blocks / scale).astype(np.float32).astype(dtype).astype(np.float64)
    return np.moveaxis((codes * scale).reshape(v.shape), -1, axis)


BF16 = ml_dtypes.bfloat16


def bf(x):
    return np.asarray(x, np.float32).astype(BF16)


def f64(x):
    return np.asarray(x).astype(np.float64)


B, C, H, W, O, K, S, P = 2, 512, 32, 32, 128, 3, 1, 1
KD = C * K * K


def unfold(x, k, s, p):
    b, c, h, w = x.shape
    ho = (h + 2 * p - k) // s + 1
    wo = (w + 2 * p - k) // s + 1
    xp = np.pad(x, ((0, 0), (0, 0), (p, p), (p, p)))
    pats = np.stack([xp[:, :, i:i + s * ho:s, j:j + s * wo:s] for i in range(k) for j in range(k)], axis=2)
    return pats.reshape(b, c * k * k, ho * wo), ho, wo


def setup_inputs():
    mu = np.random.standard_normal(C)
    g = np.random.standard_normal(O)
    x = (mu[None, :, None, None] + np.random.standard_normal((B, C, H, W))) / np.sqrt(KD)
    weight = (g[:, None] * np.repeat(mu, K * K)[None, :] + np.random.standard_normal((O, KD))) / np.sqrt(KD)
    return {"x": bf(x), "weight": bf(weight)}


def reference(x, weight):
    x, weight = f64(x), f64(weight)
    pats, ho, wo = unfold(x, K, S, P)
    x2 = np.sum(pats * pats, axis=1)
    w2 = np.sum(weight * weight, axis=1)
    pt = pats.reshape(B, C, K * K, ho * wo).transpose(0, 2, 1, 3).reshape(B, KD, ho * wo)
    wt = weight.reshape(O, C, K * K).transpose(0, 2, 1).reshape(O, KD)
    xw = mxq(wt, 1, "e4m3") @ mxq(pt, 1, "e4m3")
    d2 = np.maximum(x2[:, None, :] + w2[None, :, None] - 2.0 * xw, 0.0)
    return d2.reshape(B, O, ho, wo)

@@ -1,0 +1,189 @@
+from contextlib import ExitStack
+
+import concourse.mybir as mybir
+from concourse.masks import make_identity
+
+FLOPS = 2 * 2048 * 128 * 4608
+
+F32 = mybir.dt.float32
+BF16 = mybir.dt.bfloat16
+U32 = mybir.dt.uint32
+U8 = mybir.dt.uint8
+FP8X4 = mybir.dt.float8_e4m3fn_x4
+ALU = mybir.AluOpType
+ACT = mybir.ActivationFunctionType
+
+P = 128
+B = 2
+HW = 1024
+KD = 4608
+ROWS = 18
+XCOLS = ROWS * 64
+
+
+def tile_rbf_conv2d_kernel(tc, x, weight, out):
+    nc = tc.nc
+    with ExitStack() as ctx:
+        const = ctx.enter_context(tc.tile_pool(name="const", bufs=1))
+        keep = ctx.enter_context(tc.tile_pool(name="keep", bufs=1))
+        junkp = ctx.enter_context(tc.tile_pool(name="junkp", bufs=2))
+        ps_t = ctx.enter_context(tc.psum_pool(name="ps_t", bufs=3))
+        ps_m = ctx.enter_context(tc.psum_pool(name="ps_m", bufs=3))
+        ps_b = ctx.enter_context(tc.psum_pool(name="ps_b", bufs=2))
+
+        w_raw = keep.tile([P, KD], BF16, name="w_raw")
+        nc.sync.dma_start(out=w_raw[:], in_=weight)
+        raws = []
+        for b in range(B):
+            raw = keep.tile([P, 4, HW], BF16, name="raw%d" % b)
+            nc.sync.dma_start(out=raw[:], in_=x[b].rearrange("(p j) h w -> p j (h w)", j=4))
+            raws.append(raw)
+
+        ident = const.tile([P, P], F32, name="ident")
+        make_identity(nc, ident[:])
+        ident_bf = const.tile([P, P], BF16, name="ident_bf")
+        nc.vector.tensor_copy(out=ident_bf[:], in_=ident[:])
+        id3 = ident[:].rearrange("p (a z) -> p a z", z=32)
+        tri = const.tile([P, 4, 32], F32, name="tri")
+        nc.vector.tensor_copy(out=tri[:], in_=id3)
+        nc.vector.tensor_tensor(out=tri[:, :, 1:32], in0=tri[:, :, 1:32], in1=id3[:, :, 0:31], op=ALU.add)
+        nc.vector.tensor_tensor(out=tri[:, :, 0:31], in0=tri[:, :, 0:31], in1=id3[:, :, 1:32], op=ALU.add)
+        band = const.tile([P, 3 * P], F32, name="band")
+        nc.vector.memset(band[:], 0.0)
+        for dy in (-1, 0, 1):
+            lo = P + 32 * dy
+            nc.vector.tensor_tensor(
+                out=band[:, lo:lo + P], in0=band[:, lo:lo + P],
+                in1=tri[:].rearrange("p a z -> p (a z)"), op=ALU.add,
+            )
+        s_pad = keep.tile([P, B, 10], F32, name="s_pad")
+        nc.vector.memset(s_pad[:], 0.0)
+        x2sb = keep.tile([P, B * 8], F32, name="x2sb")
+
+        grps = []
+        for b in range(B):
+            grp = keep.tile([P, XCOLS * 4], BF16, name="grp%d" % b, align_bytes=64)
+            g4 = grp[:].rearrange("p (r h n) -> p r h n", r=ROWS, h=2)
+            nc.vector.memset(g4[:, 0, 0, :], 0.0)
+            nc.vector.memset(g4[:, ROWS - 1, 1, :], 0.0)
+            grps.append(grp)
+
+        w2 = keep.tile([P, 1], F32, name="w2")
+        junk_w = keep.tile([P, KD], BF16, name="junk_w")
+        nc.scalar.activation(out=junk_w[:], in_=w_raw[:], func=ACT.Square, accum_out=w2[:])
+
+        w_re = keep.tile([P, KD], BF16, name="w_re")
+        w_dst = w_re[:].rearrange("o (t h p e) -> o t h p e", t=9, h=2, e=2)
+        w_src = w_raw[:].rearrange("o (p h e t) -> o t h p e", h=2, e=2, t=9)
+        w32 = w_re[:].bitcast(F32)
+        w_grp = keep.tile([P, KD], BF16, name="w_grp", align_bytes=64)
+        wg32 = w_grp[:].bitcast(F32).rearrange("p (t o h) -> p t o h", o=P, h=2)
+        w_codes = keep.tile([P, 9 * P], U32, name="w_codes", align_bytes=64)
+        w_scales = keep.tile([P, 9 * P], U8, name="w_scales", align_bytes=64)
+        for k in range(5):
+            n = 4 if k < 4 else 2
+            t0 = 2 * k
+            t1 = t0 + n // 2
+            nc.vector.tensor_copy(out=w_dst[:, t0:t1], in_=w_src[:, t0:t1])
+            wt = ps_t.tile([P, 4, P], F32, name="wt", tag="tp")
+            for m in range(n):
+                c0 = (4 * k + m) * P
+                nc.tensor.transpose(wt[:, m, :], w32[:, c0:c0 + P], ident[:])
+            nc.scalar.copy(
+                out=wg32[:, t0:t1],
+                in_=wt[:, 0:n, :].rearrange("p (a h) o -> p a o h", h=2),
+            )
+        for lo, n in ((0, 2048), (2048, 2048), (4096, 512)):
+            nc.vector.quantize_mx(
+                out=w_codes[:, lo // 4:(lo + n) // 4].bitcast(FP8X4),
+                scales=w_scales[:, lo // 4:(lo + n) // 4],
+                in_=w_grp[:, lo:lo + n],
+            )
+
+        for b in range(B):
+            raw = raws[b]
+            grp = grps[b]
+            g4 = grp[:].rearrange("p (r h n) -> p r h n", r=ROWS, h=2)
+            g6 = grp[:].rearrange("p (r h c i t) -> p r h c i t", r=ROWS, h=2, c=8, i=4, t=4)
+            r5 = raw[:].rearrange("p t (y c i) -> p t y c i", y=32, c=8, i=4)
+            for h in range(2):
+                nc.vector.tensor_copy(
+                    out=g6[:, 1:17, h].rearrange("p r c i t -> p r c t i"),
+                    in_=r5[:, :, 16 * h:16 * h + 16].rearrange("p t y c i -> p y c t i"),
+                )
+            nc.vector.tensor_copy(out=g4[:, ROWS - 1, 0, :], in_=g4[:, 1, 1, :])
+            nc.vector.tensor_copy(out=g4[:, 0, 1, :], in_=g4[:, 16, 0, :])
+            xc = keep.tile([P, XCOLS], U32, name="xc%d" % b, align_bytes=64)
+            xs = keep.tile([P, XCOLS], U8, name="xs%d" % b, align_bytes=64)
+            for lo, n in ((0, 2048), (2048, 2048), (4096, 512)):
+                nc.vector.quantize_mx(
+                    out=xc[:, lo // 4:(lo + n) // 4].bitcast(FP8X4),
+                    scales=xs[:, lo // 4:(lo + n) // 4],
+                    in_=grp[:, lo:lo + n],
+                )
+
+            for ch in range(8):
+                tp = ps_t.tile([P, 4, P], BF16, name="tp", tag="tp")
+                for j in range(4):
+                    nc.tensor.transpose(tp[:, j, :], raw[:, j, ch * P:(ch + 1) * P], ident_bf[:])
+                junk = junkp.tile([P, 4 * P], BF16, name="junk")
+                nc.scalar.activation(
+                    out=junk[:], in_=tp[:].rearrange("p j c -> p (j c)"), func=ACT.Square,
+                    accum_out=s_pad[:, b, 1 + ch:2 + ch],
+                )
+            f = ps_b.tile([P, 8], F32, name="f", tag="xb")
+            for rel in range(3):
+                nc.tensor.matmul(
+                    f[:], lhsT=band[:, rel * P:(rel + 1) * P], rhs=s_pad[:, b, 2 - rel:10 - rel],
+                    start=(rel == 0), stop=(rel == 2),
+                )
+            nc.vector.tensor_copy(out=x2sb[:, 8 * b:8 * b + 8], in_=f[:])
+            acc = keep.tile([P, HW], F32, name="acc%d" % b)
+            acc5 = acc[:].rearrange("p (w y h z) -> p w y h z", w=2, y=8, h=2)
+            for h in range(2):
+                xb = ps_b.tile([P, 512], F32, name="xb", tag="xb")
+                for q in range(4):
+                    col = 8 * b + 4 * h + q
+                    nc.tensor.transpose(
+                        xb[:, q * P:(q + 1) * P], x2sb[:, col:col + 1].to_broadcast([P, P]), ident[:]
+                    )
+                nc.scalar.activation(
+                    out=acc5[:, :, :, h, :],
+                    in_=xb[:].rearrange("p (w y z) -> p w y z", w=2, y=8),
+                    func=ACT.Identity, bias=w2[:, 0:1],
+                )
+
+            res = keep.tile([P, HW], F32, name="res%d" % b)
+            res5 = res[:].rearrange("p (h w y z) -> p w y h z", h=2, w=2, y=8)
+            res4 = res[:].rearrange("p (h w n) -> p h w n", h=2, w=2)
+            out4 = out[b].rearrange("o (h w y) z -> o h w (y z)", h=2, w=2)
+            for w in range(2):
+                a = acc[:, 512 * w:512 * w + 512]
+                a3 = a.rearrange("p (s z) -> p s z", z=32)
+                for j in (1, 0, 2):
+                    pj = ps_m.tile([P, 512], F32, name="pj", tag="mx")
+                    for i in range(3):
+                        tap = 3 * i + j
+                        c0 = 64 * (8 * w + i)
+                        nc.tensor.matmul_mx(
+                            out=pj[:],
+                            lhsT=w_codes[:, tap * P:(tap + 1) * P].bitcast(FP8X4),
+                            lhsT_scale=w_scales[:, tap * P:(tap + 1) * P],
+                            rhs=xc[:, c0:c0 + 512].bitcast(FP8X4),
+                            rhs_scale=xs[:, c0:c0 + 512],
+                            start=(i == 0), stop=(i == 2),
+                        )
+                    p3 = pj[:].rearrange("p (s z) -> p s z", z=32)
+                    if j == 1:
+                        dst, src = a3, p3
+                    elif j == 0:
+                        dst, src = a3[:, :, 1:32], p3[:, :, 0:31]
+                    else:
+                        dst, src = a3[:, :, 0:31], p3[:, :, 1:32]
+                    nc.vector.scalar_tensor_tensor(
+                        out=dst, in0=src, scalar=-2.0, in1=dst, op0=ALU.mult, op1=ALU.add
+                    )
+                nc.scalar.activation(
+                    out=res5[:, w], in_=a.rearrange("p (y h z) -> p y h z", y=8, h=2), func=ACT.Relu
+                )
+                nc.sync.dma_start(out=out4[:, :, w, :], in_=res4[:, :, w, :])

@@ -12,6 +12,7 @@ U8 = mybir.dt.uint8
 FP8X4 = mybir.dt.float8_e4m3fn_x4
 ALU = mybir.AluOpType
 ACT = mybir.ActivationFunctionType
+AX = mybir.AxisListType
 
 P = 128
 B = 2
@@ -19,6 +20,31 @@ HW = 1024
 KD = 4608
 ROWS = 18
 XCOLS = ROWS * 64
+MANUAL = True
+
+PLAN = [
+    ("w2", 0), ("wpre", 0, 0), ("wpre", 0, 1), ("w2", 1), ("wpre", 0, 2),
+    ("wpre", 1, 0), ("w2", 2), ("wpre", 1, 1), ("wT", 0, 0), ("wT", 1, 1),
+    ("wpre", 1, 2), ("wT", 2, 2), ("wT", 3, 3), ("wev", 0), ("xre", 0, 1, 0),
+    ("wT", 4, 4), ("xT", 0, 0, 5), ("wev", 1), ("xT", 0, 1, 6), ("xre", 0, 1, 1),
+    ("wev", 2), ("xT", 0, 2, 7), ("wq", 0), ("wev", 3), ("xT", 0, 3, 0),
+    ("wev", 4), ("wq", 1), ("xT", 1, 0, 1), ("sq", 0, 0), ("xT", 1, 1, 2),
+    ("wq", 2), ("xq", 0, 0), ("sq", 0, 1), ("xT", 1, 2, 3), ("xq", 0, 1),
+    ("xre", 0, 2, 0), ("sq", 0, 2), ("xT", 1, 3, 4), ("xre", 0, 2, 1), ("sq", 0, 3),
+    ("mx", 0, 0, 1, 5), ("xq", 0, 2), ("sq", 0, 4), ("mx", 0, 0, 0, 6), ("xre", 1, 1, 0),
+    ("sq", 0, 5), ("t", 0, 0), ("mx", 0, 0, 2, 7), ("sq", 0, 6), ("stt", 0, 0, 0),
+    ("mx", 0, 1, 1, 5), ("sq", 0, 7), ("stt", 0, 0, 2), ("mx", 0, 1, 0, 6), ("xre", 1, 1, 1),
+    ("sq", 1, 0), ("mx", 0, 1, 2, 7), ("t", 0, 1), ("xq", 1, 0), ("sq", 1, 1),
+    ("xq", 1, 1), ("stt", 0, 1, 0), ("f", 0, 0), ("mx", 1, 0, 1, 5), ("sq", 1, 2),
+    ("stt", 0, 1, 2), ("sq", 1, 3), ("xre", 1, 2, 0), ("mx", 1, 0, 0, 1), ("xre", 1, 2, 1),
+    ("sq", 1, 4), ("mx", 1, 0, 2, 6), ("xq", 1, 2), ("t", 1, 0), ("x2c", 0),
+    ("sq", 1, 5), ("bc", 0, 0, 7), ("bc", 0, 1, 2), ("sq", 1, 6), ("sx", 0, 0),
+    ("mx", 1, 1, 1, 5), ("sx", 0, 1), ("sq", 1, 7), ("mx", 1, 1, 0, 0), ("stt", 1, 0, 0),
+    ("w2", 3), ("stt", 1, 0, 2), ("f", 1, 3), ("mx", 1, 1, 2, 7), ("x2c", 1), ("w2r",),
+    ("t", 1, 1), ("relu", 0, 0), ("stt", 1, 1, 0), ("bc", 1, 0, 2), ("relu", 0, 1),
+    ("bc", 1, 1, 4), ("sx", 1, 0), ("stt", 1, 1, 2), ("relu", 1, 0), ("sx", 1, 1),
+    ("relu", 1, 1),
+]
 
 
 def tile_rbf_conv2d_kernel(tc, x, weight, out):
@@ -27,12 +53,13 @@ def tile_rbf_conv2d_kernel(tc, x, weight, out):
         const = ctx.enter_context(tc.tile_pool(name="const", bufs=1))
         keep = ctx.enter_context(tc.tile_pool(name="keep", bufs=1))
         junkp = ctx.enter_context(tc.tile_pool(name="junkp", bufs=2))
-        ps_t = ctx.enter_context(tc.psum_pool(name="ps_t", bufs=3))
-        ps_m = ctx.enter_context(tc.psum_pool(name="ps_m", bufs=3))
-        ps_b = ctx.enter_context(tc.psum_pool(name="ps_b", bufs=2))
+        psum = ctx.enter_context(tc.psum_pool(name="psum", bufs=1))
+        if MANUAL:
+            ctx.enter_context(tc.manual_schedule())
 
         w_raw = keep.tile([P, KD], BF16, name="w_raw")
-        nc.sync.dma_start(out=w_raw[:], in_=weight)
+        for i in range(4):
+            nc.sync.dma_start(out=w_raw[:, 1152 * i:1152 * (i + 1)], in_=weight[:, 1152 * i:1152 * (i + 1)])
         raws = []
         for b in range(B):
             raw = keep.tile([P, 4, HW], BF16, name="raw%d" % b)
@@ -41,6 +68,17 @@ def tile_rbf_conv2d_kernel(tc, x, weight, out):
 
         ident = const.tile([P, P], F32, name="ident")
         make_identity(nc, ident[:])
+        band = const.tile([P, 3 * P], F32, name="band")
+        nc.gpsimd.memset(band[:], 0.0)
+        s_pad = keep.tile([P, B, 10], F32, name="s_pad")
+        nc.gpsimd.memset(s_pad[:], 0.0)
+        grps = []
+        for b in range(B):
+            grp = keep.tile([P, XCOLS * 4], BF16, name="grp%d" % b, align_bytes=64)
+            g4 = grp[:].rearrange("p (r h n) -> p r h n", r=ROWS, h=2)
+            nc.gpsimd.memset(g4[:, 0, 0, :], 0.0)
+            nc.gpsimd.memset(g4[:, ROWS - 1, 1, :], 0.0)
+            grps.append(grp)
         ident_bf = const.tile([P, P], BF16, name="ident_bf")
         nc.vector.tensor_copy(out=ident_bf[:], in_=ident[:])
         id3 = ident[:].rearrange("p (a z) -> p a z", z=32)
@@ -48,142 +86,189 @@ def tile_rbf_conv2d_kernel(tc, x, weight, out):
         nc.vector.tensor_copy(out=tri[:], in_=id3)
         nc.vector.tensor_tensor(out=tri[:, :, 1:32], in0=tri[:, :, 1:32], in1=id3[:, :, 0:31], op=ALU.add)
         nc.vector.tensor_tensor(out=tri[:, :, 0:31], in0=tri[:, :, 0:31], in1=id3[:, :, 1:32], op=ALU.add)
-        band = const.tile([P, 3 * P], F32, name="band")
-        nc.vector.memset(band[:], 0.0)
         for dy in (-1, 0, 1):
             lo = P + 32 * dy
             nc.vector.tensor_tensor(
                 out=band[:, lo:lo + P], in0=band[:, lo:lo + P],
                 in1=tri[:].rearrange("p a z -> p (a z)"), op=ALU.add,
             )
-        s_pad = keep.tile([P, B, 10], F32, name="s_pad")
-        nc.vector.memset(s_pad[:], 0.0)
+
         x2sb = keep.tile([P, B * 8], F32, name="x2sb")
-
-        grps = []
-        for b in range(B):
-            grp = keep.tile([P, XCOLS * 4], BF16, name="grp%d" % b, align_bytes=64)
-            g4 = grp[:].rearrange("p (r h n) -> p r h n", r=ROWS, h=2)
-            nc.vector.memset(g4[:, 0, 0, :], 0.0)
-            nc.vector.memset(g4[:, ROWS - 1, 1, :], 0.0)
-            grps.append(grp)
-
+        w2p = keep.tile([P, 4], F32, name="w2p")
         w2 = keep.tile([P, 1], F32, name="w2")
-        junk_w = keep.tile([P, KD], BF16, name="junk_w")
-        nc.scalar.activation(out=junk_w[:], in_=w_raw[:], func=ACT.Square, accum_out=w2[:])
-
         w_re = keep.tile([P, KD], BF16, name="w_re")
-        w_dst = w_re[:].rearrange("o (t h p e) -> o t h p e", t=9, h=2, e=2)
-        w_src = w_raw[:].rearrange("o (p h e t) -> o t h p e", h=2, e=2, t=9)
+        w_dst = w_re[:].rearrange("o (t h p e) -> o h p e t", t=9, h=2, e=2)
+        w_src = w_raw[:].rearrange("o (p h e t) -> o h p e t", h=2, e=2, t=9)
         w32 = w_re[:].bitcast(F32)
         w_grp = keep.tile([P, KD], BF16, name="w_grp", align_bytes=64)
         wg32 = w_grp[:].bitcast(F32).rearrange("p (t o h) -> p t o h", o=P, h=2)
         w_codes = keep.tile([P, 9 * P], U32, name="w_codes", align_bytes=64)
         w_scales = keep.tile([P, 9 * P], U8, name="w_scales", align_bytes=64)
-        for k in range(5):
+        xcs = []
+        xss = []
+        accs = []
+        ress = []
+        for b in range(B):
+            xcs.append(keep.tile([P, XCOLS], U32, name="xc%d" % b, align_bytes=64))
+            xss.append(keep.tile([P, XCOLS], U8, name="xs%d" % b, align_bytes=64))
+            accs.append(keep.tile([P, HW], F32, name="acc%d" % b))
+            ress.append(keep.tile([P, HW], F32, name="res%d" % b))
+        live = {}
+
+        def bank(key, shape, dtype, k):
+            t = psum.tile(shape, dtype, name="ps_%s" % key, tag="bank%d" % k)
+            live[key] = t
+            return t
+
+        def op_w2(i):
+            junk = junkp.tile([P, 1152], BF16, name="junk_w")
+            nc.scalar.activation(
+                out=junk[:], in_=w_raw[:, 1152 * i:1152 * (i + 1)], func=ACT.Square,
+                accum_out=w2p[:, i:i + 1],
+            )
+
+        def op_w2r():
+            nc.vector.tensor_reduce(out=w2[:], in_=w2p[:], axis=AX.X, op=ALU.add)
+
+        def op_wpre(pc, g):
+            t0 = 4 * g
+            t1 = min(t0 + 4, 9)
+            nc.vector.tensor_copy(
+                out=w_dst[:, :, 64 * pc:64 * pc + 64, :, t0:t1],
+                in_=w_src[:, :, 64 * pc:64 * pc + 64, :, t0:t1],
+            )
+
+        def op_wT(k, bk):
             n = 4 if k < 4 else 2
-            t0 = 2 * k
-            t1 = t0 + n // 2
-            nc.vector.tensor_copy(out=w_dst[:, t0:t1], in_=w_src[:, t0:t1])
-            wt = ps_t.tile([P, 4, P], F32, name="wt", tag="tp")
+            wt = bank("wT%d" % k, [P, 4, P], F32, bk)
             for m in range(n):
                 c0 = (4 * k + m) * P
                 nc.tensor.transpose(wt[:, m, :], w32[:, c0:c0 + P], ident[:])
+
+        def op_wev(k):
+            n = 4 if k < 4 else 2
+            wt = live["wT%d" % k]
             nc.scalar.copy(
-                out=wg32[:, t0:t1],
+                out=wg32[:, 2 * k:2 * k + n // 2],
                 in_=wt[:, 0:n, :].rearrange("p (a h) o -> p a o h", h=2),
             )
-        for lo, n in ((0, 2048), (2048, 2048), (4096, 512)):
+
+        def op_wq(i):
+            lo, n = ((0, 2048), (2048, 2048), (4096, 512))[i]
             nc.vector.quantize_mx(
                 out=w_codes[:, lo // 4:(lo + n) // 4].bitcast(FP8X4),
                 scales=w_scales[:, lo // 4:(lo + n) // 4],
                 in_=w_grp[:, lo:lo + n],
             )
 
-        for b in range(B):
-            raw = raws[b]
-            grp = grps[b]
-            g4 = grp[:].rearrange("p (r h n) -> p r h n", r=ROWS, h=2)
-            g6 = grp[:].rearrange("p (r h c i t) -> p r h c i t", r=ROWS, h=2, c=8, i=4, t=4)
-            r5 = raw[:].rearrange("p t (y c i) -> p t y c i", y=32, c=8, i=4)
-            for h in range(2):
-                nc.vector.tensor_copy(
-                    out=g6[:, 1:17, h].rearrange("p r c i t -> p r c t i"),
-                    in_=r5[:, :, 16 * h:16 * h + 16].rearrange("p t y c i -> p y c t i"),
-                )
-            nc.vector.tensor_copy(out=g4[:, ROWS - 1, 0, :], in_=g4[:, 1, 1, :])
-            nc.vector.tensor_copy(out=g4[:, 0, 1, :], in_=g4[:, 16, 0, :])
-            xc = keep.tile([P, XCOLS], U32, name="xc%d" % b, align_bytes=64)
-            xs = keep.tile([P, XCOLS], U8, name="xs%d" % b, align_bytes=64)
-            for lo, n in ((0, 2048), (2048, 2048), (4096, 512)):
-                nc.vector.quantize_mx(
-                    out=xc[:, lo // 4:(lo + n) // 4].bitcast(FP8X4),
-                    scales=xs[:, lo // 4:(lo + n) // 4],
-                    in_=grp[:, lo:lo + n],
-                )
+        def op_xre(b, part, h):
+            g6 = grps[b][:].rearrange("p (r h c i t) -> p r h c i t", r=ROWS, h=2, c=8, i=4, t=4)
+            r5 = raws[b][:].rearrange("p t (y c i) -> p t y c i", y=32, c=8, i=4)
+            if part == 1:
+                r0, r1 = 1 - h, 11 - h
+            else:
+                r0, r1 = 11 - h, 18 - h
+            y0 = 16 * h + r0 - 1
+            y1 = 16 * h + r1 - 1
+            nc.vector.tensor_copy(
+                out=g6[:, r0:r1, h].rearrange("p r c i t -> p r c t i"),
+                in_=r5[:, :, y0:y1].rearrange("p t y c i -> p y c t i"),
+            )
 
-            for ch in range(8):
-                tp = ps_t.tile([P, 4, P], BF16, name="tp", tag="tp")
+        def op_xq(b, i):
+            lo, n = ((0, 2048), (2048, 512), (2560, 2048))[i]
+            nc.vector.quantize_mx(
+                out=xcs[b][:, lo // 4:(lo + n) // 4].bitcast(FP8X4),
+                scales=xss[b][:, lo // 4:(lo + n) // 4],
+                in_=grps[b][:, lo:lo + n],
+            )
+
+        def op_xT(b, k, bk):
+            tp = bank("xT%d%d" % (b, k), [P, 8, P], BF16, bk)
+            for cl in range(2):
+                ch = 2 * k + cl
                 for j in range(4):
-                    nc.tensor.transpose(tp[:, j, :], raw[:, j, ch * P:(ch + 1) * P], ident_bf[:])
-                junk = junkp.tile([P, 4 * P], BF16, name="junk")
-                nc.scalar.activation(
-                    out=junk[:], in_=tp[:].rearrange("p j c -> p (j c)"), func=ACT.Square,
-                    accum_out=s_pad[:, b, 1 + ch:2 + ch],
-                )
-            f = ps_b.tile([P, 8], F32, name="f", tag="xb")
+                    nc.tensor.transpose(tp[:, 4 * cl + j, :], raws[b][:, j, ch * P:(ch + 1) * P], ident_bf[:])
+
+        def op_sq(b, c):
+            tp = live["xT%d%d" % (b, c // 2)]
+            cl = c % 2
+            junk = junkp.tile([P, 4 * P], BF16, name="junk_x")
+            nc.scalar.activation(
+                out=junk[:], in_=tp[:, 4 * cl:4 * cl + 4, :].rearrange("p j c -> p (j c)"), func=ACT.Square,
+                accum_out=s_pad[:, b, 1 + c:2 + c],
+            )
+
+        def op_f(b, bk):
+            f = bank("f%d" % b, [P, 8], F32, bk)
             for rel in range(3):
                 nc.tensor.matmul(
                     f[:], lhsT=band[:, rel * P:(rel + 1) * P], rhs=s_pad[:, b, 2 - rel:10 - rel],
                     start=(rel == 0), stop=(rel == 2),
                 )
-            nc.vector.tensor_copy(out=x2sb[:, 8 * b:8 * b + 8], in_=f[:])
-            acc = keep.tile([P, HW], F32, name="acc%d" % b)
-            acc5 = acc[:].rearrange("p (w y h z) -> p w y h z", w=2, y=8, h=2)
+
+        def op_x2c(b):
+            nc.vector.tensor_copy(out=x2sb[:, 8 * b:8 * b + 8], in_=live["f%d" % b][:])
+
+        def op_bc(b, w, bk):
+            xb = bank("bc%d%d" % (b, w), [P, 512], F32, bk)
+            xb5 = xb[:].rearrange("p (u r h z) -> p u r h z", u=2, r=4, h=2)
             for h in range(2):
-                xb = ps_b.tile([P, 512], F32, name="xb", tag="xb")
-                for q in range(4):
-                    col = 8 * b + 4 * h + q
+                for u in range(2):
+                    col = 8 * b + 4 * h + 2 * w + u
                     nc.tensor.transpose(
-                        xb[:, q * P:(q + 1) * P], x2sb[:, col:col + 1].to_broadcast([P, P]), ident[:]
+                        xb5[:, u, :, h, :], x2sb[:, col:col + 1].to_broadcast([P, P]), ident[:]
                     )
-                nc.scalar.activation(
-                    out=acc5[:, :, :, h, :],
-                    in_=xb[:].rearrange("p (w y z) -> p w y z", w=2, y=8),
-                    func=ACT.Identity, bias=w2[:, 0:1],
+
+        def op_mx(b, w, j, bk):
+            pj = bank("mx%d%d%d" % (b, w, j), [P, 512], F32, bk)
+            for i in range(3):
+                tap = 3 * i + j
+                c0 = 64 * (8 * w + i)
+                nc.tensor.matmul_mx(
+                    out=pj[:],
+                    lhsT=w_codes[:, tap * P:(tap + 1) * P].bitcast(FP8X4),
+                    lhsT_scale=w_scales[:, tap * P:(tap + 1) * P],
+                    rhs=xcs[b][:, c0:c0 + 512].bitcast(FP8X4),
+                    rhs_scale=xss[b][:, c0:c0 + 512],
+                    start=(i == 0), stop=(i == 2),
                 )
 
-            res = keep.tile([P, HW], F32, name="res%d" % b)
+        def op_t(b, w):
+            nc.scalar.activation(
+                out=accs[b][:, 512 * w:512 * w + 512], in_=live["mx%d%d1" % (b, w)][:],
+                func=ACT.Identity, scale=-2.0,
+            )
+
+        def op_stt(b, w, j):
+            a3 = accs[b][:, 512 * w:512 * w + 512].rearrange("p (s z) -> p s z", z=32)
+            p3 = live["mx%d%d%d" % (b, w, j)][:].rearrange("p (s z) -> p s z", z=32)
+            if j == 0:
+                dst, src = a3[:, :, 1:32], p3[:, :, 0:31]
+            else:
+                dst, src = a3[:, :, 0:31], p3[:, :, 1:32]
+            nc.vector.scalar_tensor_tensor(out=dst, in0=src, scalar=-2.0, in1=dst, op0=ALU.mult, op1=ALU.add)
+
+        def op_sx(b, w):
+            a = accs[b][:, 512 * w:512 * w + 512]
+            nc.vector.tensor_tensor(out=a, in0=live["bc%d%d" % (b, w)][:], in1=a, op=ALU.add)
+
+        def op_relu(b, w):
+            res = ress[b]
             res5 = res[:].rearrange("p (h w y z) -> p w y h z", h=2, w=2, y=8)
             res4 = res[:].rearrange("p (h w n) -> p h w n", h=2, w=2)
             out4 = out[b].rearrange("o (h w y) z -> o h w (y z)", h=2, w=2)
-            for w in range(2):
-                a = acc[:, 512 * w:512 * w + 512]
-                a3 = a.rearrange("p (s z) -> p s z", z=32)
-                for j in (1, 0, 2):
-                    pj = ps_m.tile([P, 512], F32, name="pj", tag="mx")
-                    for i in range(3):
-                        tap = 3 * i + j
-                        c0 = 64 * (8 * w + i)
-                        nc.tensor.matmul_mx(
-                            out=pj[:],
-                            lhsT=w_codes[:, tap * P:(tap + 1) * P].bitcast(FP8X4),
-                            lhsT_scale=w_scales[:, tap * P:(tap + 1) * P],
-                            rhs=xc[:, c0:c0 + 512].bitcast(FP8X4),
-                            rhs_scale=xs[:, c0:c0 + 512],
-                            start=(i == 0), stop=(i == 2),
-                        )
-                    p3 = pj[:].rearrange("p (s z) -> p s z", z=32)
-                    if j == 1:
-                        dst, src = a3, p3
-                    elif j == 0:
-                        dst, src = a3[:, :, 1:32], p3[:, :, 0:31]
-                    else:
-                        dst, src = a3[:, :, 0:31], p3[:, :, 1:32]
-                    nc.vector.scalar_tensor_tensor(
-                        out=dst, in0=src, scalar=-2.0, in1=dst, op0=ALU.mult, op1=ALU.add
-                    )
-                nc.scalar.activation(
-                    out=res5[:, w], in_=a.rearrange("p (y h z) -> p y h z", y=8, h=2), func=ACT.Relu
-                )
-                nc.sync.dma_start(out=out4[:, :, w, :], in_=res4[:, :, w, :])
+            nc.scalar.activation(
+                out=res5[:, w],
+                in_=accs[b][:, 512 * w:512 * w + 512].rearrange("p (y h z) -> p y h z", y=8, h=2),
+                func=ACT.Relu, bias=w2[:, 0:1],
+            )
+            nc.sync.dma_start(out=out4[:, :, w, :], in_=res4[:, :, w, :])
+
+        ops = {
+            "w2": op_w2, "w2r": op_w2r, "wpre": op_wpre, "wT": op_wT, "wev": op_wev, "wq": op_wq,
+            "xre": op_xre, "xq": op_xq, "xT": op_xT, "sq": op_sq, "f": op_f, "x2c": op_x2c,
+            "bc": op_bc, "mx": op_mx, "t": op_t, "stt": op_stt, "sx": op_sx, "relu": op_relu,
+        }
+        for step in PLAN:
+            ops[step[0]](*step[1:])

@@ -24,25 +24,26 @@ MANUAL = True
 
 PLAN = [
     ("w2", 0), ("wpre", 0, 0), ("wpre", 0, 1), ("w2", 1), ("wpre", 0, 2),
-    ("wpre", 1, 0), ("w2", 2), ("wpre", 1, 1), ("wT", 0, 0), ("wT", 1, 1),
-    ("wpre", 1, 2), ("wT", 2, 2), ("wT", 3, 3), ("wev", 0), ("xre", 0, 1, 0),
-    ("wT", 4, 4), ("xT", 0, 0, 5), ("wev", 1), ("xT", 0, 1, 6), ("xre", 0, 1, 1),
-    ("wev", 2), ("xT", 0, 2, 7), ("wq", 0), ("wev", 3), ("xT", 0, 3, 0),
-    ("wev", 4), ("wq", 1), ("xT", 1, 0, 1), ("sq", 0, 0), ("xT", 1, 1, 2),
-    ("wq", 2), ("xq", 0, 0), ("sq", 0, 1), ("xT", 1, 2, 3), ("xq", 0, 1),
-    ("xre", 0, 2, 0), ("sq", 0, 2), ("xT", 1, 3, 4), ("xre", 0, 2, 1), ("sq", 0, 3),
-    ("mx", 0, 0, 1, 5), ("xq", 0, 2), ("sq", 0, 4), ("mx", 0, 0, 0, 6), ("xre", 1, 1, 0),
-    ("sq", 0, 5), ("t", 0, 0), ("mx", 0, 0, 2, 7), ("sq", 0, 6), ("stt", 0, 0, 0),
-    ("mx", 0, 1, 1, 5), ("sq", 0, 7), ("stt", 0, 0, 2), ("mx", 0, 1, 0, 6), ("xre", 1, 1, 1),
-    ("sq", 1, 0), ("mx", 0, 1, 2, 7), ("t", 0, 1), ("xq", 1, 0), ("sq", 1, 1),
-    ("xq", 1, 1), ("stt", 0, 1, 0), ("f", 0, 0), ("mx", 1, 0, 1, 5), ("sq", 1, 2),
-    ("stt", 0, 1, 2), ("sq", 1, 3), ("xre", 1, 2, 0), ("mx", 1, 0, 0, 1), ("xre", 1, 2, 1),
-    ("sq", 1, 4), ("mx", 1, 0, 2, 6), ("xq", 1, 2), ("t", 1, 0), ("x2c", 0),
-    ("sq", 1, 5), ("bc", 0, 0, 7), ("bc", 0, 1, 2), ("sq", 1, 6), ("sx", 0, 0),
-    ("mx", 1, 1, 1, 5), ("sx", 0, 1), ("sq", 1, 7), ("mx", 1, 1, 0, 0), ("stt", 1, 0, 0),
-    ("w2", 3), ("stt", 1, 0, 2), ("f", 1, 3), ("mx", 1, 1, 2, 7), ("x2c", 1), ("w2r",),
-    ("t", 1, 1), ("relu", 0, 0), ("stt", 1, 1, 0), ("bc", 1, 0, 2), ("relu", 0, 1),
-    ("bc", 1, 1, 4), ("sx", 1, 0), ("stt", 1, 1, 2), ("relu", 1, 0), ("sx", 1, 1),
+    ("wpre", 1, 0), ("wpre", 1, 1), ("wT", 0, 0), ("wT", 1, 1), ("wev", 0),
+    ("wpre", 1, 2), ("wT", 2, 2), ("wT", 3, 3), ("wev", 1), ("xre", 0, 1, 0, 0),
+    ("wT", 4, 4), ("xG", 0, 0, 5), ("wev", 2), ("xT", 0, 0, 6), ("xre", 0, 1, 1, 0),
+    ("wev", 3), ("xG", 0, 1, 5), ("xG", 0, 2, 5), ("wev", 4), ("wq", 0),
+    ("xT", 0, 1, 7), ("sq", 0, 0), ("wq", 1), ("xG", 0, 3, 5), ("xG", 1, 0, 0),
+    ("sq", 0, 1), ("xT", 1, 0, 1), ("wq", 2), ("xq", 0, 0), ("sq", 0, 2),
+    ("xG", 1, 1, 0), ("xq", 0, 1), ("xre", 0, 2, 0, 0), ("sq", 0, 3), ("mx", 0, 0, 1, 2),
+    ("xre", 0, 2, 1, 0), ("xq", 0, 2), ("mx", 0, 0, 0, 3), ("t", 0, 0), ("xre", 1, 1, 0, 0),
+    ("xre", 1, 2, 0, 1), ("mx", 0, 0, 2, 4), ("xre", 1, 1, 1, 0), ("xG", 1, 2, 0), ("xre", 1, 2, 1, 1),
+    ("xT", 1, 1, 6), ("xq", 1, 0), ("xG", 1, 3, 0), ("xq", 1, 1), ("mx", 0, 1, 1, 7),
+    ("dg", 0, 0), ("dg", 0, 1), ("dg", 0, 2), ("mx", 0, 1, 0, 2), ("dg", 0, 3),
+    ("t", 0, 1), ("stt", 0, 0, 0), ("sq", 1, 0), ("mx", 0, 1, 2, 5), ("stt", 0, 0, 2),
+    ("sq", 1, 1), ("xq", 1, 2), ("f", 0, 7), ("stt", 0, 1, 0), ("mx", 1, 0, 1, 3),
+    ("x2c", 0), ("sq", 1, 2), ("stt", 0, 1, 2), ("mx", 1, 0, 0, 4), ("sq", 1, 3),
+    ("dg", 1, 0), ("dg", 1, 1), ("dg", 1, 2), ("t", 1, 0), ("mx", 1, 0, 2, 1),
+    ("dg", 1, 3), ("w2", 2), ("bc", 0, 0, 7), ("bc", 0, 1, 2), ("sx", 0, 0),
+    ("f", 1, 5), ("sx", 0, 1), ("mx", 1, 1, 1, 6), ("x2c", 1), ("w2", 3),
+    ("stt", 1, 0, 0), ("mx", 1, 1, 0, 0), ("stt", 1, 0, 2), ("t", 1, 1), ("w2r",),
+    ("bc", 1, 0, 3), ("bc", 1, 1, 7), ("relu", 0, 0), ("sx", 1, 0), ("mx", 1, 1, 2, 5),
+    ("relu", 0, 1), ("stt", 1, 1, 0), ("relu", 1, 0), ("sx", 1, 1), ("stt", 1, 1, 2),
     ("relu", 1, 1),
 ]
 
@@ -70,8 +71,10 @@ def tile_rbf_conv2d_kernel(tc, x, weight, out):
         make_identity(nc, ident[:])
         band = const.tile([P, 3 * P], F32, name="band")
         nc.gpsimd.memset(band[:], 0.0)
-        s_pad = keep.tile([P, B, 10], F32, name="s_pad")
-        nc.gpsimd.memset(s_pad[:], 0.0)
+        s_act = keep.tile([P, B, 10], F32, name="s_act")
+        nc.gpsimd.memset(s_act[:], 0.0)
+        s_dve = keep.tile([P, B, 10], F32, name="s_dve")
+        nc.gpsimd.memset(s_dve[:], 0.0)
         grps = []
         for b in range(B):
             grp = keep.tile([P, XCOLS * 4], BF16, name="grp%d" % b, align_bytes=64)
@@ -161,7 +164,7 @@ def tile_rbf_conv2d_kernel(tc, x, weight, out):
                 in_=w_grp[:, lo:lo + n],
             )
 
-        def op_xre(b, part, h):
+        def op_xre(b, part, h, on_scalar):
             g6 = grps[b][:].rearrange("p (r h c i t) -> p r h c i t", r=ROWS, h=2, c=8, i=4, t=4)
             r5 = raws[b][:].rearrange("p t (y c i) -> p t y c i", y=32, c=8, i=4)
             if part == 1:
@@ -170,10 +173,16 @@ def tile_rbf_conv2d_kernel(tc, x, weight, out):
                 r0, r1 = 11 - h, 18 - h
             y0 = 16 * h + r0 - 1
             y1 = 16 * h + r1 - 1
-            nc.vector.tensor_copy(
-                out=g6[:, r0:r1, h].rearrange("p r c i t -> p r c t i"),
-                in_=r5[:, :, y0:y1].rearrange("p t y c i -> p y c t i"),
-            )
+            if on_scalar:
+                nc.scalar.copy(
+                    out=grps[b][:].rearrange("p (r h z t) -> p r h z t", r=ROWS, h=2, t=4)[:, r0:r1, h],
+                    in_=raws[b][:].rearrange("p t (y z) -> p y z t", y=32)[:, y0:y1],
+                )
+            else:
+                nc.vector.tensor_copy(
+                    out=g6[:, r0:r1, h].rearrange("p r c i t -> p r c t i"),
+                    in_=r5[:, :, y0:y1].rearrange("p t y c i -> p y c t i"),
+                )
 
         def op_xq(b, i):
             lo, n = ((0, 2048), (2048, 512), (2560, 2048))[i]
@@ -186,7 +195,7 @@ def tile_rbf_conv2d_kernel(tc, x, weight, out):
         def op_xT(b, k, bk):
             tp = bank("xT%d%d" % (b, k), [P, 8, P], BF16, bk)
             for cl in range(2):
-                ch = 2 * k + cl
+                ch = 4 * k + 2 * cl + 1
                 for j in range(4):
                     nc.tensor.transpose(tp[:, 4 * cl + j, :], raws[b][:, j, ch * P:(ch + 1) * P], ident_bf[:])
 
@@ -196,19 +205,36 @@ def tile_rbf_conv2d_kernel(tc, x, weight, out):
             junk = junkp.tile([P, 4 * P], BF16, name="junk_x")
             nc.scalar.activation(
                 out=junk[:], in_=tp[:, 4 * cl:4 * cl + 4, :].rearrange("p j c -> p (j c)"), func=ACT.Square,
-                accum_out=s_pad[:, b, 1 + c:2 + c],
+                accum_out=s_act[:, b, 2 + 2 * c:3 + 2 * c],
+            )
+
+        def op_xG(b, q, bk):
+            if q == 0:
+                bank("xG%d" % b, [P, 4, P], F32, bk)
+            g = live["xG%d" % b]
+            ch = 2 * q
+            for j in range(4):
+                blk = raws[b][:, j, ch * P:(ch + 1) * P]
+                nc.tensor.matmul(g[:, q, :], lhsT=blk, rhs=blk, start=(j == 0), stop=(j == 3))
+
+        def op_dg(b, q):
+            junk = junkp.tile([P, P], F32, name="junk_g")
+            nc.vector.scalar_tensor_tensor(
+                out=junk[:], in0=live["xG%d" % b][:, q, :], scalar=1.0, in1=ident[:],
+                op0=ALU.mult, op1=ALU.mult, accum_out=s_dve[:, b, 1 + 2 * q:2 + 2 * q],
             )
 
         def op_f(b, bk):
             f = bank("f%d" % b, [P, 8], F32, bk)
-            for rel in range(3):
-                nc.tensor.matmul(
-                    f[:], lhsT=band[:, rel * P:(rel + 1) * P], rhs=s_pad[:, b, 2 - rel:10 - rel],
-                    start=(rel == 0), stop=(rel == 2),
-                )
+            for n, s in enumerate((s_act, s_dve)):
+                for rel in range(3):
+                    nc.tensor.matmul(
+                        f[:], lhsT=band[:, rel * P:(rel + 1) * P], rhs=s[:, b, 2 - rel:10 - rel],
+                        start=(n == 0 and rel == 0), stop=(n == 1 and rel == 2),
+                    )
 
         def op_x2c(b):
-            nc.vector.tensor_copy(out=x2sb[:, 8 * b:8 * b + 8], in_=live["f%d" % b][:])
+            nc.scalar.copy(out=x2sb[:, 8 * b:8 * b + 8], in_=live["f%d" % b][:])
 
         def op_bc(b, w, bk):
             xb = bank("bc%d%d" % (b, w), [P, 512], F32, bk)
@@ -267,7 +293,7 @@ def tile_rbf_conv2d_kernel(tc, x, weight, out):
 
         ops = {
             "w2": op_w2, "w2r": op_w2r, "wpre": op_wpre, "wT": op_wT, "wev": op_wev, "wq": op_wq,
-            "xre": op_xre, "xq": op_xq, "xT": op_xT, "sq": op_sq, "f": op_f, "x2c": op_x2c,
+            "xre": op_xre, "xq": op_xq, "xT": op_xT, "sq": op_sq, "xG": op_xG, "dg": op_dg, "f": op_f, "x2c": op_x2c,
             "bc": op_bc, "mx": op_mx, "t": op_t, "stt": op_stt, "sx": op_sx, "relu": op_relu,
         }
         for step in PLAN:

@@ -24,27 +24,28 @@ MANUAL = True
 
 PLAN = [
     ("w2", 0), ("wpre", 0, 0), ("wpre", 0, 1), ("w2", 1), ("wpre", 0, 2),
-    ("wpre", 1, 0), ("wpre", 1, 1), ("wT", 0, 0), ("wT", 1, 1), ("wev", 0),
-    ("wpre", 1, 2), ("wT", 2, 2), ("wT", 3, 3), ("wev", 1), ("xre", 0, 1, 0, 0),
-    ("wT", 4, 4), ("xG", 0, 0, 5), ("wev", 2), ("xT", 0, 0, 6), ("xre", 0, 1, 1, 0),
-    ("wev", 3), ("xG", 0, 1, 5), ("xG", 0, 2, 5), ("wev", 4), ("wq", 0),
-    ("xT", 0, 1, 7), ("sq", 0, 0), ("wq", 1), ("xG", 0, 3, 5), ("xG", 1, 0, 0),
-    ("sq", 0, 1), ("xT", 1, 0, 1), ("wq", 2), ("xq", 0, 0), ("sq", 0, 2),
-    ("xG", 1, 1, 0), ("xq", 0, 1), ("xre", 0, 2, 0, 0), ("sq", 0, 3), ("mx", 0, 0, 1, 2),
-    ("xre", 0, 2, 1, 0), ("xq", 0, 2), ("mx", 0, 0, 0, 3), ("t", 0, 0), ("xre", 1, 1, 0, 0),
-    ("xre", 1, 2, 0, 1), ("mx", 0, 0, 2, 4), ("xre", 1, 1, 1, 0), ("xG", 1, 2, 0), ("xre", 1, 2, 1, 1),
-    ("xT", 1, 1, 6), ("xq", 1, 0), ("xG", 1, 3, 0), ("xq", 1, 1), ("mx", 0, 1, 1, 7),
-    ("dg", 0, 0), ("dg", 0, 1), ("dg", 0, 2), ("mx", 0, 1, 0, 2), ("dg", 0, 3),
-    ("t", 0, 1), ("stt", 0, 0, 0), ("sq", 1, 0), ("mx", 0, 1, 2, 5), ("stt", 0, 0, 2),
-    ("sq", 1, 1), ("xq", 1, 2), ("f", 0, 7), ("stt", 0, 1, 0), ("mx", 1, 0, 1, 3),
-    ("x2c", 0), ("sq", 1, 2), ("stt", 0, 1, 2), ("mx", 1, 0, 0, 4), ("sq", 1, 3),
-    ("dg", 1, 0), ("dg", 1, 1), ("dg", 1, 2), ("t", 1, 0), ("mx", 1, 0, 2, 1),
-    ("dg", 1, 3), ("w2", 2), ("bc", 0, 0, 7), ("bc", 0, 1, 2), ("sx", 0, 0),
-    ("f", 1, 5), ("sx", 0, 1), ("mx", 1, 1, 1, 6), ("x2c", 1), ("w2", 3),
-    ("stt", 1, 0, 0), ("mx", 1, 1, 0, 0), ("stt", 1, 0, 2), ("t", 1, 1), ("w2r",),
-    ("bc", 1, 0, 3), ("bc", 1, 1, 7), ("relu", 0, 0), ("sx", 1, 0), ("mx", 1, 1, 2, 5),
-    ("relu", 0, 1), ("stt", 1, 1, 0), ("relu", 1, 0), ("sx", 1, 1), ("stt", 1, 1, 2),
-    ("relu", 1, 1),
+    ("wpre", 0, 3), ("wpre", 0, 4), ("wpre", 1, 0), ("wpre", 1, 1), ("wT", 0, 0),
+    ("wpre", 1, 2), ("wT", 1, 1), ("wev", 0), ("wpre", 1, 3), ("wT", 2, 2),
+    ("wpre", 1, 4), ("wev", 1), ("wT", 3, 3), ("xre", 0, 1, 0, 0), ("wev", 2),
+    ("wT", 4, 4), ("xG", 0, 0, 5), ("xre", 0, 1, 1, 0), ("xT", 0, 0, 6), ("wev", 3),
+    ("wev", 4), ("xG", 0, 1, 5), ("wq", 0), ("sq", 0, 0), ("xG", 0, 2, 5),
+    ("wq", 1), ("xT", 0, 1, 7), ("sq", 0, 1), ("wq", 2), ("xG", 0, 3, 5),
+    ("xq", 0, 0), ("sq", 0, 2), ("xG", 1, 0, 0), ("xq", 0, 1), ("xT", 1, 0, 1),
+    ("xre", 0, 2, 0, 0), ("sq", 0, 3), ("xG", 1, 1, 0), ("xre", 0, 2, 1, 0), ("mx", 0, 0, 1, 2),
+    ("xq", 0, 2), ("xre", 1, 1, 0, 0), ("mx", 0, 0, 0, 3), ("t", 0, 0), ("xre", 1, 2, 0, 1),
+    ("xre", 1, 1, 1, 0), ("mx", 0, 0, 2, 4), ("xq", 1, 0), ("xG", 1, 2, 0), ("xre", 1, 2, 1, 1),
+    ("xT", 1, 1, 6), ("xq", 1, 1), ("dg", 0, 0), ("dg", 0, 1), ("xG", 1, 3, 0),
+    ("dg", 0, 2), ("mx", 0, 1, 1, 7), ("dg", 0, 3), ("sadd", 0), ("stt", 0, 0, 0),
+    ("mx", 0, 1, 0, 2), ("t", 0, 1), ("stt", 0, 0, 2), ("sq", 1, 0), ("xq", 1, 2),
+    ("mx", 0, 1, 2, 5), ("stt", 0, 1, 0), ("sq", 1, 1), ("f", 0, 3), ("stt", 0, 1, 2),
+    ("mx", 1, 0, 1, 7), ("x2c", 0), ("sq", 1, 2), ("dg", 1, 0), ("dg", 1, 1),
+    ("sq", 1, 3), ("mx", 1, 0, 0, 4), ("dg", 1, 2), ("dg", 1, 3), ("t", 1, 0),
+    ("sadd", 1), ("mx", 1, 0, 2, 2), ("w2", 2), ("bc", 0, 0, 1), ("bc", 0, 1, 3),
+    ("sx", 0, 0), ("f", 1, 5), ("sx", 0, 1), ("mx", 1, 1, 1, 6), ("x2c", 1),
+    ("w2", 3), ("stt", 1, 0, 0), ("mx", 1, 1, 0, 0), ("stt", 1, 0, 2), ("t", 1, 1),
+    ("w2r",), ("bc", 1, 0, 7), ("relu", 0, 0), ("bc", 1, 1, 1), ("sx", 1, 0),
+    ("relu", 0, 1), ("mx", 1, 1, 2, 5), ("stt", 1, 1, 0), ("relu", 1, 0), ("sx", 1, 1),
+    ("stt", 1, 1, 2), ("relu", 1, 1),
 ]
 
 
@@ -97,6 +98,7 @@ def tile_rbf_conv2d_kernel(tc, x, weight, out):
             )
 
         x2sb = keep.tile([P, B * 8], F32, name="x2sb")
+        s_sum = keep.tile([P, B, 10], F32, name="s_sum")
         w2p = keep.tile([P, 4], F32, name="w2p")
         w2 = keep.tile([P, 1], F32, name="w2")
         w_re = keep.tile([P, KD], BF16, name="w_re")
@@ -134,8 +136,8 @@ def tile_rbf_conv2d_kernel(tc, x, weight, out):
             nc.vector.tensor_reduce(out=w2[:], in_=w2p[:], axis=AX.X, op=ALU.add)
 
         def op_wpre(pc, g):
-            t0 = 4 * g
-            t1 = min(t0 + 4, 9)
+            t0 = 2 * g
+            t1 = min(t0 + 2, 9)
             nc.vector.tensor_copy(
                 out=w_dst[:, :, 64 * pc:64 * pc + 64, :, t0:t1],
                 in_=w_src[:, :, 64 * pc:64 * pc + 64, :, t0:t1],
@@ -226,12 +228,14 @@ def tile_rbf_conv2d_kernel(tc, x, weight, out):
 
         def op_f(b, bk):
             f = bank("f%d" % b, [P, 8], F32, bk)
-            for n, s in enumerate((s_act, s_dve)):
-                for rel in range(3):
-                    nc.tensor.matmul(
-                        f[:], lhsT=band[:, rel * P:(rel + 1) * P], rhs=s[:, b, 2 - rel:10 - rel],
-                        start=(n == 0 and rel == 0), stop=(n == 1 and rel == 2),
-                    )
+            for rel in range(3):
+                nc.tensor.matmul(
+                    f[:], lhsT=band[:, rel * P:(rel + 1) * P], rhs=s_sum[:, b, 2 - rel:10 - rel],
+                    start=(rel == 0), stop=(rel == 2),
+                )
+
+        def op_sadd(b):
+            nc.vector.tensor_tensor(out=s_sum[:, b, :], in0=s_act[:, b, :], in1=s_dve[:, b, :], op=ALU.add)
 
         def op_x2c(b):
             nc.scalar.copy(out=x2sb[:, 8 * b:8 * b + 8], in_=live["f%d" % b][:])
@@ -293,7 +297,7 @@ def tile_rbf_conv2d_kernel(tc, x, weight, out):
 
         ops = {
             "w2": op_w2, "w2r": op_w2r, "wpre": op_wpre, "wT": op_wT, "wev": op_wev, "wq": op_wq,
-            "xre": op_xre, "xq": op_xq, "xT": op_xT, "sq": op_sq, "xG": op_xG, "dg": op_dg, "f": op_f, "x2c": op_x2c,
+            "xre": op_xre, "xq": op_xq, "xT": op_xT, "sq": op_sq, "xG": op_xG, "dg": op_dg, "sadd": op_sadd, "f": op_f, "x2c": op_x2c,
             "bc": op_bc, "mx": op_mx, "t": op_t, "stt": op_stt, "sx": op_sx, "relu": op_relu,
         }
         for step in PLAN:

@@ -18,75 +18,49 @@ P = 128
 B = 2
 HW = 1024
 KD = 4608
+TAPS = 9
 ROWS = 18
 XCOLS = ROWS * 64
-MANUAL = True
-
-PLAN = [
-    ("w2", 0), ("wpre", 0, 0), ("wpre", 0, 1), ("w2", 1), ("wpre", 0, 2),
-    ("wpre", 0, 3), ("wpre", 0, 4), ("wpre", 1, 0), ("wpre", 1, 1), ("wT", 0, 0),
-    ("wpre", 1, 2), ("wT", 1, 1), ("wev", 0), ("wpre", 1, 3), ("wT", 2, 2),
-    ("wpre", 1, 4), ("wev", 1), ("wT", 3, 3), ("xre", 0, 1, 0, 0), ("wev", 2),
-    ("wT", 4, 4), ("xG", 0, 0, 5), ("xre", 0, 1, 1, 0), ("xT", 0, 0, 6), ("wev", 3),
-    ("wev", 4), ("xG", 0, 1, 5), ("wq", 0), ("sq", 0, 0), ("xG", 0, 2, 5),
-    ("wq", 1), ("xT", 0, 1, 7), ("sq", 0, 1), ("wq", 2), ("xG", 0, 3, 5),
-    ("xq", 0, 0), ("sq", 0, 2), ("xG", 1, 0, 0), ("xq", 0, 1), ("xT", 1, 0, 1),
-    ("xre", 0, 2, 0, 0), ("sq", 0, 3), ("xG", 1, 1, 0), ("xre", 0, 2, 1, 0), ("mx", 0, 0, 1, 2),
-    ("xq", 0, 2), ("xre", 1, 1, 0, 0), ("mx", 0, 0, 0, 3), ("t", 0, 0), ("xre", 1, 2, 0, 1),
-    ("xre", 1, 1, 1, 0), ("mx", 0, 0, 2, 4), ("xq", 1, 0), ("xG", 1, 2, 0), ("xre", 1, 2, 1, 1),
-    ("xT", 1, 1, 6), ("xq", 1, 1), ("dg", 0, 0), ("dg", 0, 1), ("xG", 1, 3, 0),
-    ("dg", 0, 2), ("mx", 0, 1, 1, 7), ("dg", 0, 3), ("sadd", 0), ("stt", 0, 0, 0),
-    ("mx", 0, 1, 0, 2), ("t", 0, 1), ("stt", 0, 0, 2), ("sq", 1, 0), ("xq", 1, 2),
-    ("mx", 0, 1, 2, 5), ("stt", 0, 1, 0), ("sq", 1, 1), ("f", 0, 3), ("stt", 0, 1, 2),
-    ("mx", 1, 0, 1, 7), ("x2c", 0), ("sq", 1, 2), ("dg", 1, 0), ("dg", 1, 1),
-    ("sq", 1, 3), ("mx", 1, 0, 0, 4), ("dg", 1, 2), ("dg", 1, 3), ("t", 1, 0),
-    ("sadd", 1), ("mx", 1, 0, 2, 2), ("w2", 2), ("bc", 0, 0, 1), ("bc", 0, 1, 3),
-    ("sx", 0, 0), ("f", 1, 5), ("sx", 0, 1), ("mx", 1, 1, 1, 6), ("x2c", 1),
-    ("w2", 3), ("stt", 1, 0, 0), ("mx", 1, 1, 0, 0), ("stt", 1, 0, 2), ("t", 1, 1),
-    ("w2r",), ("bc", 1, 0, 7), ("relu", 0, 0), ("bc", 1, 1, 1), ("sx", 1, 0),
-    ("relu", 0, 1), ("mx", 1, 1, 2, 5), ("stt", 1, 1, 0), ("relu", 1, 0), ("sx", 1, 1),
-    ("stt", 1, 1, 2), ("relu", 1, 1),
-]
+W_PIECE = KD // 4
+X_QUANT = ((0, 2048), (2048, 512), (2560, 2048))
+W_QUANT = ((0, 2048), (2048, 2048), (4096, 512))
 
 
 def tile_rbf_conv2d_kernel(tc, x, weight, out):
     nc = tc.nc
     with ExitStack() as ctx:
-        const = ctx.enter_context(tc.tile_pool(name="const", bufs=1))
         keep = ctx.enter_context(tc.tile_pool(name="keep", bufs=1))
-        junkp = ctx.enter_context(tc.tile_pool(name="junkp", bufs=2))
+        scrap = ctx.enter_context(tc.tile_pool(name="scrap", bufs=2))
         psum = ctx.enter_context(tc.psum_pool(name="psum", bufs=1))
-        if MANUAL:
-            ctx.enter_context(tc.manual_schedule())
+        ctx.enter_context(tc.manual_schedule())
 
         w_raw = keep.tile([P, KD], BF16, name="w_raw")
         for i in range(4):
-            nc.sync.dma_start(out=w_raw[:, 1152 * i:1152 * (i + 1)], in_=weight[:, 1152 * i:1152 * (i + 1)])
-        raws = []
+            cols = slice(W_PIECE * i, W_PIECE * (i + 1))
+            nc.sync.dma_start(out=w_raw[:, cols], in_=weight[:, cols])
+        raw = []
         for b in range(B):
-            raw = keep.tile([P, 4, HW], BF16, name="raw%d" % b)
-            nc.sync.dma_start(out=raw[:], in_=x[b].rearrange("(p j) h w -> p j (h w)", j=4))
-            raws.append(raw)
+            raw.append(keep.tile([P, 4, HW], BF16, name="raw%d" % b))
+            nc.sync.dma_start(out=raw[b][:], in_=x[b].rearrange("(p j) h w -> p j (h w)", j=4))
 
-        ident = const.tile([P, P], F32, name="ident")
+        ident = keep.tile([P, P], F32, name="ident")
         make_identity(nc, ident[:])
-        band = const.tile([P, 3 * P], F32, name="band")
+        band = keep.tile([P, 3 * P], F32, name="band")
         nc.gpsimd.memset(band[:], 0.0)
         s_act = keep.tile([P, B, 10], F32, name="s_act")
         nc.gpsimd.memset(s_act[:], 0.0)
         s_dve = keep.tile([P, B, 10], F32, name="s_dve")
         nc.gpsimd.memset(s_dve[:], 0.0)
-        grps = []
+        grp = []
         for b in range(B):
-            grp = keep.tile([P, XCOLS * 4], BF16, name="grp%d" % b, align_bytes=64)
-            g4 = grp[:].rearrange("p (r h n) -> p r h n", r=ROWS, h=2)
-            nc.gpsimd.memset(g4[:, 0, 0, :], 0.0)
-            nc.gpsimd.memset(g4[:, ROWS - 1, 1, :], 0.0)
-            grps.append(grp)
-        ident_bf = const.tile([P, P], BF16, name="ident_bf")
+            grp.append(keep.tile([P, XCOLS * 4], BF16, name="grp%d" % b, align_bytes=64))
+            halves = grp[b][:].rearrange("p (r h n) -> p r h n", r=ROWS, h=2)
+            nc.gpsimd.memset(halves[:, 0, 0, :], 0.0)
+            nc.gpsimd.memset(halves[:, ROWS - 1, 1, :], 0.0)
+        ident_bf = keep.tile([P, P], BF16, name="ident_bf")
         nc.vector.tensor_copy(out=ident_bf[:], in_=ident[:])
         id3 = ident[:].rearrange("p (a z) -> p a z", z=32)
-        tri = const.tile([P, 4, 32], F32, name="tri")
+        tri = keep.tile([P, 4, 32], F32, name="tri")
         nc.vector.tensor_copy(out=tri[:], in_=id3)
         nc.vector.tensor_tensor(out=tri[:, :, 1:32], in0=tri[:, :, 1:32], in1=id3[:, :, 0:31], op=ALU.add)
         nc.vector.tensor_tensor(out=tri[:, :, 0:31], in0=tri[:, :, 0:31], in1=id3[:, :, 1:32], op=ALU.add)
@@ -97,161 +71,165 @@ def tile_rbf_conv2d_kernel(tc, x, weight, out):
                 in1=tri[:].rearrange("p a z -> p (a z)"), op=ALU.add,
             )
 
-        x2sb = keep.tile([P, B * 8], F32, name="x2sb")
         s_sum = keep.tile([P, B, 10], F32, name="s_sum")
-        w2p = keep.tile([P, 4], F32, name="w2p")
+        x2 = keep.tile([P, B, 8], F32, name="x2")
+        w2_parts = keep.tile([P, 4], F32, name="w2_parts")
         w2 = keep.tile([P, 1], F32, name="w2")
-        w_re = keep.tile([P, KD], BF16, name="w_re")
-        w_dst = w_re[:].rearrange("o (t h p e) -> o h p e t", t=9, h=2, e=2)
-        w_src = w_raw[:].rearrange("o (p h e t) -> o h p e t", h=2, e=2, t=9)
-        w32 = w_re[:].bitcast(F32)
+        w_pairs = keep.tile([P, KD], BF16, name="w_pairs")
+        w_pairs_view = w_pairs[:].rearrange("o (t h p e) -> o h p e t", t=TAPS, h=2, e=2)
+        w_raw_view = w_raw[:].rearrange("o (p h e t) -> o h p e t", h=2, e=2, t=TAPS)
+        w_words = w_pairs[:].bitcast(F32)
         w_grp = keep.tile([P, KD], BF16, name="w_grp", align_bytes=64)
-        wg32 = w_grp[:].bitcast(F32).rearrange("p (t o h) -> p t o h", o=P, h=2)
-        w_codes = keep.tile([P, 9 * P], U32, name="w_codes", align_bytes=64)
-        w_scales = keep.tile([P, 9 * P], U8, name="w_scales", align_bytes=64)
-        xcs = []
-        xss = []
-        accs = []
-        ress = []
-        for b in range(B):
-            xcs.append(keep.tile([P, XCOLS], U32, name="xc%d" % b, align_bytes=64))
-            xss.append(keep.tile([P, XCOLS], U8, name="xs%d" % b, align_bytes=64))
-            accs.append(keep.tile([P, HW], F32, name="acc%d" % b))
-            ress.append(keep.tile([P, HW], F32, name="res%d" % b))
-        live = {}
+        w_grp_words = w_grp[:].bitcast(F32).rearrange("p (t o h) -> p t o h", o=P, h=2)
+        w_codes = keep.tile([P, TAPS * P], U32, name="w_codes", align_bytes=64)
+        w_scales = keep.tile([P, TAPS * P], U8, name="w_scales", align_bytes=64)
+        x_codes = [keep.tile([P, XCOLS], U32, name="x_codes%d" % b, align_bytes=64) for b in range(B)]
+        x_scales = [keep.tile([P, XCOLS], U8, name="x_scales%d" % b, align_bytes=64) for b in range(B)]
+        acc = [keep.tile([P, HW], F32, name="acc%d" % b) for b in range(B)]
+        res = [keep.tile([P, HW], F32, name="res%d" % b) for b in range(B)]
 
-        def bank(key, shape, dtype, k):
-            t = psum.tile(shape, dtype, name="ps_%s" % key, tag="bank%d" % k)
-            live[key] = t
-            return t
+        free_banks = list(range(8))
+        held = {}
 
-        def op_w2(i):
-            junk = junkp.tile([P, 1152], BF16, name="junk_w")
+        def take_bank(key, shape, dtype):
+            k = free_banks.pop(0)
+            held[key] = (psum.tile(shape, dtype, name="ps_%s" % key, tag="bank%d" % k), k)
+            return held[key][0]
+
+        def bank_of(key):
+            return held[key][0]
+
+        def give_back(key):
+            free_banks.append(held[key][1])
+
+        def square_weights(i):
+            junk = scrap.tile([P, W_PIECE], BF16, name="junk_w")
             nc.scalar.activation(
-                out=junk[:], in_=w_raw[:, 1152 * i:1152 * (i + 1)], func=ACT.Square,
-                accum_out=w2p[:, i:i + 1],
+                out=junk[:], in_=w_raw[:, W_PIECE * i:W_PIECE * (i + 1)], func=ACT.Square,
+                accum_out=w2_parts[:, i:i + 1],
             )
 
-        def op_w2r():
-            nc.vector.tensor_reduce(out=w2[:], in_=w2p[:], axis=AX.X, op=ALU.add)
+        def pair_weights(half, g):
+            taps = slice(2 * g, min(2 * g + 2, TAPS))
+            rows = slice(64 * half, 64 * half + 64)
+            nc.vector.tensor_copy(out=w_pairs_view[:, :, rows, :, taps], in_=w_raw_view[:, :, rows, :, taps])
 
-        def op_wpre(pc, g):
-            t0 = 2 * g
-            t1 = min(t0 + 2, 9)
-            nc.vector.tensor_copy(
-                out=w_dst[:, :, 64 * pc:64 * pc + 64, :, t0:t1],
-                in_=w_src[:, :, 64 * pc:64 * pc + 64, :, t0:t1],
-            )
-
-        def op_wT(k, bk):
-            n = 4 if k < 4 else 2
-            wt = bank("wT%d" % k, [P, 4, P], F32, bk)
+        def transpose_weights(g):
+            n = 4 if g < 4 else 2
+            wt = take_bank("wT%d" % g, [P, 4, P], F32)
             for m in range(n):
-                c0 = (4 * k + m) * P
-                nc.tensor.transpose(wt[:, m, :], w32[:, c0:c0 + P], ident[:])
-
-        def op_wev(k):
-            n = 4 if k < 4 else 2
-            wt = live["wT%d" % k]
+                c0 = (4 * g + m) * P
+                nc.tensor.transpose(wt[:, m, :], w_words[:, c0:c0 + P], ident[:])
             nc.scalar.copy(
-                out=wg32[:, 2 * k:2 * k + n // 2],
+                out=w_grp_words[:, 2 * g:2 * g + n // 2],
                 in_=wt[:, 0:n, :].rearrange("p (a h) o -> p a o h", h=2),
             )
+            give_back("wT%d" % g)
 
-        def op_wq(i):
-            lo, n = ((0, 2048), (2048, 2048), (4096, 512))[i]
+        def quantise_weights(i):
+            lo, n = W_QUANT[i]
             nc.vector.quantize_mx(
                 out=w_codes[:, lo // 4:(lo + n) // 4].bitcast(FP8X4),
                 scales=w_scales[:, lo // 4:(lo + n) // 4],
                 in_=w_grp[:, lo:lo + n],
             )
 
-        def op_xre(b, part, h, on_scalar):
-            g6 = grps[b][:].rearrange("p (r h c i t) -> p r h c i t", r=ROWS, h=2, c=8, i=4, t=4)
-            r5 = raws[b][:].rearrange("p t (y c i) -> p t y c i", y=32, c=8, i=4)
-            if part == 1:
-                r0, r1 = 1 - h, 11 - h
-            else:
-                r0, r1 = 11 - h, 18 - h
+        def group_x(b, r0, r1, h, on_scalar):
             y0 = 16 * h + r0 - 1
             y1 = 16 * h + r1 - 1
             if on_scalar:
                 nc.scalar.copy(
-                    out=grps[b][:].rearrange("p (r h z t) -> p r h z t", r=ROWS, h=2, t=4)[:, r0:r1, h],
-                    in_=raws[b][:].rearrange("p t (y z) -> p y z t", y=32)[:, y0:y1],
+                    out=grp[b][:].rearrange("p (r h z t) -> p r h z t", r=ROWS, h=2, t=4)[:, r0:r1, h],
+                    in_=raw[b][:].rearrange("p t (y z) -> p y z t", y=32)[:, y0:y1],
                 )
             else:
+                dst = grp[b][:].rearrange("p (r h c i t) -> p r h c i t", r=ROWS, h=2, c=8, i=4, t=4)
+                src = raw[b][:].rearrange("p t (y c i) -> p t y c i", y=32, c=8, i=4)
                 nc.vector.tensor_copy(
-                    out=g6[:, r0:r1, h].rearrange("p r c i t -> p r c t i"),
-                    in_=r5[:, :, y0:y1].rearrange("p t y c i -> p y c t i"),
+                    out=dst[:, r0:r1, h].rearrange("p r c i t -> p r c t i"),
+                    in_=src[:, :, y0:y1].rearrange("p t y c i -> p y c t i"),
                 )
 
-        def op_xq(b, i):
-            lo, n = ((0, 2048), (2048, 512), (2560, 2048))[i]
+        def group_x_first(b):
+            for h in range(2):
+                group_x(b, 1 - h, 11 - h, h, False)
+
+        def group_x_rest(b, on_scalar):
+            for h in range(2):
+                group_x(b, 11 - h, 18 - h, h, on_scalar)
+
+        def quantise_x(b, i):
+            lo, n = X_QUANT[i]
             nc.vector.quantize_mx(
-                out=xcs[b][:, lo // 4:(lo + n) // 4].bitcast(FP8X4),
-                scales=xss[b][:, lo // 4:(lo + n) // 4],
-                in_=grps[b][:, lo:lo + n],
+                out=x_codes[b][:, lo // 4:(lo + n) // 4].bitcast(FP8X4),
+                scales=x_scales[b][:, lo // 4:(lo + n) // 4],
+                in_=grp[b][:, lo:lo + n],
             )
 
-        def op_xT(b, k, bk):
-            tp = bank("xT%d%d" % (b, k), [P, 8, P], BF16, bk)
-            for cl in range(2):
-                ch = 4 * k + 2 * cl + 1
-                for j in range(4):
-                    nc.tensor.transpose(tp[:, 4 * cl + j, :], raws[b][:, j, ch * P:(ch + 1) * P], ident_bf[:])
-
-        def op_sq(b, c):
-            tp = live["xT%d%d" % (b, c // 2)]
-            cl = c % 2
-            junk = junkp.tile([P, 4 * P], BF16, name="junk_x")
-            nc.scalar.activation(
-                out=junk[:], in_=tp[:, 4 * cl:4 * cl + 4, :].rearrange("p j c -> p (j c)"), func=ACT.Square,
-                accum_out=s_act[:, b, 2 + 2 * c:3 + 2 * c],
-            )
-
-        def op_xG(b, q, bk):
-            if q == 0:
-                bank("xG%d" % b, [P, 4, P], F32, bk)
-            g = live["xG%d" % b]
-            ch = 2 * q
+        def gram(b, q):
+            g = bank_of("gram%d" % b)
+            blocks = [raw[b][:, j, 2 * q * P:(2 * q + 1) * P] for j in range(4)]
             for j in range(4):
-                blk = raws[b][:, j, ch * P:(ch + 1) * P]
-                nc.tensor.matmul(g[:, q, :], lhsT=blk, rhs=blk, start=(j == 0), stop=(j == 3))
+                nc.tensor.matmul(g[:, q, :], lhsT=blocks[j], rhs=blocks[j], start=(j == 0), stop=(j == 3))
 
-        def op_dg(b, q):
-            junk = junkp.tile([P, P], F32, name="junk_g")
-            nc.vector.scalar_tensor_tensor(
-                out=junk[:], in0=live["xG%d" % b][:, q, :], scalar=1.0, in1=ident[:],
-                op0=ALU.mult, op1=ALU.mult, accum_out=s_dve[:, b, 1 + 2 * q:2 + 2 * q],
-            )
+        def flip(b, k):
+            tp = take_bank("flip%d%d" % (b, k), [P, 8, P], BF16)
+            for n in range(2):
+                ch = 4 * k + 2 * n + 1
+                for j in range(4):
+                    nc.tensor.transpose(tp[:, 4 * n + j, :], raw[b][:, j, ch * P:(ch + 1) * P], ident_bf[:])
 
-        def op_f(b, bk):
-            f = bank("f%d" % b, [P, 8], F32, bk)
+        def stats_on_tensor(b):
+            take_bank("gram%d" % b, [P, 4, P], F32)
+            gram(b, 0)
+            flip(b, 0)
+            gram(b, 1)
+            gram(b, 2)
+            flip(b, 1)
+            gram(b, 3)
+
+        def square_flipped(b, k):
+            tp = bank_of("flip%d%d" % (b, k))
+            for n in range(2):
+                ch = 4 * k + 2 * n + 1
+                junk = scrap.tile([P, 4 * P], BF16, name="junk_x")
+                nc.scalar.activation(
+                    out=junk[:], in_=tp[:, 4 * n:4 * n + 4, :].rearrange("p j c -> p (j c)"), func=ACT.Square,
+                    accum_out=s_act[:, b, 1 + ch:2 + ch],
+                )
+            give_back("flip%d%d" % (b, k))
+
+        def gram_diagonals(b):
+            g = bank_of("gram%d" % b)
+            for q in range(4):
+                junk = scrap.tile([P, P], F32, name="junk_g")
+                nc.vector.scalar_tensor_tensor(
+                    out=junk[:], in0=g[:, q, :], scalar=1.0, in1=ident[:],
+                    op0=ALU.mult, op1=ALU.mult, accum_out=s_dve[:, b, 1 + 2 * q:2 + 2 * q],
+                )
+            give_back("gram%d" % b)
+
+        def box_sum():
+            f = take_bank("box", [P, B, 8], F32)
             for rel in range(3):
                 nc.tensor.matmul(
-                    f[:], lhsT=band[:, rel * P:(rel + 1) * P], rhs=s_sum[:, b, 2 - rel:10 - rel],
+                    f[:], lhsT=band[:, rel * P:(rel + 1) * P], rhs=s_sum[:, :, 2 - rel:10 - rel],
                     start=(rel == 0), stop=(rel == 2),
                 )
 
-        def op_sadd(b):
-            nc.vector.tensor_tensor(out=s_sum[:, b, :], in0=s_act[:, b, :], in1=s_dve[:, b, :], op=ALU.add)
-
-        def op_x2c(b):
-            nc.scalar.copy(out=x2sb[:, 8 * b:8 * b + 8], in_=live["f%d" % b][:])
-
-        def op_bc(b, w, bk):
-            xb = bank("bc%d%d" % (b, w), [P, 512], F32, bk)
+        def spread_x2(b, w):
+            xb = take_bank("x2_%d%d" % (b, w), [P, 512], F32)
             xb5 = xb[:].rearrange("p (u r h z) -> p u r h z", u=2, r=4, h=2)
             for h in range(2):
                 for u in range(2):
-                    col = 8 * b + 4 * h + 2 * w + u
-                    nc.tensor.transpose(
-                        xb5[:, u, :, h, :], x2sb[:, col:col + 1].to_broadcast([P, P]), ident[:]
-                    )
+                    ch = 4 * h + 2 * w + u
+                    nc.tensor.transpose(xb5[:, u, :, h, :], x2[:, b, ch:ch + 1].to_broadcast([P, P]), ident[:])
 
-        def op_mx(b, w, j, bk):
-            pj = bank("mx%d%d%d" % (b, w, j), [P, 512], F32, bk)
+        def window(b, w):
+            return acc[b][:, 512 * w:512 * w + 512]
+
+        def mx_group(b, w, j):
+            pj = take_bank("mx%d%d%d" % (b, w, j), [P, 512], F32)
             for i in range(3):
                 tap = 3 * i + j
                 c0 = 64 * (8 * w + i)
@@ -259,46 +237,105 @@ def tile_rbf_conv2d_kernel(tc, x, weight, out):
                     out=pj[:],
                     lhsT=w_codes[:, tap * P:(tap + 1) * P].bitcast(FP8X4),
                     lhsT_scale=w_scales[:, tap * P:(tap + 1) * P],
-                    rhs=xcs[b][:, c0:c0 + 512].bitcast(FP8X4),
-                    rhs_scale=xss[b][:, c0:c0 + 512],
+                    rhs=x_codes[b][:, c0:c0 + 512].bitcast(FP8X4),
+                    rhs_scale=x_scales[b][:, c0:c0 + 512],
                     start=(i == 0), stop=(i == 2),
                 )
 
-        def op_t(b, w):
-            nc.scalar.activation(
-                out=accs[b][:, 512 * w:512 * w + 512], in_=live["mx%d%d1" % (b, w)][:],
-                func=ACT.Identity, scale=-2.0,
-            )
+        def take_middle(b, w):
+            nc.scalar.activation(out=window(b, w), in_=bank_of("mx%d%d1" % (b, w))[:], func=ACT.Identity, scale=-2.0)
+            give_back("mx%d%d1" % (b, w))
 
-        def op_stt(b, w, j):
-            a3 = accs[b][:, 512 * w:512 * w + 512].rearrange("p (s z) -> p s z", z=32)
-            p3 = live["mx%d%d%d" % (b, w, j)][:].rearrange("p (s z) -> p s z", z=32)
+        def add_side(b, w, j):
+            a3 = window(b, w).rearrange("p (s z) -> p s z", z=32)
+            p3 = bank_of("mx%d%d%d" % (b, w, j))[:].rearrange("p (s z) -> p s z", z=32)
             if j == 0:
                 dst, src = a3[:, :, 1:32], p3[:, :, 0:31]
             else:
                 dst, src = a3[:, :, 0:31], p3[:, :, 1:32]
             nc.vector.scalar_tensor_tensor(out=dst, in0=src, scalar=-2.0, in1=dst, op0=ALU.mult, op1=ALU.add)
+            give_back("mx%d%d%d" % (b, w, j))
 
-        def op_sx(b, w):
-            a = accs[b][:, 512 * w:512 * w + 512]
-            nc.vector.tensor_tensor(out=a, in0=live["bc%d%d" % (b, w)][:], in1=a, op=ALU.add)
+        def add_x2(b, w):
+            nc.vector.tensor_tensor(out=window(b, w), in0=bank_of("x2_%d%d" % (b, w))[:], in1=window(b, w), op=ALU.add)
+            give_back("x2_%d%d" % (b, w))
 
-        def op_relu(b, w):
-            res = ress[b]
-            res5 = res[:].rearrange("p (h w y z) -> p w y h z", h=2, w=2, y=8)
-            res4 = res[:].rearrange("p (h w n) -> p h w n", h=2, w=2)
-            out4 = out[b].rearrange("o (h w y) z -> o h w (y z)", h=2, w=2)
+        def finish(b, w):
             nc.scalar.activation(
-                out=res5[:, w],
-                in_=accs[b][:, 512 * w:512 * w + 512].rearrange("p (y h z) -> p y h z", y=8, h=2),
+                out=res[b][:].rearrange("p (h w y z) -> p w y h z", h=2, w=2, y=8)[:, w],
+                in_=window(b, w).rearrange("p (y h z) -> p y h z", y=8, h=2),
                 func=ACT.Relu, bias=w2[:, 0:1],
             )
-            nc.sync.dma_start(out=out4[:, :, w, :], in_=res4[:, :, w, :])
+            nc.sync.dma_start(
+                out=out[b].rearrange("o (h w y) z -> o h w (y z)", h=2, w=2)[:, :, w, :],
+                in_=res[b][:].rearrange("p (h w n) -> p h w n", h=2, w=2)[:, :, w, :],
+            )
 
-        ops = {
-            "w2": op_w2, "w2r": op_w2r, "wpre": op_wpre, "wT": op_wT, "wev": op_wev, "wq": op_wq,
-            "xre": op_xre, "xq": op_xq, "xT": op_xT, "sq": op_sq, "xG": op_xG, "dg": op_dg, "sadd": op_sadd, "f": op_f, "x2c": op_x2c,
-            "bc": op_bc, "mx": op_mx, "t": op_t, "stt": op_stt, "sx": op_sx, "relu": op_relu,
-        }
-        for step in PLAN:
-            ops[step[0]](*step[1:])
+        square_weights(0)
+        square_weights(1)
+        for half in range(2):
+            for g in range(5):
+                pair_weights(half, g)
+        for g in range(5):
+            transpose_weights(g)
+
+        stats_on_tensor(0)
+        square_flipped(0, 0)
+        square_flipped(0, 1)
+        group_x_first(0)
+        for i in range(3):
+            quantise_weights(i)
+        quantise_x(0, 0)
+        quantise_x(0, 1)
+        group_x_rest(0, False)
+        quantise_x(0, 2)
+        stats_on_tensor(1)
+        square_flipped(1, 0)
+        group_x_first(1)
+        quantise_x(1, 0)
+        quantise_x(1, 1)
+
+        for j in (1, 0, 2):
+            mx_group(0, 0, j)
+        take_middle(0, 0)
+        gram_diagonals(0)
+        add_side(0, 0, 0)
+        add_side(0, 0, 2)
+        group_x_rest(1, True)
+        quantise_x(1, 2)
+
+        for j in (1, 0, 2):
+            mx_group(0, 1, j)
+        take_middle(0, 1)
+        square_flipped(1, 1)
+        gram_diagonals(1)
+        nc.vector.tensor_tensor(out=s_sum[:], in0=s_act[:], in1=s_dve[:], op=ALU.add)
+        add_side(0, 1, 0)
+        add_side(0, 1, 2)
+        square_weights(2)
+
+        mx_group(1, 0, 1)
+        mx_group(1, 0, 0)
+        box_sum()
+        mx_group(1, 0, 2)
+        take_middle(1, 0)
+        nc.scalar.copy(out=x2[:], in_=bank_of("box")[:])
+        give_back("box")
+        square_weights(3)
+        add_side(1, 0, 0)
+        add_side(1, 0, 2)
+        nc.vector.tensor_reduce(out=w2[:], in_=w2_parts[:], axis=AX.X, op=ALU.add)
+
+        mx_group(1, 1, 1)
+        take_middle(1, 1)
+        for b, w in ((0, 0), (0, 1), (1, 0), (1, 1)):
+            spread_x2(b, w)
+        for b, w in ((0, 0), (0, 1), (1, 0)):
+            add_x2(b, w)
+            finish(b, w)
+        mx_group(1, 1, 0)
+        mx_group(1, 1, 2)
+        add_side(1, 1, 0)
+        add_x2(1, 1)
+        add_side(1, 1, 2)
+        finish(1, 1)

@@ -112,7 +112,11 @@ def tile_rbf_conv2d_kernel(tc, x, weight, out):
         def pair_weights(half, g):
             taps = slice(2 * g, min(2 * g + 2, TAPS))
             rows = slice(64 * half, 64 * half + 64)
-            nc.vector.tensor_copy(out=w_pairs_view[:, :, rows, :, taps], in_=w_raw_view[:, :, rows, :, taps])
+            if g < 3:
+                nc.vector.tensor_copy(out=w_pairs_view[:, :, rows, :, taps], in_=w_raw_view[:, :, rows, :, taps])
+            else:
+                for h in range(2):
+                    nc.scalar.copy(out=w_pairs_view[:, h, rows, :, taps], in_=w_raw_view[:, h, rows, :, taps])
 
         def transpose_weights(g):
             n = 4 if g < 4 else 2
@@ -228,51 +232,52 @@ def tile_rbf_conv2d_kernel(tc, x, weight, out):
         def window(b, w):
             return acc[b][:, 512 * w:512 * w + 512]
 
-        def mx_group(b, w, j):
+        def mx_group(b, w, j, pieces=1):
             pj = take_bank("mx%d%d%d" % (b, w, j), [P, 512], F32)
-            for i in range(3):
-                tap = 3 * i + j
-                c0 = 64 * (8 * w + i)
-                nc.tensor.matmul_mx(
-                    out=pj[:],
-                    lhsT=w_codes[:, tap * P:(tap + 1) * P].bitcast(FP8X4),
-                    lhsT_scale=w_scales[:, tap * P:(tap + 1) * P],
-                    rhs=x_codes[b][:, c0:c0 + 512].bitcast(FP8X4),
-                    rhs_scale=x_scales[b][:, c0:c0 + 512],
-                    start=(i == 0), stop=(i == 2),
-                )
+            n = 512 // pieces
+            for lo in range(0, 512, n):
+                for i in range(3):
+                    tap = 3 * i + j
+                    c0 = 64 * (8 * w + i) + lo
+                    nc.tensor.matmul_mx(
+                        out=pj[:, lo:lo + n],
+                        lhsT=w_codes[:, tap * P:(tap + 1) * P].bitcast(FP8X4),
+                        lhsT_scale=w_scales[:, tap * P:(tap + 1) * P],
+                        rhs=x_codes[b][:, c0:c0 + n].bitcast(FP8X4),
+                        rhs_scale=x_scales[b][:, c0:c0 + n],
+                        start=(i == 0), stop=(i == 2),
+                    )
 
         def take_middle(b, w):
             nc.scalar.activation(out=window(b, w), in_=bank_of("mx%d%d1" % (b, w))[:], func=ACT.Identity, scale=-2.0)
             give_back("mx%d%d1" % (b, w))
 
-        def add_side(b, w, j):
-            a3 = window(b, w).rearrange("p (s z) -> p s z", z=32)
-            p3 = bank_of("mx%d%d%d" % (b, w, j))[:].rearrange("p (s z) -> p s z", z=32)
+        def add_side(b, w, j, s0=0, s1=16):
+            a3 = window(b, w).rearrange("p (s z) -> p s z", z=32)[:, s0:s1]
+            p3 = bank_of("mx%d%d%d" % (b, w, j))[:].rearrange("p (s z) -> p s z", z=32)[:, s0:s1]
             if j == 0:
                 dst, src = a3[:, :, 1:32], p3[:, :, 0:31]
             else:
                 dst, src = a3[:, :, 0:31], p3[:, :, 1:32]
             nc.vector.scalar_tensor_tensor(out=dst, in0=src, scalar=-2.0, in1=dst, op0=ALU.mult, op1=ALU.add)
-            give_back("mx%d%d%d" % (b, w, j))
+            if s1 == 16:
+                give_back("mx%d%d%d" % (b, w, j))
 
         def add_x2(b, w):
             nc.vector.tensor_tensor(out=window(b, w), in0=bank_of("x2_%d%d" % (b, w))[:], in1=window(b, w), op=ALU.add)
             give_back("x2_%d%d" % (b, w))
 
-        def finish(b, w):
+        def finish(b, w, y0=0, y1=8):
             nc.scalar.activation(
-                out=res[b][:].rearrange("p (h w y z) -> p w y h z", h=2, w=2, y=8)[:, w],
-                in_=window(b, w).rearrange("p (y h z) -> p y h z", y=8, h=2),
+                out=res[b][:].rearrange("p (h w y z) -> p w y h z", h=2, w=2, y=8)[:, w, y0:y1],
+                in_=window(b, w).rearrange("p (y h z) -> p y h z", y=8, h=2)[:, y0:y1],
                 func=ACT.Relu, bias=w2[:, 0:1],
             )
             nc.sync.dma_start(
-                out=out[b].rearrange("o (h w y) z -> o h w (y z)", h=2, w=2)[:, :, w, :],
-                in_=res[b][:].rearrange("p (h w n) -> p h w n", h=2, w=2)[:, :, w, :],
+                out=out[b].rearrange("o (h w y) z -> o h w y z", h=2, w=2)[:, :, w, y0:y1, :],
+                in_=res[b][:].rearrange("p (h w y z) -> p h w y z", h=2, w=2, y=8)[:, :, w, y0:y1, :],
             )
 
-        square_weights(0)
-        square_weights(1)
         for half in range(2):
             for g in range(5):
                 pair_weights(half, g)
@@ -297,6 +302,7 @@ def tile_rbf_conv2d_kernel(tc, x, weight, out):
 
         for j in (1, 0, 2):
             mx_group(0, 0, j)
+        square_weights(0)
         take_middle(0, 0)
         gram_diagonals(0)
         add_side(0, 0, 0)
@@ -308,6 +314,7 @@ def tile_rbf_conv2d_kernel(tc, x, weight, out):
             mx_group(0, 1, j)
         take_middle(0, 1)
         square_flipped(1, 1)
+        square_weights(1)
         gram_diagonals(1)
         nc.vector.tensor_tensor(out=s_sum[:], in0=s_act[:], in1=s_dve[:], op=ALU.add)
         add_side(0, 1, 0)
@@ -333,9 +340,11 @@ def tile_rbf_conv2d_kernel(tc, x, weight, out):
         for b, w in ((0, 0), (0, 1), (1, 0)):
             add_x2(b, w)
             finish(b, w)
-        mx_group(1, 1, 0)
-        mx_group(1, 1, 2)
-        add_side(1, 1, 0)
         add_x2(1, 1)
-        add_side(1, 1, 2)
-        finish(1, 1)
+        mx_group(1, 1, 0)
+        mx_group(1, 1, 2, pieces=2)
+        add_side(1, 1, 0)
+        add_side(1, 1, 2, 0, 8)
+        finish(1, 1, 0, 4)
+        add_side(1, 1, 2, 8, 16)
+        finish(1, 1, 4, 8)

@@ -102,6 +102,16 @@ def tile_rbf_conv2d_kernel(tc, x, weight, out):
         def give_back(key):
             free_banks.append(held[key][1])
 
+        def warm_up():
+            junk = take_bank("warm", [P, 512], F32)
+            for i in range(2):
+                for n in range(2):
+                    c0 = W_PIECE * i + 512 * n
+                    nc.tensor.matmul(
+                        junk[:], lhsT=w_raw[:, c0:c0 + P], rhs=w_raw[:, c0:c0 + 512], start=True, stop=True
+                    )
+            give_back("warm")
+
         def square_weights(i):
             junk = scrap.tile([P, W_PIECE], BF16, name="junk_w")
             nc.scalar.activation(
@@ -278,6 +288,7 @@ def tile_rbf_conv2d_kernel(tc, x, weight, out):
                 in_=res[b][:].rearrange("p (h w y z) -> p h w y z", h=2, w=2, y=8)[:, :, w, y0:y1, :],
             )
 
+        warm_up()
         for half in range(2):
             for g in range(5):
                 pair_weights(half, g)

@@ -19,10 +19,11 @@ B = 2
 HW = 1024
 KD = 4608
 TAPS = 9
-ROWS = 18
-XCOLS = ROWS * 64
+TAP_ORDER = [3 * i + j for j in (1, 2, 0) for i in (1, 0, 2)]
+GRAM = ((0, 2, 4, 6), (0, 2, 4, 6))
+FLIP = ((1, 3, 5, 7), (1, 3, 5, 7))
+PLANE = 10 * 64
 W_PIECE = KD // 4
-X_QUANT = ((0, 2048), (2048, 512), (2560, 2048))
 W_QUANT = ((0, 2048), (2048, 2048), (4096, 512))
 
 
@@ -35,13 +36,24 @@ def tile_rbf_conv2d_kernel(tc, x, weight, out):
         ctx.enter_context(tc.manual_schedule())
 
         w_raw = keep.tile([P, KD], BF16, name="w_raw")
-        for i in range(4):
+        raw = [keep.tile([P, 4, HW], BF16, name="raw%d" % b) for b in range(B)]
+
+        def load_x(b, y0, y1):
+            nc.sync.dma_start(
+                out=raw[b][:, :, 32 * y0:32 * y1],
+                in_=x[b].rearrange("(t p) h w -> p t (h w)", t=4)[:, :, 32 * y0:32 * y1],
+            )
+
+        def load_w(i):
             cols = slice(W_PIECE * i, W_PIECE * (i + 1))
             nc.sync.dma_start(out=w_raw[:, cols], in_=weight[:, cols])
-        raw = []
-        for b in range(B):
-            raw.append(keep.tile([P, 4, HW], BF16, name="raw%d" % b))
-            nc.sync.dma_start(out=raw[b][:], in_=x[b].rearrange("(p j) h w -> p j (h w)", j=4))
+
+        load_x(0, 0, 16)
+        load_x(0, 16, 32)
+        for i in range(4):
+            load_w(i)
+        load_x(1, 0, 16)
+        load_x(1, 16, 32)
 
         ident = keep.tile([P, P], F32, name="ident")
         make_identity(nc, ident[:])
@@ -52,11 +64,16 @@ def tile_rbf_conv2d_kernel(tc, x, weight, out):
         s_dve = keep.tile([P, B, 10], F32, name="s_dve")
         nc.gpsimd.memset(s_dve[:], 0.0)
         grp = []
+        x_codes = []
+        x_scales = []
         for b in range(B):
-            grp.append(keep.tile([P, XCOLS * 4], BF16, name="grp%d" % b, align_bytes=64))
-            halves = grp[b][:].rearrange("p (r h n) -> p r h n", r=ROWS, h=2)
-            nc.gpsimd.memset(halves[:, 0, 0, :], 0.0)
-            nc.gpsimd.memset(halves[:, ROWS - 1, 1, :], 0.0)
+            grp.append(keep.tile([P, HW * 4], BF16, name="grp%d" % b, align_bytes=64))
+            x_codes.append(keep.tile([P, 2 * PLANE], U32, name="x_codes%d" % b, align_bytes=64))
+            x_scales.append(keep.tile([P, 2 * PLANE], U8, name="x_scales%d" % b, align_bytes=64))
+            nc.gpsimd.memset(x_scales[b][:].bitcast(U32), 0)
+            planes = x_codes[b][:].rearrange("p (e r n) -> p e r n", e=2, r=10)
+            nc.gpsimd.memset(planes[:, :, 0, 0:16], 0)
+            nc.gpsimd.memset(planes[:, :, 9, 48:64], 0)
         ident_bf = keep.tile([P, P], BF16, name="ident_bf")
         nc.vector.tensor_copy(out=ident_bf[:], in_=ident[:])
         id3 = ident[:].rearrange("p (a z) -> p a z", z=32)
@@ -75,16 +92,11 @@ def tile_rbf_conv2d_kernel(tc, x, weight, out):
         x2 = keep.tile([P, B, 8], F32, name="x2")
         w2_parts = keep.tile([P, 4], F32, name="w2_parts")
         w2 = keep.tile([P, 1], F32, name="w2")
-        w_pairs = keep.tile([P, KD], BF16, name="w_pairs")
-        w_pairs_view = w_pairs[:].rearrange("o (t h p e) -> o h p e t", t=TAPS, h=2, e=2)
-        w_raw_view = w_raw[:].rearrange("o (p h e t) -> o h p e t", h=2, e=2, t=TAPS)
-        w_words = w_pairs[:].bitcast(F32)
+        w_by_tap = w_raw[:].rearrange("o (t c a) -> o t a c", t=4, a=TAPS)
         w_grp = keep.tile([P, KD], BF16, name="w_grp", align_bytes=64)
-        w_grp_words = w_grp[:].bitcast(F32).rearrange("p (t o h) -> p t o h", o=P, h=2)
+        w_grp_view = w_grp[:].rearrange("p (a o t) -> p a o t", o=P, t=4)
         w_codes = keep.tile([P, TAPS * P], U32, name="w_codes", align_bytes=64)
         w_scales = keep.tile([P, TAPS * P], U8, name="w_scales", align_bytes=64)
-        x_codes = [keep.tile([P, XCOLS], U32, name="x_codes%d" % b, align_bytes=64) for b in range(B)]
-        x_scales = [keep.tile([P, XCOLS], U8, name="x_scales%d" % b, align_bytes=64) for b in range(B)]
         acc = [keep.tile([P, HW], F32, name="acc%d" % b) for b in range(B)]
         res = [keep.tile([P, HW], F32, name="res%d" % b) for b in range(B)]
 
@@ -102,16 +114,6 @@ def tile_rbf_conv2d_kernel(tc, x, weight, out):
         def give_back(key):
             free_banks.append(held[key][1])
 
-        def warm_up():
-            junk = take_bank("warm", [P, 512], F32)
-            for i in range(2):
-                for n in range(2):
-                    c0 = W_PIECE * i + 512 * n
-                    nc.tensor.matmul(
-                        junk[:], lhsT=w_raw[:, c0:c0 + P], rhs=w_raw[:, c0:c0 + 512], start=True, stop=True
-                    )
-            give_back("warm")
-
         def square_weights(i):
             junk = scrap.tile([P, W_PIECE], BF16, name="junk_w")
             nc.scalar.activation(
@@ -119,24 +121,16 @@ def tile_rbf_conv2d_kernel(tc, x, weight, out):
                 accum_out=w2_parts[:, i:i + 1],
             )
 
-        def pair_weights(half, g):
-            taps = slice(2 * g, min(2 * g + 2, TAPS))
-            rows = slice(64 * half, 64 * half + 64)
-            if g < 3:
-                nc.vector.tensor_copy(out=w_pairs_view[:, :, rows, :, taps], in_=w_raw_view[:, :, rows, :, taps])
-            else:
-                for h in range(2):
-                    nc.scalar.copy(out=w_pairs_view[:, h, rows, :, taps], in_=w_raw_view[:, h, rows, :, taps])
+        def transpose_weights(t):
+            for k, tap in enumerate(TAP_ORDER):
+                nc.tensor.transpose(bank_of("wT%d" % (k // 2))[:, k % 2, t, :], w_by_tap[:, t, tap, :], ident_bf[:])
 
-        def transpose_weights(g):
-            n = 4 if g < 4 else 2
-            wt = take_bank("wT%d" % g, [P, 4, P], F32)
-            for m in range(n):
-                c0 = (4 * g + m) * P
-                nc.tensor.transpose(wt[:, m, :], w_words[:, c0:c0 + P], ident[:])
-            nc.scalar.copy(
-                out=w_grp_words[:, 2 * g:2 * g + n // 2],
-                in_=wt[:, 0:n, :].rearrange("p (a h) o -> p a o h", h=2),
+        def copy_weights(g):
+            n = min(2, TAPS - 2 * g)
+            copy = nc.vector.tensor_copy if g == 1 else nc.scalar.copy
+            copy(
+                out=w_grp_view[:, 2 * g:2 * g + n],
+                in_=bank_of("wT%d" % g)[:, 0:n].rearrange("p a t o -> p a o t"),
             )
             give_back("wT%d" % g)
 
@@ -148,64 +142,54 @@ def tile_rbf_conv2d_kernel(tc, x, weight, out):
                 in_=w_grp[:, lo:lo + n],
             )
 
-        def group_x(b, r0, r1, h, on_scalar):
-            y0 = 16 * h + r0 - 1
-            y1 = 16 * h + r1 - 1
-            if on_scalar:
-                nc.scalar.copy(
-                    out=grp[b][:].rearrange("p (r h z t) -> p r h z t", r=ROWS, h=2, t=4)[:, r0:r1, h],
-                    in_=raw[b][:].rearrange("p t (y z) -> p y z t", y=32)[:, y0:y1],
-                )
-            else:
-                dst = grp[b][:].rearrange("p (r h c i t) -> p r h c i t", r=ROWS, h=2, c=8, i=4, t=4)
-                src = raw[b][:].rearrange("p t (y c i) -> p t y c i", y=32, c=8, i=4)
-                nc.vector.tensor_copy(
-                    out=dst[:, r0:r1, h].rearrange("p r c i t -> p r c t i"),
-                    in_=src[:, :, y0:y1].rearrange("p t y c i -> p y c t i"),
-                )
-
-        def group_x_first(b):
-            for h in range(2):
-                group_x(b, 1 - h, 11 - h, h, False)
-
-        def group_x_rest(b, on_scalar):
-            for h in range(2):
-                group_x(b, 11 - h, 18 - h, h, on_scalar)
-
-        def quantise_x(b, i):
-            lo, n = X_QUANT[i]
-            nc.vector.quantize_mx(
-                out=x_codes[b][:, lo // 4:(lo + n) // 4].bitcast(FP8X4),
-                scales=x_scales[b][:, lo // 4:(lo + n) // 4],
-                in_=grp[b][:, lo:lo + n],
+        def group_x(b, half, e, on_scalar=False):
+            copy = nc.scalar.copy if on_scalar else nc.vector.tensor_copy
+            hs = slice(2 * half, 2 * half + 2)
+            copy(
+                out=grp[b][:].rearrange("p (e r h m t) -> p e r h m t", e=2, r=8, h=4, t=4)[:, e, :, hs],
+                in_=raw[b][:].rearrange("p t (h r m e) -> p e r h m t", h=4, r=8, e=2)[:, e, :, hs],
             )
 
-        def gram(b, q):
-            g = bank_of("gram%d" % b)
-            blocks = [raw[b][:, j, 2 * q * P:(2 * q + 1) * P] for j in range(4)]
+        def quantise_x(b, e):
+            c0 = PLANE * e + 64
+            nc.vector.quantize_mx(
+                out=x_codes[b][:, c0:c0 + 512].bitcast(FP8X4),
+                scales=x_scales[b][:, c0:c0 + 512],
+                in_=grp[b][:, 2048 * e:2048 * (e + 1)],
+            )
+
+        def copy_halo(b, e):
+            for tile in (x_codes[b], x_scales[b]):
+                rows = tile[:, PLANE * e:PLANE * (e + 1)].rearrange("p (r n) -> p r n", r=10)
+                nc.gpsimd.tensor_copy(out=rows[:, 0, 16:64], in_=rows[:, 8, 0:48])
+                nc.gpsimd.tensor_copy(out=rows[:, 9, 0:48], in_=rows[:, 1, 16:64])
+
+        def gram(b, ch):
+            k, q = divmod(GRAM[b].index(ch), 4)
+            if q == 0:
+                take_bank("gram%d%d" % (b, k), [P, 4, P], F32)
+            blocks = [raw[b][:, j, ch * P:(ch + 1) * P] for j in range(4)]
             for j in range(4):
-                nc.tensor.matmul(g[:, q, :], lhsT=blocks[j], rhs=blocks[j], start=(j == 0), stop=(j == 3))
+                nc.tensor.matmul(bank_of("gram%d%d" % (b, k))[:, q, :], lhsT=blocks[j], rhs=blocks[j], start=(j == 0), stop=(j == 3))
 
-        def flip(b, k):
-            tp = take_bank("flip%d%d" % (b, k), [P, 8, P], BF16)
-            for n in range(2):
-                ch = 4 * k + 2 * n + 1
-                for j in range(4):
-                    nc.tensor.transpose(tp[:, 4 * n + j, :], raw[b][:, j, ch * P:(ch + 1) * P], ident_bf[:])
+        def flip(b, ch):
+            k, n = divmod(FLIP[b].index(ch), 2)
+            if n == 0:
+                take_bank("flip%d%d" % (b, k), [P, 8, P], BF16)
+            for j in range(4):
+                nc.tensor.transpose(bank_of("flip%d%d" % (b, k))[:, 4 * n + j, :], raw[b][:, j, ch * P:(ch + 1) * P], ident_bf[:])
 
-        def stats_on_tensor(b):
-            take_bank("gram%d" % b, [P, 4, P], F32)
-            gram(b, 0)
-            flip(b, 0)
-            gram(b, 1)
-            gram(b, 2)
-            flip(b, 1)
-            gram(b, 3)
+        def stats_on_tensor(b, chunks):
+            for ch in chunks:
+                if ch in GRAM[b]:
+                    gram(b, ch)
+                else:
+                    flip(b, ch)
 
         def square_flipped(b, k):
             tp = bank_of("flip%d%d" % (b, k))
             for n in range(2):
-                ch = 4 * k + 2 * n + 1
+                ch = FLIP[b][2 * k + n]
                 junk = scrap.tile([P, 4 * P], BF16, name="junk_x")
                 nc.scalar.activation(
                     out=junk[:], in_=tp[:, 4 * n:4 * n + 4, :].rearrange("p j c -> p (j c)"), func=ACT.Square,
@@ -213,15 +197,16 @@ def tile_rbf_conv2d_kernel(tc, x, weight, out):
                 )
             give_back("flip%d%d" % (b, k))
 
-        def gram_diagonals(b):
-            g = bank_of("gram%d" % b)
+        def gram_diagonals(b, k):
+            g = bank_of("gram%d%d" % (b, k))
             for q in range(4):
+                ch = GRAM[b][4 * k + q]
                 junk = scrap.tile([P, P], F32, name="junk_g")
                 nc.vector.scalar_tensor_tensor(
                     out=junk[:], in0=g[:, q, :], scalar=1.0, in1=ident[:],
-                    op0=ALU.mult, op1=ALU.mult, accum_out=s_dve[:, b, 1 + 2 * q:2 + 2 * q],
+                    op0=ALU.mult, op1=ALU.mult, accum_out=s_dve[:, b, 1 + ch:2 + ch],
                 )
-            give_back("gram%d" % b)
+            give_back("gram%d%d" % (b, k))
 
         def box_sum():
             f = take_bank("box", [P, B, 8], F32)
@@ -231,131 +216,143 @@ def tile_rbf_conv2d_kernel(tc, x, weight, out):
                     start=(rel == 0), stop=(rel == 2),
                 )
 
-        def spread_x2(b, w):
-            xb = take_bank("x2_%d%d" % (b, w), [P, 512], F32)
-            xb5 = xb[:].rearrange("p (u r h z) -> p u r h z", u=2, r=4, h=2)
-            for h in range(2):
-                for u in range(2):
-                    ch = 4 * h + 2 * w + u
-                    nc.tensor.transpose(xb5[:, u, :, h, :], x2[:, b, ch:ch + 1].to_broadcast([P, P]), ident[:])
+        def spread_x2(b, k):
+            xb = take_bank("x2_%d%d" % (b, k), [P, 4, P], F32)
+            for h in range(4):
+                ch = 2 * h + k
+                nc.tensor.transpose(xb[:, h, :], x2[:, b, ch:ch + 1].to_broadcast([P, P]), ident[:])
 
-        def window(b, w):
-            return acc[b][:, 512 * w:512 * w + 512]
+        def mx_taps(b, e, shifted):
+            if shifted:
+                return [(3 * i + 2 * e, 1 - e, i) for i in (1, 0, 2)]
+            return [(3 * i + 1, e, i) for i in (1, 0, 2)] + [(3 * i + 2 - 2 * e, 1 - e, i) for i in (1, 0, 2)]
 
-        def mx_group(b, w, j, pieces=1):
-            pj = take_bank("mx%d%d%d" % (b, w, j), [P, 512], F32)
+        def mx_group(b, e, shifted, pieces=1):
+            ps = take_bank("mx%d%d%d" % (b, e, shifted), [P, 512], F32)
             n = 512 // pieces
+            taps = mx_taps(b, e, shifted)
             for lo in range(0, 512, n):
-                for i in range(3):
-                    tap = 3 * i + j
-                    c0 = 64 * (8 * w + i) + lo
+                for k, (tap, plane, i) in enumerate(taps):
+                    w0 = P * TAP_ORDER.index(tap)
+                    c0 = PLANE * plane + 64 * i + lo
                     nc.tensor.matmul_mx(
-                        out=pj[:, lo:lo + n],
-                        lhsT=w_codes[:, tap * P:(tap + 1) * P].bitcast(FP8X4),
-                        lhsT_scale=w_scales[:, tap * P:(tap + 1) * P],
+                        out=ps[:, lo:lo + n],
+                        lhsT=w_codes[:, w0:w0 + P].bitcast(FP8X4),
+                        lhsT_scale=w_scales[:, w0:w0 + P],
                         rhs=x_codes[b][:, c0:c0 + n].bitcast(FP8X4),
                         rhs_scale=x_scales[b][:, c0:c0 + n],
-                        start=(i == 0), stop=(i == 2),
+                        start=(k == 0), stop=(k == len(taps) - 1),
                     )
 
-        def take_middle(b, w):
-            nc.scalar.activation(out=window(b, w), in_=bank_of("mx%d%d1" % (b, w))[:], func=ACT.Identity, scale=-2.0)
-            give_back("mx%d%d1" % (b, w))
-
-        def add_side(b, w, j, s0=0, s1=16):
-            a3 = window(b, w).rearrange("p (s z) -> p s z", z=32)[:, s0:s1]
-            p3 = bank_of("mx%d%d%d" % (b, w, j))[:].rearrange("p (s z) -> p s z", z=32)[:, s0:s1]
-            if j == 0:
-                dst, src = a3[:, :, 1:32], p3[:, :, 0:31]
-            else:
-                dst, src = a3[:, :, 0:31], p3[:, :, 1:32]
-            nc.vector.scalar_tensor_tensor(out=dst, in0=src, scalar=-2.0, in1=dst, op0=ALU.mult, op1=ALU.add)
-            if s1 == 16:
-                give_back("mx%d%d%d" % (b, w, j))
-
-        def add_x2(b, w):
-            nc.vector.tensor_tensor(out=window(b, w), in0=bank_of("x2_%d%d" % (b, w))[:], in1=window(b, w), op=ALU.add)
-            give_back("x2_%d%d" % (b, w))
-
-        def finish(b, w, y0=0, y1=8):
+        def take_main(b, e):
             nc.scalar.activation(
-                out=res[b][:].rearrange("p (h w y z) -> p w y h z", h=2, w=2, y=8)[:, w, y0:y1],
-                in_=window(b, w).rearrange("p (y h z) -> p y h z", y=8, h=2)[:, y0:y1],
-                func=ACT.Relu, bias=w2[:, 0:1],
+                out=acc[b][:, 512 * e:512 * (e + 1)], in_=bank_of("mx%d%d0" % (b, e))[:], func=ACT.Identity, scale=-2.0
             )
+            give_back("mx%d%d0" % (b, e))
+
+        def add_shifted(b, e, r0=0, r1=8):
+            a3 = acc[b][:, 512 * e:512 * (e + 1)].rearrange("p (s m) -> p s m", m=16)[:, 4 * r0:4 * r1]
+            p3 = bank_of("mx%d%d1" % (b, e))[:].rearrange("p (s m) -> p s m", m=16)[:, 4 * r0:4 * r1]
+            dst, src = (a3[:, :, 0:15], p3[:, :, 1:16]) if e else (a3[:, :, 1:16], p3[:, :, 0:15])
+            nc.vector.scalar_tensor_tensor(out=dst, in0=src, scalar=-2.0, in1=dst, op0=ALU.mult, op1=ALU.add)
+            if r1 == 8:
+                give_back("mx%d%d1" % (b, e))
+
+        def half_planes(b, k):
+            return acc[b][:].rearrange("p (e r h m) -> p r h m e", e=2, r=8, h=4)[:, 4 * k:4 * k + 4]
+
+        def add_x2(b, k):
+            view = half_planes(b, k)
+            nc.vector.tensor_tensor(
+                out=view, in0=bank_of("x2_%d%d" % (b, k))[:].rearrange("p h (r m e) -> p r h m e", r=4, e=2), in1=view, op=ALU.add
+            )
+            give_back("x2_%d%d" % (b, k))
+
+        def finish(b, k, engine):
+            dst = res[b][:].rearrange("p (h r m e) -> p r h m e", h=4, r=8, e=2)[:, 4 * k:4 * k + 4]
+            if engine == "S":
+                nc.scalar.activation(out=dst, in_=half_planes(b, k), func=ACT.Relu, bias=w2[:, 0:1])
+            else:
+                eng = nc.gpsimd if engine == "G" else nc.vector
+                eng.tensor_scalar(out=dst, in0=half_planes(b, k), scalar1=w2[:, 0:1], scalar2=0.0, op0=ALU.add, op1=ALU.max)
             nc.sync.dma_start(
-                out=out[b].rearrange("o (h w y) z -> o h w y z", h=2, w=2)[:, :, w, y0:y1, :],
-                in_=res[b][:].rearrange("p (h w y z) -> p h w y z", h=2, w=2, y=8)[:, :, w, y0:y1, :],
+                out=out[b].rearrange("o (h r) z -> o h r z", h=4)[:, :, 4 * k:4 * k + 4, :],
+                in_=res[b][:].rearrange("p (h r z) -> p h r z", h=4, r=8)[:, :, 4 * k:4 * k + 4, :],
             )
 
-        warm_up()
-        for half in range(2):
-            for g in range(5):
-                pair_weights(half, g)
+        stats_on_tensor(0, range(4))
+        group_x(0, 0, 0)
+        group_x(0, 0, 1)
         for g in range(5):
-            transpose_weights(g)
-
-        stats_on_tensor(0)
+            take_bank("wT%d" % g, [P, 2, 4, P], BF16)
+        transpose_weights(0)
         square_flipped(0, 0)
-        square_flipped(0, 1)
-        group_x_first(0)
-        for i in range(3):
-            quantise_weights(i)
+        stats_on_tensor(0, range(4, 8))
+        group_x(0, 1, 0)
+        group_x(0, 1, 1)
         quantise_x(0, 0)
         quantise_x(0, 1)
-        group_x_rest(0, False)
-        quantise_x(0, 2)
-        stats_on_tensor(1)
-        square_flipped(1, 0)
-        group_x_first(1)
-        quantise_x(1, 0)
-        quantise_x(1, 1)
-
-        for j in (1, 0, 2):
-            mx_group(0, 0, j)
+        copy_halo(0, 0)
+        copy_halo(0, 1)
         square_weights(0)
-        take_middle(0, 0)
-        gram_diagonals(0)
-        add_side(0, 0, 0)
-        add_side(0, 0, 2)
-        group_x_rest(1, True)
-        quantise_x(1, 2)
-
-        for j in (1, 0, 2):
-            mx_group(0, 1, j)
-        take_middle(0, 1)
+        square_flipped(0, 1)
+        gram_diagonals(0, 0)
+        for t in range(1, 4):
+            transpose_weights(t)
+        stats_on_tensor(1, range(8))
+        copy_weights(0)
+        copy_weights(1)
+        quantise_weights(0)
+        copy_weights(2)
+        copy_weights(3)
+        copy_weights(4)
+        group_x(1, 0, 0)
+        group_x(1, 0, 1)
+        quantise_weights(1)
+        group_x(1, 1, 0)
+        group_x(1, 1, 1)
+        quantise_weights(2)
+        mx_group(0, 0, 0)
+        square_flipped(1, 0)
+        take_main(0, 0)
         square_flipped(1, 1)
         square_weights(1)
-        gram_diagonals(1)
+        mx_group(0, 1, 1)
+        mx_group(0, 0, 1)
+        mx_group(0, 1, 0)
+        take_main(0, 1)
+        quantise_x(1, 0)
+        quantise_x(1, 1)
+        copy_halo(1, 0)
+        copy_halo(1, 1)
+        gram_diagonals(1, 0)
         nc.vector.tensor_tensor(out=s_sum[:], in0=s_act[:], in1=s_dve[:], op=ALU.add)
-        add_side(0, 1, 0)
-        add_side(0, 1, 2)
-        square_weights(2)
-
-        mx_group(1, 0, 1)
-        mx_group(1, 0, 0)
+        add_shifted(0, 0)
+        add_shifted(0, 1)
         box_sum()
-        mx_group(1, 0, 2)
-        take_middle(1, 0)
+        mx_group(1, 0, 0)
         nc.scalar.copy(out=x2[:], in_=bank_of("box")[:])
         give_back("box")
+        square_weights(2)
+        take_main(1, 0)
         square_weights(3)
-        add_side(1, 0, 0)
-        add_side(1, 0, 2)
-        nc.vector.tensor_reduce(out=w2[:], in_=w2_parts[:], axis=AX.X, op=ALU.add)
-
-        mx_group(1, 1, 1)
-        take_middle(1, 1)
-        for b, w in ((0, 0), (0, 1), (1, 0), (1, 1)):
-            spread_x2(b, w)
-        for b, w in ((0, 0), (0, 1), (1, 0)):
-            add_x2(b, w)
-            finish(b, w)
-        add_x2(1, 1)
+        for k in range(2):
+            spread_x2(0, k)
         mx_group(1, 1, 0)
-        mx_group(1, 1, 2, pieces=2)
-        add_side(1, 1, 0)
-        add_side(1, 1, 2, 0, 8)
-        finish(1, 1, 0, 4)
-        add_side(1, 1, 2, 8, 16)
-        finish(1, 1, 4, 8)
+        take_main(1, 1)
+        for k in range(2):
+            spread_x2(1, k)
+        mx_group(1, 0, 1)
+        for k in range(2):
+            add_x2(0, k)
+        nc.vector.tensor_reduce(out=w2[:], in_=w2_parts[:], axis=AX.X, op=ALU.add)
+        finish(0, 0, "G")
+        finish(0, 1, "S")
+        for k in range(2):
+            add_x2(1, k)
+        mx_group(1, 1, 1, 2)
+        add_shifted(1, 0)
+        add_shifted(1, 1, 0, 4)
+        finish(1, 0, "S")
+        add_shifted(1, 1, 4, 8)
+        finish(1, 1, "V")

@@ -20,8 +20,8 @@ HW = 1024
 KD = 4608
 TAPS = 9
 TAP_ORDER = [3 * i + j for j in (1, 2, 0) for i in (1, 0, 2)]
-GRAM = ((0, 2, 4, 6), (0, 2, 4, 6))
-FLIP = ((1, 3, 5, 7), (1, 3, 5, 7))
+GRAM = ((0, 2, 4, 6), (0, 2, 4, 6, 1, 3))
+FLIP = ((1, 3, 5, 7), (5, 7))
 PLANE = 10 * 64
 W_PIECE = KD // 4
 W_QUANT = ((0, 2048), (2048, 2048), (4096, 512))
@@ -199,8 +199,7 @@ def tile_rbf_conv2d_kernel(tc, x, weight, out):
 
         def gram_diagonals(b, k):
             g = bank_of("gram%d%d" % (b, k))
-            for q in range(4):
-                ch = GRAM[b][4 * k + q]
+            for q, ch in enumerate(GRAM[b][4 * k:4 * k + 4]):
                 junk = scrap.tile([P, P], F32, name="junk_g")
                 nc.vector.scalar_tensor_tensor(
                     out=junk[:], in0=g[:, q, :], scalar=1.0, in1=ident[:],
@@ -227,16 +226,16 @@ def tile_rbf_conv2d_kernel(tc, x, weight, out):
                 return [(3 * i + 2 * e, 1 - e, i) for i in (1, 0, 2)]
             return [(3 * i + 1, e, i) for i in (1, 0, 2)] + [(3 * i + 2 - 2 * e, 1 - e, i) for i in (1, 0, 2)]
 
-        def mx_group(b, e, shifted, pieces=1):
-            ps = take_bank("mx%d%d%d" % (b, e, shifted), [P, 512], F32)
-            n = 512 // pieces
+        def mx_group(b, e, shifted, r0=0, r1=8):
+            ps = take_bank("mx%d%d%d%d" % (b, e, shifted, r0), [P, 512], F32)
             taps = mx_taps(b, e, shifted)
-            for lo in range(0, 512, n):
+            for lo in (64 * r0,):
+                n = 64 * (r1 - r0)
                 for k, (tap, plane, i) in enumerate(taps):
                     w0 = P * TAP_ORDER.index(tap)
                     c0 = PLANE * plane + 64 * i + lo
                     nc.tensor.matmul_mx(
-                        out=ps[:, lo:lo + n],
+                        out=ps[:, 0:n],
                         lhsT=w_codes[:, w0:w0 + P].bitcast(FP8X4),
                         lhsT_scale=w_scales[:, w0:w0 + P],
                         rhs=x_codes[b][:, c0:c0 + n].bitcast(FP8X4),
@@ -246,20 +245,37 @@ def tile_rbf_conv2d_kernel(tc, x, weight, out):
 
         def take_main(b, e):
             nc.scalar.activation(
-                out=acc[b][:, 512 * e:512 * (e + 1)], in_=bank_of("mx%d%d0" % (b, e))[:], func=ACT.Identity, scale=-2.0
+                out=acc[b][:, 512 * e:512 * (e + 1)], in_=bank_of("mx%d%d00" % (b, e))[:], func=ACT.Identity, scale=-2.0
             )
-            give_back("mx%d%d0" % (b, e))
+            give_back("mx%d%d00" % (b, e))
+
+        def copy_x2(b, k):
+            nc.scalar.copy(
+                out=half_planes(b, k), in_=bank_of("x2_%d%d" % (b, k))[:].rearrange("p h (r m e) -> p r h m e", r=4, e=2)
+            )
+            give_back("x2_%d%d" % (b, k))
+
+        def add_main(b, e, r0=0, r1=8):
+            key = "mx%d%d0%d" % (b, e, r0)
+            a = acc[b][:, 512 * e + 64 * r0:512 * e + 64 * r1]
+            nc.vector.scalar_tensor_tensor(
+                out=a, in0=bank_of(key)[:, 0:64 * (r1 - r0)], scalar=-2.0, in1=a, op0=ALU.mult, op1=ALU.add
+            )
+            give_back(key)
 
         def add_shifted(b, e, r0=0, r1=8):
-            a3 = acc[b][:, 512 * e:512 * (e + 1)].rearrange("p (s m) -> p s m", m=16)[:, 4 * r0:4 * r1]
-            p3 = bank_of("mx%d%d1" % (b, e))[:].rearrange("p (s m) -> p s m", m=16)[:, 4 * r0:4 * r1]
+            key = "mx%d%d1%d" % (b, e, r0)
+            a3 = acc[b][:, 512 * e + 64 * r0:512 * e + 64 * r1].rearrange("p (s m) -> p s m", m=16)
+            p3 = bank_of(key)[:, 0:64 * (r1 - r0)].rearrange("p (s m) -> p s m", m=16)
             dst, src = (a3[:, :, 0:15], p3[:, :, 1:16]) if e else (a3[:, :, 1:16], p3[:, :, 0:15])
             nc.vector.scalar_tensor_tensor(out=dst, in0=src, scalar=-2.0, in1=dst, op0=ALU.mult, op1=ALU.add)
-            if r1 == 8:
-                give_back("mx%d%d1" % (b, e))
+            give_back(key)
 
         def half_planes(b, k):
-            return acc[b][:].rearrange("p (e r h m) -> p r h m e", e=2, r=8, h=4)[:, 4 * k:4 * k + 4]
+            return planes_rows(b, 4 * k, 4 * k + 4)
+
+        def planes_rows(b, r0, r1):
+            return acc[b][:].rearrange("p (e r h m) -> p r h m e", e=2, r=8, h=4)[:, r0:r1]
 
         def add_x2(b, k):
             view = half_planes(b, k)
@@ -268,16 +284,16 @@ def tile_rbf_conv2d_kernel(tc, x, weight, out):
             )
             give_back("x2_%d%d" % (b, k))
 
-        def finish(b, k, engine):
-            dst = res[b][:].rearrange("p (h r m e) -> p r h m e", h=4, r=8, e=2)[:, 4 * k:4 * k + 4]
+        def finish(b, r0, r1, engine):
+            dst = res[b][:].rearrange("p (h r m e) -> p r h m e", h=4, r=8, e=2)[:, r0:r1]
             if engine == "S":
-                nc.scalar.activation(out=dst, in_=half_planes(b, k), func=ACT.Relu, bias=w2[:, 0:1])
+                nc.scalar.activation(out=dst, in_=planes_rows(b, r0, r1), func=ACT.Relu, bias=w2[:, 0:1])
             else:
                 eng = nc.gpsimd if engine == "G" else nc.vector
-                eng.tensor_scalar(out=dst, in0=half_planes(b, k), scalar1=w2[:, 0:1], scalar2=0.0, op0=ALU.add, op1=ALU.max)
+                eng.tensor_scalar(out=dst, in0=planes_rows(b, r0, r1), scalar1=w2[:, 0:1], scalar2=0.0, op0=ALU.add, op1=ALU.max)
             nc.sync.dma_start(
-                out=out[b].rearrange("o (h r) z -> o h r z", h=4)[:, :, 4 * k:4 * k + 4, :],
-                in_=res[b][:].rearrange("p (h r z) -> p h r z", h=4, r=8)[:, :, 4 * k:4 * k + 4, :],
+                out=out[b].rearrange("o (h r) z -> o h r z", h=4)[:, :, r0:r1, :],
+                in_=res[b][:].rearrange("p (h r z) -> p h r z", h=4, r=8)[:, :, r0:r1, :],
             )
 
         stats_on_tensor(0, range(4))
@@ -315,7 +331,7 @@ def tile_rbf_conv2d_kernel(tc, x, weight, out):
         mx_group(0, 0, 0)
         square_flipped(1, 0)
         take_main(0, 0)
-        square_flipped(1, 1)
+        square_weights(2)
         square_weights(1)
         mx_group(0, 1, 1)
         mx_group(0, 0, 1)
@@ -326,33 +342,40 @@ def tile_rbf_conv2d_kernel(tc, x, weight, out):
         copy_halo(1, 0)
         copy_halo(1, 1)
         gram_diagonals(1, 0)
+        gram_diagonals(1, 1)
         nc.vector.tensor_tensor(out=s_sum[:], in0=s_act[:], in1=s_dve[:], op=ALU.add)
         add_shifted(0, 0)
         add_shifted(0, 1)
+        mx_group(1, 0, 0, 0, 4)
         box_sum()
-        mx_group(1, 0, 0)
         nc.scalar.copy(out=x2[:], in_=bank_of("box")[:])
         give_back("box")
-        square_weights(2)
-        take_main(1, 0)
         square_weights(3)
-        for k in range(2):
-            spread_x2(0, k)
-        mx_group(1, 1, 0)
-        take_main(1, 1)
-        for k in range(2):
-            spread_x2(1, k)
-        mx_group(1, 0, 1)
+        mx_group(1, 0, 1, 0, 4)
+        for b in (0, 1):
+            for k in range(2):
+                spread_x2(b, k)
+        copy_x2(1, 0)
+        copy_x2(1, 1)
         for k in range(2):
             add_x2(0, k)
+        mx_group(1, 1, 0, 0, 4)
+        mx_group(1, 1, 1, 0, 4)
         nc.vector.tensor_reduce(out=w2[:], in_=w2_parts[:], axis=AX.X, op=ALU.add)
-        finish(0, 0, "G")
-        finish(0, 1, "S")
-        for k in range(2):
-            add_x2(1, k)
-        mx_group(1, 1, 1, 2)
-        add_shifted(1, 0)
+        add_main(1, 0, 0, 4)
+        add_shifted(1, 0, 0, 4)
+        finish(0, 0, 4, "G")
+        finish(0, 4, 8, "S")
+        add_main(1, 1, 0, 4)
+        mx_group(1, 0, 0, 4, 8)
+        mx_group(1, 1, 0, 4, 8)
         add_shifted(1, 1, 0, 4)
-        finish(1, 0, "S")
+        finish(1, 0, 4, "S")
+        add_main(1, 0, 4, 8)
+        mx_group(1, 0, 1, 4, 8)
+        add_main(1, 1, 4, 8)
+        mx_group(1, 1, 1, 4, 8)
+        add_shifted(1, 0, 4, 8)
         add_shifted(1, 1, 4, 8)
-        finish(1, 1, "V")
+        finish(1, 4, 6, "V")
+        finish(1, 6, 8, "S")

@@ -7,6 +7,7 @@ FLOPS = 2 * 2048 * 128 * 4608
 
 F32 = mybir.dt.float32
 BF16 = mybir.dt.bfloat16
+I32 = mybir.dt.int32
 U32 = mybir.dt.uint32
 U8 = mybir.dt.uint8
 FP8X4 = mybir.dt.float8_e4m3fn_x4
@@ -20,8 +21,9 @@ HW = 1024
 KD = 4608
 TAPS = 9
 TAP_ORDER = [3 * i + j for j in (1, 2, 0) for i in (1, 0, 2)]
-GRAM = ((0, 2, 4, 6), (0, 2, 4, 6, 1, 3))
-FLIP = ((1, 3, 5, 7), (5, 7))
+ON_VECTOR = (1,)
+GRAM = ((0, 1, 2, 3, 4, 5, 6, 7), (0, 2, 4, 6))
+FLIP = ((), (1, 3, 5, 7))
 PLANE = 10 * 64
 W_PIECE = KD // 4
 W_QUANT = ((0, 2048), (2048, 2048), (4096, 512))
@@ -114,6 +116,12 @@ def tile_rbf_conv2d_kernel(tc, x, weight, out):
         def give_back(key):
             free_banks.append(held[key][1])
 
+        def warm_up(n):
+            junk = take_bank("warm", [P, P], F32)
+            for i in range(n):
+                nc.tensor.matmul(junk[:], lhsT=ident[:], rhs=ident[:], start=True, stop=True)
+            give_back("warm")
+
         def square_weights(i):
             junk = scrap.tile([P, W_PIECE], BF16, name="junk_w")
             nc.scalar.activation(
@@ -127,7 +135,7 @@ def tile_rbf_conv2d_kernel(tc, x, weight, out):
 
         def copy_weights(g):
             n = min(2, TAPS - 2 * g)
-            copy = nc.vector.tensor_copy if g == 1 else nc.scalar.copy
+            copy = nc.vector.tensor_copy if g in ON_VECTOR else nc.scalar.copy
             copy(
                 out=w_grp_view[:, 2 * g:2 * g + n],
                 in_=bank_of("wT%d" % g)[:, 0:n].rearrange("p a t o -> p a o t"),
@@ -143,12 +151,17 @@ def tile_rbf_conv2d_kernel(tc, x, weight, out):
             )
 
         def group_x(b, half, e, on_scalar=False):
-            copy = nc.scalar.copy if on_scalar else nc.vector.tensor_copy
-            hs = slice(2 * half, 2 * half + 2)
-            copy(
-                out=grp[b][:].rearrange("p (e r h m t) -> p e r h m t", e=2, r=8, h=4, t=4)[:, e, :, hs],
-                in_=raw[b][:].rearrange("p t (h r m e) -> p e r h m t", h=4, r=8, e=2)[:, e, :, hs],
-            )
+            dst = grp[b][:].rearrange("p (e r h m t) -> p e h r m t", e=2, r=8, h=4, t=4)[:, e]
+            src = raw[b][:].rearrange("p t (h r m e) -> p e h r m t", h=4, r=8, e=2)[:, e]
+            hs = range(2 * half, 2 * half + 2)
+            if on_scalar:
+                for h in hs:
+                    nc.scalar.copy(out=dst[:, h], in_=src[:, h])
+            else:
+                nc.vector.tensor_copy(
+                    out=dst[:, hs.start:hs.stop].rearrange("p h r m t -> p r h m t"),
+                    in_=src[:, hs.start:hs.stop].rearrange("p h r m t -> p r h m t"),
+                )
 
         def quantise_x(b, e):
             c0 = PLANE * e + 64
@@ -158,11 +171,11 @@ def tile_rbf_conv2d_kernel(tc, x, weight, out):
                 in_=grp[b][:, 2048 * e:2048 * (e + 1)],
             )
 
-        def copy_halo(b, e):
-            for tile in (x_codes[b], x_scales[b]):
-                rows = tile[:, PLANE * e:PLANE * (e + 1)].rearrange("p (r n) -> p r n", r=10)
-                nc.gpsimd.tensor_copy(out=rows[:, 0, 16:64], in_=rows[:, 8, 0:48])
-                nc.gpsimd.tensor_copy(out=rows[:, 9, 0:48], in_=rows[:, 1, 16:64])
+        def copy_halo(b):
+            for tile in (x_codes[b][:].bitcast(I32), x_scales[b][:]):
+                rows = tile.rearrange("p (e r n) -> p e r n", e=2, r=10)
+                nc.vector.tensor_copy(out=rows[:, :, 0, 16:64], in_=rows[:, :, 8, 0:48])
+                nc.vector.tensor_copy(out=rows[:, :, 9, 0:48], in_=rows[:, :, 1, 16:64])
 
         def gram(b, ch):
             k, q = divmod(GRAM[b].index(ch), 4)
@@ -296,57 +309,59 @@ def tile_rbf_conv2d_kernel(tc, x, weight, out):
                 in_=res[b][:].rearrange("p (h r z) -> p h r z", h=4, r=8)[:, :, r0:r1, :],
             )
 
-        stats_on_tensor(0, range(4))
+        warm_up(4)
+        gram(0, 0)
+        gram(0, 1)
         group_x(0, 0, 0)
-        group_x(0, 0, 1)
+        group_x(0, 0, 1, True)
+        gram(0, 4)
+        gram(0, 5)
+        group_x(0, 1, 0)
+        group_x(0, 1, 1, True)
         for g in range(5):
             take_bank("wT%d" % g, [P, 2, 4, P], BF16)
-        transpose_weights(0)
-        square_flipped(0, 0)
-        stats_on_tensor(0, range(4, 8))
-        group_x(0, 1, 0)
-        group_x(0, 1, 1)
+        for t, ch in enumerate((2, 3, 6, 7)):
+            transpose_weights(t)
+            gram(0, ch)
+        square_weights(0)
         quantise_x(0, 0)
         quantise_x(0, 1)
-        copy_halo(0, 0)
-        copy_halo(0, 1)
-        square_weights(0)
-        square_flipped(0, 1)
+        square_weights(1)
         gram_diagonals(0, 0)
-        for t in range(1, 4):
-            transpose_weights(t)
-        stats_on_tensor(1, range(8))
+        copy_halo(0)
         copy_weights(0)
         copy_weights(1)
         quantise_weights(0)
         copy_weights(2)
         copy_weights(3)
         copy_weights(4)
+        stats_on_tensor(1, range(4))
         group_x(1, 0, 0)
         group_x(1, 0, 1)
+        stats_on_tensor(1, range(4, 8))
         quantise_weights(1)
         group_x(1, 1, 0)
-        group_x(1, 1, 1)
         quantise_weights(2)
+        group_x(1, 1, 1)
         mx_group(0, 0, 0)
         square_flipped(1, 0)
         take_main(0, 0)
+        square_flipped(1, 1)
         square_weights(2)
-        square_weights(1)
         mx_group(0, 1, 1)
         mx_group(0, 0, 1)
         mx_group(0, 1, 0)
         take_main(0, 1)
         quantise_x(1, 0)
         quantise_x(1, 1)
-        copy_halo(1, 0)
-        copy_halo(1, 1)
+        gram_diagonals(0, 1)
+        copy_halo(1)
         gram_diagonals(1, 0)
-        gram_diagonals(1, 1)
         nc.vector.tensor_tensor(out=s_sum[:], in0=s_act[:], in1=s_dve[:], op=ALU.add)
         add_shifted(0, 0)
         add_shifted(0, 1)
         mx_group(1, 0, 0, 0, 4)
+        mx_group(1, 1, 0, 0, 4)
         box_sum()
         nc.scalar.copy(out=x2[:], in_=bank_of("box")[:])
         give_back("box")
@@ -359,7 +374,6 @@ def tile_rbf_conv2d_kernel(tc, x, weight, out):
         copy_x2(1, 1)
         for k in range(2):
             add_x2(0, k)
-        mx_group(1, 1, 0, 0, 4)
         mx_group(1, 1, 1, 0, 4)
         nc.vector.tensor_reduce(out=w2[:], in_=w2_parts[:], axis=AX.X, op=ALU.add)
         add_main(1, 0, 0, 4)

@@ -26,7 +26,7 @@ GRAM = ((0, 1, 2, 3, 4, 5, 6, 7), (0, 2, 4, 6))
 FLIP = ((), (1, 3, 5, 7))
 PLANE = 10 * 64
 W_PIECE = KD // 4
-W_QUANT = ((0, 2048), (2048, 2048), (4096, 512))
+W_QUANT = ((0, 2048), (2048, 1024), (3072, 1024), (4096, 512))
 
 
 def tile_rbf_conv2d_kernel(tc, x, weight, out):
@@ -38,24 +38,24 @@ def tile_rbf_conv2d_kernel(tc, x, weight, out):
         ctx.enter_context(tc.manual_schedule())
 
         w_raw = keep.tile([P, KD], BF16, name="w_raw")
-        raw = [keep.tile([P, 4, HW], BF16, name="raw%d" % b) for b in range(B)]
+        raw = [[keep.tile([P, 4, 512], BF16, name="raw%d%d" % (b, k)) for k in range(2)] for b in range(B)]
 
-        def load_x(b, y0, y1):
+        def load_x(b, k):
             nc.sync.dma_start(
-                out=raw[b][:, :, 32 * y0:32 * y1],
-                in_=x[b].rearrange("(t p) h w -> p t (h w)", t=4)[:, :, 32 * y0:32 * y1],
+                out=raw[b][k][:],
+                in_=x[b].rearrange("(t p) h w -> p t (h w)", t=4)[:, :, 512 * k:512 * k + 512],
             )
 
         def load_w(i):
             cols = slice(W_PIECE * i, W_PIECE * (i + 1))
             nc.sync.dma_start(out=w_raw[:, cols], in_=weight[:, cols])
 
-        load_x(0, 0, 16)
-        load_x(0, 16, 32)
+        load_x(0, 0)
+        load_x(0, 1)
         for i in range(4):
             load_w(i)
-        load_x(1, 0, 16)
-        load_x(1, 16, 32)
+        load_x(1, 0)
+        load_x(1, 1)
 
         ident = keep.tile([P, P], F32, name="ident")
         make_identity(nc, ident[:])
@@ -69,7 +69,7 @@ def tile_rbf_conv2d_kernel(tc, x, weight, out):
         x_codes = []
         x_scales = []
         for b in range(B):
-            grp.append(keep.tile([P, HW * 4], BF16, name="grp%d" % b, align_bytes=64))
+            grp.append([keep.tile([P, HW * 2], BF16, name="grp%d%d" % (b, e), align_bytes=64) for e in range(2)])
             x_codes.append(keep.tile([P, 2 * PLANE], U32, name="x_codes%d" % b, align_bytes=64))
             x_scales.append(keep.tile([P, 2 * PLANE], U8, name="x_scales%d" % b, align_bytes=64))
             nc.gpsimd.memset(x_scales[b][:].bitcast(U32), 0)
@@ -99,8 +99,7 @@ def tile_rbf_conv2d_kernel(tc, x, weight, out):
         w_grp_view = w_grp[:].rearrange("p (a o t) -> p a o t", o=P, t=4)
         w_codes = keep.tile([P, TAPS * P], U32, name="w_codes", align_bytes=64)
         w_scales = keep.tile([P, TAPS * P], U8, name="w_scales", align_bytes=64)
-        acc = [keep.tile([P, HW], F32, name="acc%d" % b) for b in range(B)]
-        res = [keep.tile([P, HW], F32, name="res%d" % b) for b in range(B)]
+        acc = [[keep.tile([P, 2, 256], F32, name="acc%d%d" % (b, k)) for k in range(2)] for b in range(B)]
 
         free_banks = list(range(8))
         held = {}
@@ -151,16 +150,15 @@ def tile_rbf_conv2d_kernel(tc, x, weight, out):
             )
 
         def group_x(b, half, e, on_scalar=False):
-            dst = grp[b][:].rearrange("p (e r h m t) -> p e h r m t", e=2, r=8, h=4, t=4)[:, e]
-            src = raw[b][:].rearrange("p t (h r m e) -> p e h r m t", h=4, r=8, e=2)[:, e]
-            hs = range(2 * half, 2 * half + 2)
+            dst = grp[b][e][:].rearrange("p (r h m t) -> p h r m t", r=8, h=4, t=4)
+            src = raw[b][half][:].rearrange("p t (h r m e) -> p e h r m t", h=2, r=8, e=2)[:, e]
             if on_scalar:
-                for h in hs:
-                    nc.scalar.copy(out=dst[:, h], in_=src[:, h])
+                for h in range(2):
+                    nc.scalar.copy(out=dst[:, 2 * half + h], in_=src[:, h])
             else:
                 nc.vector.tensor_copy(
-                    out=dst[:, hs.start:hs.stop].rearrange("p h r m t -> p r h m t"),
-                    in_=src[:, hs.start:hs.stop].rearrange("p h r m t -> p r h m t"),
+                    out=dst[:, 2 * half:2 * half + 2].rearrange("p h r m t -> p r h m t"),
+                    in_=src.rearrange("p h r m t -> p r h m t"),
                 )
 
         def quantise_x(b, e):
@@ -168,7 +166,7 @@ def tile_rbf_conv2d_kernel(tc, x, weight, out):
             nc.vector.quantize_mx(
                 out=x_codes[b][:, c0:c0 + 512].bitcast(FP8X4),
                 scales=x_scales[b][:, c0:c0 + 512],
-                in_=grp[b][:, 2048 * e:2048 * (e + 1)],
+                in_=grp[b][e][:],
             )
 
         def copy_halo(b):
@@ -181,7 +179,7 @@ def tile_rbf_conv2d_kernel(tc, x, weight, out):
             k, q = divmod(GRAM[b].index(ch), 4)
             if q == 0:
                 take_bank("gram%d%d" % (b, k), [P, 4, P], F32)
-            blocks = [raw[b][:, j, ch * P:(ch + 1) * P] for j in range(4)]
+            blocks = [raw[b][ch // 4][:, j, ch % 4 * P:(ch % 4 + 1) * P] for j in range(4)]
             for j in range(4):
                 nc.tensor.matmul(bank_of("gram%d%d" % (b, k))[:, q, :], lhsT=blocks[j], rhs=blocks[j], start=(j == 0), stop=(j == 3))
 
@@ -190,7 +188,7 @@ def tile_rbf_conv2d_kernel(tc, x, weight, out):
             if n == 0:
                 take_bank("flip%d%d" % (b, k), [P, 8, P], BF16)
             for j in range(4):
-                nc.tensor.transpose(bank_of("flip%d%d" % (b, k))[:, 4 * n + j, :], raw[b][:, j, ch * P:(ch + 1) * P], ident_bf[:])
+                nc.tensor.transpose(bank_of("flip%d%d" % (b, k))[:, 4 * n + j, :], raw[b][ch // 4][:, j, ch % 4 * P:(ch % 4 + 1) * P], ident_bf[:])
 
         def stats_on_tensor(b, chunks):
             for ch in chunks:
@@ -256,11 +254,14 @@ def tile_rbf_conv2d_kernel(tc, x, weight, out):
                         start=(k == 0), stop=(k == len(taps) - 1),
                     )
 
-        def take_main(b, e):
-            nc.scalar.activation(
-                out=acc[b][:, 512 * e:512 * (e + 1)], in_=bank_of("mx%d%d00" % (b, e))[:], func=ACT.Identity, scale=-2.0
-            )
-            give_back("mx%d%d00" % (b, e))
+        def take_main(b, e, r0=0, r1=8):
+            key = "mx%d%d0%d" % (b, e, r0)
+            for k in range(r0 // 4, r1 // 4):
+                lo = 256 * k - 64 * r0
+                nc.scalar.activation(
+                    out=acc[b][k][:, e, :], in_=bank_of(key)[:, lo:lo + 256], func=ACT.Identity, scale=-2.0
+                )
+            give_back(key)
 
         def copy_x2(b, k):
             nc.scalar.copy(
@@ -270,7 +271,7 @@ def tile_rbf_conv2d_kernel(tc, x, weight, out):
 
         def add_main(b, e, r0=0, r1=8):
             key = "mx%d%d0%d" % (b, e, r0)
-            a = acc[b][:, 512 * e + 64 * r0:512 * e + 64 * r1]
+            a = acc[b][r0 // 4][:, e, :]
             nc.vector.scalar_tensor_tensor(
                 out=a, in0=bank_of(key)[:, 0:64 * (r1 - r0)], scalar=-2.0, in1=a, op0=ALU.mult, op1=ALU.add
             )
@@ -278,17 +279,16 @@ def tile_rbf_conv2d_kernel(tc, x, weight, out):
 
         def add_shifted(b, e, r0=0, r1=8):
             key = "mx%d%d1%d" % (b, e, r0)
-            a3 = acc[b][:, 512 * e + 64 * r0:512 * e + 64 * r1].rearrange("p (s m) -> p s m", m=16)
-            p3 = bank_of(key)[:, 0:64 * (r1 - r0)].rearrange("p (s m) -> p s m", m=16)
-            dst, src = (a3[:, :, 0:15], p3[:, :, 1:16]) if e else (a3[:, :, 1:16], p3[:, :, 0:15])
-            nc.vector.scalar_tensor_tensor(out=dst, in0=src, scalar=-2.0, in1=dst, op0=ALU.mult, op1=ALU.add)
+            for k in range(r0 // 4, r1 // 4):
+                lo = 256 * k - 64 * r0
+                a3 = acc[b][k][:, e, :].rearrange("p (s m) -> p s m", m=16)
+                p3 = bank_of(key)[:, lo:lo + 256].rearrange("p (s m) -> p s m", m=16)
+                dst, src = (a3[:, :, 0:15], p3[:, :, 1:16]) if e else (a3[:, :, 1:16], p3[:, :, 0:15])
+                nc.vector.scalar_tensor_tensor(out=dst, in0=src, scalar=-2.0, in1=dst, op0=ALU.mult, op1=ALU.add)
             give_back(key)
 
         def half_planes(b, k):
-            return planes_rows(b, 4 * k, 4 * k + 4)
-
-        def planes_rows(b, r0, r1):
-            return acc[b][:].rearrange("p (e r h m) -> p r h m e", e=2, r=8, h=4)[:, r0:r1]
+            return acc[b][k][:].rearrange("p e (r h m) -> p r h m e", r=4, h=4)
 
         def add_x2(b, k):
             view = half_planes(b, k)
@@ -298,16 +298,16 @@ def tile_rbf_conv2d_kernel(tc, x, weight, out):
             give_back("x2_%d%d" % (b, k))
 
         def finish(b, r0, r1, engine):
-            dst = res[b][:].rearrange("p (h r m e) -> p r h m e", h=4, r=8, e=2)[:, r0:r1]
+            k, n = r0 // 4, r1 - r0
+            src = half_planes(b, k)[:, r0 - 4 * k:r1 - 4 * k]
+            res = keep.tile([P, 4, n, 32], F32, name="res%d%d" % (b, r0))
+            dst = res[:].rearrange("p h r (m e) -> p r h m e", e=2)
             if engine == "S":
-                nc.scalar.activation(out=dst, in_=planes_rows(b, r0, r1), func=ACT.Relu, bias=w2[:, 0:1])
+                nc.scalar.activation(out=dst, in_=src, func=ACT.Relu, bias=w2[:, 0:1])
             else:
                 eng = nc.gpsimd if engine == "G" else nc.vector
-                eng.tensor_scalar(out=dst, in0=planes_rows(b, r0, r1), scalar1=w2[:, 0:1], scalar2=0.0, op0=ALU.add, op1=ALU.max)
-            nc.sync.dma_start(
-                out=out[b].rearrange("o (h r) z -> o h r z", h=4)[:, :, r0:r1, :],
-                in_=res[b][:].rearrange("p (h r z) -> p h r z", h=4, r=8)[:, :, r0:r1, :],
-            )
+                eng.tensor_scalar(out=dst, in0=src, scalar1=w2[:, 0:1], scalar2=0.0, op0=ALU.add, op1=ALU.max)
+            nc.sync.dma_start(out=out[b].rearrange("o (h r) z -> o h r z", h=4)[:, :, r0:r1, :], in_=res[:])
 
         warm_up(4)
         gram(0, 0)
@@ -317,7 +317,7 @@ def tile_rbf_conv2d_kernel(tc, x, weight, out):
         gram(0, 4)
         gram(0, 5)
         group_x(0, 1, 0)
-        group_x(0, 1, 1, True)
+        group_x(0, 1, 1)
         for g in range(5):
             take_bank("wT%d" % g, [P, 2, 4, P], BF16)
         for t, ch in enumerate((2, 3, 6, 7)):
@@ -337,11 +337,12 @@ def tile_rbf_conv2d_kernel(tc, x, weight, out):
         copy_weights(4)
         stats_on_tensor(1, range(4))
         group_x(1, 0, 0)
+        quantise_weights(1)
         group_x(1, 0, 1)
         stats_on_tensor(1, range(4, 8))
-        quantise_weights(1)
-        group_x(1, 1, 0)
         quantise_weights(2)
+        group_x(1, 1, 0)
+        quantise_weights(3)
         group_x(1, 1, 1)
         mx_group(0, 0, 0)
         square_flipped(1, 0)
@@ -354,37 +355,36 @@ def tile_rbf_conv2d_kernel(tc, x, weight, out):
         take_main(0, 1)
         quantise_x(1, 0)
         quantise_x(1, 1)
-        gram_diagonals(0, 1)
         copy_halo(1)
+        gram_diagonals(0, 1)
         gram_diagonals(1, 0)
         nc.vector.tensor_tensor(out=s_sum[:], in0=s_act[:], in1=s_dve[:], op=ALU.add)
         add_shifted(0, 0)
         add_shifted(0, 1)
         mx_group(1, 0, 0, 0, 4)
+        take_main(1, 0, 0, 4)
         mx_group(1, 1, 0, 0, 4)
+        take_main(1, 1, 0, 4)
+        mx_group(1, 0, 1, 0, 4)
+        mx_group(1, 1, 1, 0, 4)
         box_sum()
         nc.scalar.copy(out=x2[:], in_=bank_of("box")[:])
         give_back("box")
         square_weights(3)
-        mx_group(1, 0, 1, 0, 4)
-        for b in (0, 1):
-            for k in range(2):
-                spread_x2(b, k)
-        copy_x2(1, 0)
-        copy_x2(1, 1)
+        add_shifted(1, 0, 0, 4)
+        add_shifted(1, 1, 0, 4)
+        mx_group(1, 0, 0, 4, 8)
+        for b, k in ((0, 0), (0, 1), (1, 1), (1, 0)):
+            spread_x2(b, k)
+        nc.vector.tensor_reduce(out=w2[:], in_=w2_parts[:], axis=AX.X, op=ALU.add)
         for k in range(2):
             add_x2(0, k)
-        mx_group(1, 1, 1, 0, 4)
-        nc.vector.tensor_reduce(out=w2[:], in_=w2_parts[:], axis=AX.X, op=ALU.add)
-        add_main(1, 0, 0, 4)
-        add_shifted(1, 0, 0, 4)
-        finish(0, 0, 4, "G")
+        copy_x2(1, 1)
+        finish(0, 0, 4, "S")
         finish(0, 4, 8, "S")
-        add_main(1, 1, 0, 4)
-        mx_group(1, 0, 0, 4, 8)
-        mx_group(1, 1, 0, 4, 8)
-        add_shifted(1, 1, 0, 4)
+        add_x2(1, 0)
         finish(1, 0, 4, "S")
+        mx_group(1, 1, 0, 4, 8)
         add_main(1, 0, 4, 8)
         mx_group(1, 0, 1, 4, 8)
         add_main(1, 1, 4, 8)

@@ -20,13 +20,15 @@ B = 2
 HW = 1024
 KD = 4608
 TAPS = 9
-TAP_ORDER = [3 * i + j for j in (1, 2, 0) for i in (1, 0, 2)]
+TAP_ORDER = [3 * i + j for i in (1, 0, 2) for j in (1, 2)] + [3, 0, 6]
+TAP_GROUPS = (slice(4, 6), slice(1, 3), slice(7, 9), slice(0, 9, 3))
+GROUP_OF_SLOT = ((0, 0), (0, 1), (1, 0), (1, 1), (2, 0), (2, 1), (3, 1), (3, 0), (3, 2))
 ON_VECTOR = (1,)
 GRAM = ((0, 1, 2, 3, 4, 5, 6, 7), (0, 2, 4, 6))
 FLIP = ((), (1, 3, 5, 7))
 PLANE = 10 * 64
 W_PIECE = KD // 4
-W_QUANT = ((0, 2048), (2048, 1024), (3072, 1024), (4096, 512))
+W_QUANT = ((0, 1024), (1024, 1024), (2048, 1024), (3072, 1024), (4096, 512))
 
 
 def tile_rbf_conv2d_kernel(tc, x, weight, out):
@@ -41,19 +43,20 @@ def tile_rbf_conv2d_kernel(tc, x, weight, out):
         raw = [[keep.tile([P, 4, 512], BF16, name="raw%d%d" % (b, k)) for k in range(2)] for b in range(B)]
 
         def load_x(b, k):
-            nc.sync.dma_start(
-                out=raw[b][k][:],
-                in_=x[b].rearrange("(t p) h w -> p t (h w)", t=4)[:, :, 512 * k:512 * k + 512],
-            )
+            for u in range(2):
+                nc.sync.dma_start(
+                    out=raw[b][k][:, 2 * u:2 * u + 2, :],
+                    in_=x[b].rearrange("(u p e) h w -> u p e (h w)", u=2, e=2)[u, :, :, 512 * k:512 * k + 512],
+                )
 
-        def load_w(i):
-            cols = slice(W_PIECE * i, W_PIECE * (i + 1))
+        def load_w(u):
+            cols = slice(KD // 2 * u, KD // 2 * (u + 1))
             nc.sync.dma_start(out=w_raw[:, cols], in_=weight[:, cols])
 
         load_x(0, 0)
         load_x(0, 1)
-        for i in range(4):
-            load_w(i)
+        load_w(0)
+        load_w(1)
         load_x(1, 0)
         load_x(1, 1)
 
@@ -94,9 +97,15 @@ def tile_rbf_conv2d_kernel(tc, x, weight, out):
         x2 = keep.tile([P, B, 8], F32, name="x2")
         w2_parts = keep.tile([P, 4], F32, name="w2_parts")
         w2 = keep.tile([P, 1], F32, name="w2")
-        w_by_tap = w_raw[:].rearrange("o (t c a) -> o t a c", t=4, a=TAPS)
+        w_by_parity = w_raw[:].rearrange("o (u p e a) -> o u e a p", u=2, e=2, a=TAPS)
+        w_by_tap = w_raw[:].rearrange("o (u c a) -> o u a c", u=2, a=TAPS)
+        w_pairs = {}
+        for u in range(2):
+            for g in range(4):
+                w_pairs[u, g] = keep.tile([P, 2 + g // 3, 256], BF16, name="w_pairs%d%d" % (u, g))
         w_grp = keep.tile([P, KD], BF16, name="w_grp", align_bytes=64)
         w_grp_view = w_grp[:].rearrange("p (a o t) -> p a o t", o=P, t=4)
+        w_grp_words = w_grp[:].bitcast(F32).rearrange("p (a o u) -> p a o u", o=P, u=2)
         w_codes = keep.tile([P, TAPS * P], U32, name="w_codes", align_bytes=64)
         w_scales = keep.tile([P, TAPS * P], U8, name="w_scales", align_bytes=64)
         acc = [[keep.tile([P, 2, 256], F32, name="acc%d%d" % (b, k)) for k in range(2)] for b in range(B)]
@@ -128,16 +137,38 @@ def tile_rbf_conv2d_kernel(tc, x, weight, out):
                 accum_out=w2_parts[:, i:i + 1],
             )
 
-        def transpose_weights(t):
-            for k, tap in enumerate(TAP_ORDER):
-                nc.tensor.transpose(bank_of("wT%d" % (k // 2))[:, k % 2, t, :], w_by_tap[:, t, tap, :], ident_bf[:])
+        def pair_weights(u, g, on_scalar=False):
+            dst = w_pairs[u, g][:].rearrange("o a c -> o c a")
+            src = w_by_tap[:, u, TAP_GROUPS[g], :].rearrange("o a c -> o c a")
+            if on_scalar:
+                nc.scalar.copy(out=dst, in_=src)
+            else:
+                nc.vector.tensor_copy(out=dst, in_=src)
 
-        def copy_weights(g):
+        def transpose_words(u, s0, s1):
+            for s in range(s0, s1):
+                g, n = GROUP_OF_SLOT[s]
+                words = w_pairs[u, g][:].rearrange("o a c -> o (a c)").bitcast(F32)
+                nc.tensor.transpose(bank_of("wT%d" % (s // 2))[:, s % 2, u, :], words[:, P * n:P * n + P], ident[:])
+
+        def transpose_direct(u, s0, s1):
+            for s in range(s0, s1):
+                for e in range(2):
+                    nc.tensor.transpose(
+                        bank_of("wT%d" % (s // 2))[:, s % 2, 2 * u + e, :], w_by_parity[:, u, e, TAP_ORDER[s], :], ident_bf[:]
+                    )
+
+        def copy_direct(g, on_scalar=True):
+            copy = nc.scalar.copy if on_scalar else nc.vector.tensor_copy
+            copy(out=w_grp_view[:, 2 * g:2 * g + 2], in_=bank_of("wT%d" % g)[:].rearrange("p a t o -> p a o t"))
+            give_back("wT%d" % g)
+
+        def copy_words(g, on_scalar=True):
             n = min(2, TAPS - 2 * g)
-            copy = nc.vector.tensor_copy if g in ON_VECTOR else nc.scalar.copy
+            copy = nc.scalar.copy if on_scalar else nc.vector.tensor_copy
             copy(
-                out=w_grp_view[:, 2 * g:2 * g + n],
-                in_=bank_of("wT%d" % g)[:, 0:n].rearrange("p a t o -> p a o t"),
+                out=w_grp_words[:, 2 * g:2 * g + n],
+                in_=bank_of("wT%d" % g)[:, 0:n].rearrange("p a u o -> p a o u"),
             )
             give_back("wT%d" % g)
 
@@ -235,7 +266,7 @@ def tile_rbf_conv2d_kernel(tc, x, weight, out):
         def mx_taps(b, e, shifted):
             if shifted:
                 return [(3 * i + 2 * e, 1 - e, i) for i in (1, 0, 2)]
-            return [(3 * i + 1, e, i) for i in (1, 0, 2)] + [(3 * i + 2 - 2 * e, 1 - e, i) for i in (1, 0, 2)]
+            return [tap for i in (1, 0, 2) for tap in ((3 * i + 1, e, i), (3 * i + 2 - 2 * e, 1 - e, i))]
 
         def mx_group(b, e, shifted, r0=0, r1=8):
             ps = take_bank("mx%d%d%d%d" % (b, e, shifted, r0), [P, 512], F32)
@@ -309,7 +340,7 @@ def tile_rbf_conv2d_kernel(tc, x, weight, out):
                 eng.tensor_scalar(out=dst, in0=src, scalar1=w2[:, 0:1], scalar2=0.0, op0=ALU.add, op1=ALU.max)
             nc.sync.dma_start(out=out[b].rearrange("o (h r) z -> o h r z", h=4)[:, :, r0:r1, :], in_=res[:])
 
-        warm_up(4)
+        warm_up(3)
         gram(0, 0)
         gram(0, 1)
         group_x(0, 0, 0)
@@ -319,37 +350,50 @@ def tile_rbf_conv2d_kernel(tc, x, weight, out):
         group_x(0, 1, 0)
         group_x(0, 1, 1)
         for g in range(5):
-            take_bank("wT%d" % g, [P, 2, 4, P], BF16)
-        for t, ch in enumerate((2, 3, 6, 7)):
-            transpose_weights(t)
-            gram(0, ch)
-        square_weights(0)
+            take_bank("wT%d" % g, [P, 2, 2, P], F32)
+        for g in range(4):
+            pair_weights(0, g, True)
+        gram(0, 2)
         quantise_x(0, 0)
         quantise_x(0, 1)
-        square_weights(1)
+        for g in range(4):
+            pair_weights(1, g)
+        warm_up(2)
+        gram(0, 3)
+        for s in range(0, 9, 2):
+            transpose_words(0, s, min(s + 2, 9))
+            if s == 0:
+                warm_up(2)
+                gram(0, 6)
+            transpose_words(1, s, min(s + 2, 9))
+            if s == 4:
+                gram(0, 7)
+        copy_words(0)
         gram_diagonals(0, 0)
-        copy_halo(0)
-        copy_weights(0)
-        copy_weights(1)
         quantise_weights(0)
-        copy_weights(2)
-        copy_weights(3)
-        copy_weights(4)
-        stats_on_tensor(1, range(4))
-        group_x(1, 0, 0)
+        copy_words(1)
+        copy_words(2)
+        copy_halo(0)
         quantise_weights(1)
-        group_x(1, 0, 1)
-        stats_on_tensor(1, range(4, 8))
+        copy_words(3)
+        copy_words(4)
         quantise_weights(2)
-        group_x(1, 1, 0)
+        group_x(1, 0, 0)
+        group_x(1, 0, 1)
         quantise_weights(3)
+        quantise_weights(4)
+        group_x(1, 1, 0)
         group_x(1, 1, 1)
+        stats_on_tensor(1, range(4))
         mx_group(0, 0, 0)
-        square_flipped(1, 0)
+        square_weights(0)
         take_main(0, 0)
+        mx_group(0, 1, 1)
+        stats_on_tensor(1, range(4, 8))
+        square_weights(1)
+        square_flipped(1, 0)
         square_flipped(1, 1)
         square_weights(2)
-        mx_group(0, 1, 1)
         mx_group(0, 0, 1)
         mx_group(0, 1, 0)
         take_main(0, 1)

@@ -310,10 +310,11 @@ def tile_rbf_conv2d_kernel(tc, x, weight, out):
 
         def add_shifted(b, e, r0=0, r1=8):
             key = "mx%d%d1%d" % (b, e, r0)
-            for k in range(r0 // 4, r1 // 4):
-                lo = 256 * k - 64 * r0
-                a3 = acc[b][k][:, e, :].rearrange("p (s m) -> p s m", m=16)
-                p3 = bank_of(key)[:, lo:lo + 256].rearrange("p (s m) -> p s m", m=16)
+            for r in range(r0, r1, 4):
+                n, lo = 64 * min(4, r1 - r), 64 * (r - r0)
+                at = 64 * (r % 4)
+                a3 = acc[b][r // 4][:, e, at:at + n].rearrange("p (s m) -> p s m", m=16)
+                p3 = bank_of(key)[:, lo:lo + n].rearrange("p (s m) -> p s m", m=16)
                 dst, src = (a3[:, :, 0:15], p3[:, :, 1:16]) if e else (a3[:, :, 1:16], p3[:, :, 0:15])
                 nc.vector.scalar_tensor_tensor(out=dst, in0=src, scalar=-2.0, in1=dst, op0=ALU.mult, op1=ALU.add)
             give_back(key)
@@ -384,15 +385,14 @@ def tile_rbf_conv2d_kernel(tc, x, weight, out):
         quantise_weights(4)
         group_x(1, 1, 0)
         group_x(1, 1, 1)
-        stats_on_tensor(1, range(4))
+        stats_on_tensor(1, range(8))
         mx_group(0, 0, 0)
         square_weights(0)
+        square_flipped(1, 0)
         take_main(0, 0)
         mx_group(0, 1, 1)
-        stats_on_tensor(1, range(4, 8))
-        square_weights(1)
-        square_flipped(1, 0)
         square_flipped(1, 1)
+        square_weights(1)
         square_weights(2)
         mx_group(0, 0, 1)
         mx_group(0, 1, 0)
@@ -408,21 +408,21 @@ def tile_rbf_conv2d_kernel(tc, x, weight, out):
         mx_group(1, 0, 0, 0, 4)
         take_main(1, 0, 0, 4)
         mx_group(1, 1, 0, 0, 4)
-        take_main(1, 1, 0, 4)
         mx_group(1, 0, 1, 0, 4)
-        mx_group(1, 1, 1, 0, 4)
         box_sum()
         nc.scalar.copy(out=x2[:], in_=bank_of("box")[:])
         give_back("box")
+        take_main(1, 1, 0, 4)
         square_weights(3)
+        mx_group(1, 1, 1, 0, 4)
         add_shifted(1, 0, 0, 4)
         add_shifted(1, 1, 0, 4)
-        mx_group(1, 0, 0, 4, 8)
         for b, k in ((0, 0), (0, 1), (1, 1), (1, 0)):
             spread_x2(b, k)
-        nc.vector.tensor_reduce(out=w2[:], in_=w2_parts[:], axis=AX.X, op=ALU.add)
+        mx_group(1, 0, 0, 4, 8)
         for k in range(2):
             add_x2(0, k)
+        nc.vector.tensor_reduce(out=w2[:], in_=w2_parts[:], axis=AX.X, op=ALU.add)
         copy_x2(1, 1)
         finish(0, 0, 4, "S")
         finish(0, 4, 8, "S")
@@ -432,8 +432,10 @@ def tile_rbf_conv2d_kernel(tc, x, weight, out):
         add_main(1, 0, 4, 8)
         mx_group(1, 0, 1, 4, 8)
         add_main(1, 1, 4, 8)
-        mx_group(1, 1, 1, 4, 8)
+        mx_group(1, 1, 1, 4, 6)
+        mx_group(1, 1, 1, 6, 8)
         add_shifted(1, 0, 4, 8)
-        add_shifted(1, 1, 4, 8)
-        finish(1, 4, 6, "V")
-        finish(1, 6, 8, "S")
+        add_shifted(1, 1, 4, 6)
+        finish(1, 4, 6, "S")
+        add_shifted(1, 1, 6, 8)
+        finish(1, 6, 8, "V")

@@ -181,16 +181,16 @@ def tile_rbf_conv2d_kernel(tc, x, weight, out):
             )
 
         def group_x(b, half, e, on_scalar=False):
-            dst = grp[b][e][:].rearrange("p (r h m t) -> p h r m t", r=8, h=4, t=4)
-            src = raw[b][half][:].rearrange("p t (h r m e) -> p e h r m t", h=2, r=8, e=2)[:, e]
-            if on_scalar:
-                for h in range(2):
-                    nc.scalar.copy(out=dst[:, 2 * half + h], in_=src[:, h])
-            else:
-                nc.vector.tensor_copy(
-                    out=dst[:, 2 * half:2 * half + 2].rearrange("p h r m t -> p r h m t"),
-                    in_=src.rearrange("p h r m t -> p r h m t"),
-                )
+            for h in range(2):
+                dst = grp[b][e][:].rearrange("p (r h n) -> p h r n", r=8, h=4)[:, 2 * half + h]
+                src = raw[b][half][:].rearrange("p t (h r m e) -> p h e t r m", h=2, r=8, e=2)[:, h, e]
+                if on_scalar:
+                    nc.scalar.copy(out=dst.rearrange("p r (m t) -> p r m t", t=4), in_=src.rearrange("p t r m -> p r m t"))
+                else:
+                    nc.vector.tensor_copy(
+                        out=dst.rearrange("p r (c i t) -> p r c t i", i=4, t=4),
+                        in_=src.rearrange("p t r (c i) -> p r c t i", i=4),
+                    )
 
         def quantise_x(b, e):
             c0 = PLANE * e + 64

@@ -184,13 +184,11 @@ def tile_rbf_conv2d_kernel(tc, x, weight, out):
             for h in range(2):
                 dst = grp[b][e][:].rearrange("p (r h n) -> p h r n", r=8, h=4)[:, 2 * half + h]
                 src = raw[b][half][:].rearrange("p t (h r m e) -> p h e t r m", h=2, r=8, e=2)[:, h, e]
-                if on_scalar:
-                    nc.scalar.copy(out=dst.rearrange("p r (m t) -> p r m t", t=4), in_=src.rearrange("p t r m -> p r m t"))
-                else:
-                    nc.vector.tensor_copy(
-                        out=dst.rearrange("p r (c i t) -> p r c t i", i=4, t=4),
-                        in_=src.rearrange("p t r (c i) -> p r c t i", i=4),
-                    )
+                copy = nc.scalar.copy if on_scalar else nc.vector.tensor_copy
+                copy(
+                    out=dst.rearrange("p r (c i t) -> p r c t i", i=4, t=4),
+                    in_=src.rearrange("p t r (c i) -> p r c t i", i=4),
+                )
 
         def quantise_x(b, e):
             c0 = PLANE * e + 64
@@ -239,15 +237,17 @@ def tile_rbf_conv2d_kernel(tc, x, weight, out):
                 )
             give_back("flip%d%d" % (b, k))
 
-        def gram_diagonals(b, k):
+        def gram_diagonals(b, k, q0=0, q1=4):
             g = bank_of("gram%d%d" % (b, k))
-            for q, ch in enumerate(GRAM[b][4 * k:4 * k + 4]):
+            for q in range(q0, q1):
+                ch = GRAM[b][4 * k + q]
                 junk = scrap.tile([P, P], F32, name="junk_g")
                 nc.vector.scalar_tensor_tensor(
                     out=junk[:], in0=g[:, q, :], scalar=1.0, in1=ident[:],
                     op0=ALU.mult, op1=ALU.mult, accum_out=s_dve[:, b, 1 + ch:2 + ch],
                 )
-            give_back("gram%d%d" % (b, k))
+            if q1 == 4:
+                give_back("gram%d%d" % (b, k))
 
         def box_sum():
             f = take_bank("box", [P, B, 8], F32)
@@ -258,10 +258,17 @@ def tile_rbf_conv2d_kernel(tc, x, weight, out):
                 )
 
         def spread_x2(b, k):
-            xb = take_bank("x2_%d%d" % (b, k), [P, 4, P], F32)
+            xb = take_bank("x2_%d%d" % (b, k), [P, 512], F32)
+            rows = xb[:].rearrange("p (r h z) -> p r h z", r=4, h=4)
             for h in range(4):
                 ch = 2 * h + k
-                nc.tensor.transpose(xb[:, h, :], x2[:, b, ch:ch + 1].to_broadcast([P, P]), ident[:])
+                nc.tensor.transpose(rows[:, :, h, :], x2[:, b, ch:ch + 1].to_broadcast([P, P]), ident[:])
+
+        def spread_planes(b, k):
+            return bank_of("x2_%d%d" % (b, k))[:].rearrange("p (n m e) -> p e n m", m=16, e=2)
+
+        def acc_planes(b, k):
+            return acc[b][k][:].rearrange("p e (n m) -> p e n m", m=16)
 
         def mx_taps(b, e, shifted):
             if shifted:
@@ -295,9 +302,7 @@ def tile_rbf_conv2d_kernel(tc, x, weight, out):
             give_back(key)
 
         def copy_x2(b, k):
-            nc.scalar.copy(
-                out=half_planes(b, k), in_=bank_of("x2_%d%d" % (b, k))[:].rearrange("p h (r m e) -> p r h m e", r=4, e=2)
-            )
+            nc.scalar.copy(out=acc_planes(b, k), in_=spread_planes(b, k))
             give_back("x2_%d%d" % (b, k))
 
         def add_main(b, e, r0=0, r1=8):
@@ -323,10 +328,7 @@ def tile_rbf_conv2d_kernel(tc, x, weight, out):
             return acc[b][k][:].rearrange("p e (r h m) -> p r h m e", r=4, h=4)
 
         def add_x2(b, k):
-            view = half_planes(b, k)
-            nc.vector.tensor_tensor(
-                out=view, in0=bank_of("x2_%d%d" % (b, k))[:].rearrange("p h (r m e) -> p r h m e", r=4, e=2), in1=view, op=ALU.add
-            )
+            nc.vector.tensor_tensor(out=acc_planes(b, k), in0=spread_planes(b, k), in1=acc_planes(b, k), op=ALU.add)
             give_back("x2_%d%d" % (b, k))
 
         def finish(b, r0, r1, engine):
@@ -399,8 +401,9 @@ def tile_rbf_conv2d_kernel(tc, x, weight, out):
         take_main(0, 1)
         quantise_x(1, 0)
         quantise_x(1, 1)
+        gram_diagonals(0, 1, 0, 1)
         copy_halo(1)
-        gram_diagonals(0, 1)
+        gram_diagonals(0, 1, 1, 4)
         gram_diagonals(1, 0)
         nc.vector.tensor_tensor(out=s_sum[:], in0=s_act[:], in1=s_dve[:], op=ALU.add)
         add_shifted(0, 0)

@@ -24,10 +24,10 @@ TAP_ORDER = [3 * i + j for i in (1, 0, 2) for j in (1, 2)] + [3, 0, 6]
 TAP_GROUPS = (slice(4, 6), slice(1, 3), slice(7, 9), slice(0, 9, 3))
 GROUP_OF_SLOT = ((0, 0), (0, 1), (1, 0), (1, 1), (2, 0), (2, 1), (3, 1), (3, 0), (3, 2))
 ON_VECTOR = (1,)
+W2_PIECES = ((0, slice(0, 2304)), (1, slice(0, 1152)), (1, slice(1152, 2304)))
 GRAM = ((0, 1, 2, 3, 4, 5, 6, 7), (0, 2, 4, 6))
 FLIP = ((), (1, 3, 5, 7))
 PLANE = 10 * 64
-W_PIECE = KD // 4
 W_QUANT = ((0, 1024), (1024, 1024), (2048, 1024), (3072, 1024), (4096, 512))
 
 
@@ -39,7 +39,7 @@ def tile_rbf_conv2d_kernel(tc, x, weight, out):
         psum = ctx.enter_context(tc.psum_pool(name="psum", bufs=1))
         ctx.enter_context(tc.manual_schedule())
 
-        w_raw = keep.tile([P, KD], BF16, name="w_raw")
+        w_raw = [keep.tile([P, KD // 2], BF16, name="w_raw%d" % u) for u in range(2)]
         raw = [[keep.tile([P, 4, 512], BF16, name="raw%d%d" % (b, k)) for k in range(2)] for b in range(B)]
 
         def load_x(b, k):
@@ -50,8 +50,7 @@ def tile_rbf_conv2d_kernel(tc, x, weight, out):
                 )
 
         def load_w(u):
-            cols = slice(KD // 2 * u, KD // 2 * (u + 1))
-            nc.sync.dma_start(out=w_raw[:, cols], in_=weight[:, cols])
+            nc.sync.dma_start(out=w_raw[u][:], in_=weight[:, KD // 2 * u:KD // 2 * (u + 1)])
 
         load_x(0, 0)
         load_x(0, 1)
@@ -95,20 +94,19 @@ def tile_rbf_conv2d_kernel(tc, x, weight, out):
 
         s_sum = keep.tile([P, B, 10], F32, name="s_sum")
         x2 = keep.tile([P, B, 8], F32, name="x2")
-        w2_parts = keep.tile([P, 4], F32, name="w2_parts")
         w2 = keep.tile([P, 1], F32, name="w2")
-        w_by_parity = w_raw[:].rearrange("o (u p e a) -> o u e a p", u=2, e=2, a=TAPS)
-        w_by_tap = w_raw[:].rearrange("o (u c a) -> o u a c", u=2, a=TAPS)
+        w_by_tap = [w_raw[u][:].rearrange("o (c a) -> o a c", a=TAPS) for u in range(2)]
         w_pairs = {}
         for u in range(2):
             for g in range(4):
                 w_pairs[u, g] = keep.tile([P, 2 + g // 3, 256], BF16, name="w_pairs%d%d" % (u, g))
         w_grp = keep.tile([P, KD], BF16, name="w_grp", align_bytes=64)
-        w_grp_view = w_grp[:].rearrange("p (a o t) -> p a o t", o=P, t=4)
         w_grp_words = w_grp[:].bitcast(F32).rearrange("p (a o u) -> p a o u", o=P, u=2)
         w_codes = keep.tile([P, TAPS * P], U32, name="w_codes", align_bytes=64)
         w_scales = keep.tile([P, TAPS * P], U8, name="w_scales", align_bytes=64)
-        acc = [[keep.tile([P, 2, 256], F32, name="acc%d%d" % (b, k)) for k in range(2)] for b in range(B)]
+        acc_whole = keep.tile([P, 2, 512], F32, name="acc0")
+        acc_halves = [keep.tile([P, 2, 256], F32, name="acc1%d" % k) for k in range(2)]
+        w2_parts = keep.tile([P, 3], F32, name="w2_parts")
 
         free_banks = list(range(8))
         held = {}
@@ -131,37 +129,28 @@ def tile_rbf_conv2d_kernel(tc, x, weight, out):
             give_back("warm")
 
         def square_weights(i):
-            junk = scrap.tile([P, W_PIECE], BF16, name="junk_w")
+            u, cols = W2_PIECES[i]
+            junk = scrap.tile([P, KD // 2], BF16, name="junk_w")
             nc.scalar.activation(
-                out=junk[:], in_=w_raw[:, W_PIECE * i:W_PIECE * (i + 1)], func=ACT.Square,
+                out=junk[:, 0:cols.stop - cols.start], in_=w_raw[u][:, cols], func=ACT.Square,
                 accum_out=w2_parts[:, i:i + 1],
             )
 
         def pair_weights(u, g, on_scalar=False):
             dst = w_pairs[u, g][:].rearrange("o a c -> o c a")
-            src = w_by_tap[:, u, TAP_GROUPS[g], :].rearrange("o a c -> o c a")
+            src = w_by_tap[u][:, TAP_GROUPS[g], :].rearrange("o a c -> o c a")
             if on_scalar:
                 nc.scalar.copy(out=dst, in_=src)
             else:
-                nc.vector.tensor_copy(out=dst, in_=src)
+                for a in range(0, 2 + g // 3, 2):
+                    two = slice(a, min(a + 2, 2 + g // 3))
+                    nc.vector.tensor_copy(out=dst[:, :, two], in_=src[:, :, two])
 
         def transpose_words(u, s0, s1):
             for s in range(s0, s1):
                 g, n = GROUP_OF_SLOT[s]
                 words = w_pairs[u, g][:].rearrange("o a c -> o (a c)").bitcast(F32)
                 nc.tensor.transpose(bank_of("wT%d" % (s // 2))[:, s % 2, u, :], words[:, P * n:P * n + P], ident[:])
-
-        def transpose_direct(u, s0, s1):
-            for s in range(s0, s1):
-                for e in range(2):
-                    nc.tensor.transpose(
-                        bank_of("wT%d" % (s // 2))[:, s % 2, 2 * u + e, :], w_by_parity[:, u, e, TAP_ORDER[s], :], ident_bf[:]
-                    )
-
-        def copy_direct(g, on_scalar=True):
-            copy = nc.scalar.copy if on_scalar else nc.vector.tensor_copy
-            copy(out=w_grp_view[:, 2 * g:2 * g + 2], in_=bank_of("wT%d" % g)[:].rearrange("p a t o -> p a o t"))
-            give_back("wT%d" % g)
 
         def copy_words(g, on_scalar=True):
             n = min(2, TAPS - 2 * g)
@@ -267,8 +256,14 @@ def tile_rbf_conv2d_kernel(tc, x, weight, out):
         def spread_planes(b, k):
             return bank_of("x2_%d%d" % (b, k))[:].rearrange("p (n m e) -> p e n m", m=16, e=2)
 
+        def acc_of(b, r0, r1):
+            if b == 0:
+                return acc_whole[:, :, 64 * r0:64 * r1]
+            k = r0 // 4
+            return acc_halves[k][:, :, 64 * (r0 - 4 * k):64 * (r1 - 4 * k)]
+
         def acc_planes(b, k):
-            return acc[b][k][:].rearrange("p e (n m) -> p e n m", m=16)
+            return acc_of(b, 4 * k, 4 * k + 4).rearrange("p e (n m) -> p e n m", m=16)
 
         def mx_taps(b, e, shifted):
             if shifted:
@@ -294,11 +289,9 @@ def tile_rbf_conv2d_kernel(tc, x, weight, out):
 
         def take_main(b, e, r0=0, r1=8):
             key = "mx%d%d0%d" % (b, e, r0)
-            for k in range(r0 // 4, r1 // 4):
-                lo = 256 * k - 64 * r0
-                nc.scalar.activation(
-                    out=acc[b][k][:, e, :], in_=bank_of(key)[:, lo:lo + 256], func=ACT.Identity, scale=-2.0
-                )
+            nc.scalar.activation(
+                out=acc_of(b, r0, r1)[:, e, :], in_=bank_of(key)[:, 0:64 * (r1 - r0)], func=ACT.Identity, scale=-2.0
+            )
             give_back(key)
 
         def copy_x2(b, k):
@@ -307,7 +300,7 @@ def tile_rbf_conv2d_kernel(tc, x, weight, out):
 
         def add_main(b, e, r0=0, r1=8):
             key = "mx%d%d0%d" % (b, e, r0)
-            a = acc[b][r0 // 4][:, e, :]
+            a = acc_of(b, r0, r1)[:, e, :]
             nc.vector.scalar_tensor_tensor(
                 out=a, in0=bank_of(key)[:, 0:64 * (r1 - r0)], scalar=-2.0, in1=a, op0=ALU.mult, op1=ALU.add
             )
@@ -315,25 +308,19 @@ def tile_rbf_conv2d_kernel(tc, x, weight, out):
 
         def add_shifted(b, e, r0=0, r1=8):
             key = "mx%d%d1%d" % (b, e, r0)
-            for r in range(r0, r1, 4):
-                n, lo = 64 * min(4, r1 - r), 64 * (r - r0)
-                at = 64 * (r % 4)
-                a3 = acc[b][r // 4][:, e, at:at + n].rearrange("p (s m) -> p s m", m=16)
-                p3 = bank_of(key)[:, lo:lo + n].rearrange("p (s m) -> p s m", m=16)
-                dst, src = (a3[:, :, 0:15], p3[:, :, 1:16]) if e else (a3[:, :, 1:16], p3[:, :, 0:15])
-                nc.vector.scalar_tensor_tensor(out=dst, in0=src, scalar=-2.0, in1=dst, op0=ALU.mult, op1=ALU.add)
+            a3 = acc_of(b, r0, r1)[:, e, :].rearrange("p (s m) -> p s m", m=16)
+            p3 = bank_of(key)[:, 0:64 * (r1 - r0)].rearrange("p (s m) -> p s m", m=16)
+            dst, src = (a3[:, :, 0:15], p3[:, :, 1:16]) if e else (a3[:, :, 1:16], p3[:, :, 0:15])
+            nc.vector.scalar_tensor_tensor(out=dst, in0=src, scalar=-2.0, in1=dst, op0=ALU.mult, op1=ALU.add)
             give_back(key)
-
-        def half_planes(b, k):
-            return acc[b][k][:].rearrange("p e (r h m) -> p r h m e", r=4, h=4)
 
         def add_x2(b, k):
             nc.vector.tensor_tensor(out=acc_planes(b, k), in0=spread_planes(b, k), in1=acc_planes(b, k), op=ALU.add)
             give_back("x2_%d%d" % (b, k))
 
         def finish(b, r0, r1, engine):
-            k, n = r0 // 4, r1 - r0
-            src = half_planes(b, k)[:, r0 - 4 * k:r1 - 4 * k]
+            n = r1 - r0
+            src = acc_of(b, r0, r1).rearrange("p e (r h m) -> p r h m e", h=4, m=16)
             res = keep.tile([P, 4, n, 32], F32, name="res%d%d" % (b, r0))
             dst = res[:].rearrange("p h r (m e) -> p r h m e", e=2)
             if engine == "S":
@@ -395,7 +382,6 @@ def tile_rbf_conv2d_kernel(tc, x, weight, out):
         mx_group(0, 1, 1)
         square_flipped(1, 1)
         square_weights(1)
-        square_weights(2)
         mx_group(0, 0, 1)
         mx_group(0, 1, 0)
         take_main(0, 1)
@@ -416,7 +402,7 @@ def tile_rbf_conv2d_kernel(tc, x, weight, out):
         nc.scalar.copy(out=x2[:], in_=bank_of("box")[:])
         give_back("box")
         take_main(1, 1, 0, 4)
-        square_weights(3)
+        square_weights(2)
         mx_group(1, 1, 1, 0, 4)
         add_shifted(1, 0, 0, 4)
         add_shifted(1, 1, 0, 4)

from contextlib import ExitStack

import concourse.mybir as mybir
from concourse.masks import make_identity

FLOPS = 2 * 2048 * 128 * 4608

F32 = mybir.dt.float32
BF16 = mybir.dt.bfloat16
I32 = mybir.dt.int32
U32 = mybir.dt.uint32
U8 = mybir.dt.uint8
FP8X4 = mybir.dt.float8_e4m3fn_x4
ALU = mybir.AluOpType
ACT = mybir.ActivationFunctionType
AX = mybir.AxisListType

P = 128
B = 2
HW = 1024
KD = 4608
TAPS = 9
TAP_ORDER = [3 * i + j for i in (1, 0, 2) for j in (1, 2)] + [3, 0, 6]
TAP_GROUPS = (slice(4, 6), slice(1, 3), slice(7, 9), slice(0, 9, 3))
GROUP_OF_SLOT = ((0, 0), (0, 1), (1, 0), (1, 1), (2, 0), (2, 1), (3, 1), (3, 0), (3, 2))
ON_VECTOR = (1,)
W2_PIECES = ((0, slice(0, 2304)), (1, slice(0, 1152)), (1, slice(1152, 2304)))
GRAM = ((0, 1, 2, 3, 4, 5, 6, 7), (0, 2, 4, 6))
FLIP = ((), (1, 3, 5, 7))
PLANE = 10 * 64
W_QUANT = ((0, 1024), (1024, 1024), (2048, 1024), (3072, 1024), (4096, 512))


def tile_rbf_conv2d_kernel(tc, x, weight, out):
    nc = tc.nc
    with ExitStack() as ctx:
        keep = ctx.enter_context(tc.tile_pool(name="keep", bufs=1))
        scrap = ctx.enter_context(tc.tile_pool(name="scrap", bufs=2))
        psum = ctx.enter_context(tc.psum_pool(name="psum", bufs=1))
        ctx.enter_context(tc.manual_schedule())

        w_raw = [keep.tile([P, KD // 2], BF16, name="w_raw%d" % u) for u in range(2)]
        raw = [[keep.tile([P, 4, 512], BF16, name="raw%d%d" % (b, k)) for k in range(2)] for b in range(B)]

        def load_x(b, k):
            for u in range(2):
                nc.sync.dma_start(
                    out=raw[b][k][:, 2 * u:2 * u + 2, :],
                    in_=x[b].rearrange("(u p e) h w -> u p e (h w)", u=2, e=2)[u, :, :, 512 * k:512 * k + 512],
                )

        def load_w(u):
            nc.sync.dma_start(out=w_raw[u][:], in_=weight[:, KD // 2 * u:KD // 2 * (u + 1)])

        load_x(0, 0)
        load_x(0, 1)
        load_w(0)
        load_w(1)
        load_x(1, 0)
        load_x(1, 1)

        ident = keep.tile([P, P], F32, name="ident")
        make_identity(nc, ident[:])
        band = keep.tile([P, 3 * P], F32, name="band")
        nc.gpsimd.memset(band[:], 0.0)
        s_act = keep.tile([P, B, 10], F32, name="s_act")
        nc.gpsimd.memset(s_act[:], 0.0)
        s_dve = keep.tile([P, B, 10], F32, name="s_dve")
        nc.gpsimd.memset(s_dve[:], 0.0)
        grp = []
        x_codes = []
        x_scales = []
        for b in range(B):
            grp.append([keep.tile([P, HW * 2], BF16, name="grp%d%d" % (b, e), align_bytes=64) for e in range(2)])
            x_codes.append(keep.tile([P, 2 * PLANE], U32, name="x_codes%d" % b, align_bytes=64))
            x_scales.append(keep.tile([P, 2 * PLANE], U8, name="x_scales%d" % b, align_bytes=64))
            nc.gpsimd.memset(x_scales[b][:].bitcast(U32), 0)
            planes = x_codes[b][:].rearrange("p (e r n) -> p e r n", e=2, r=10)
            nc.gpsimd.memset(planes[:, :, 0, 0:16], 0)
            nc.gpsimd.memset(planes[:, :, 9, 48:64], 0)
        ident_bf = keep.tile([P, P], BF16, name="ident_bf")
        nc.vector.tensor_copy(out=ident_bf[:], in_=ident[:])
        id3 = ident[:].rearrange("p (a z) -> p a z", z=32)
        tri = keep.tile([P, 4, 32], F32, name="tri")
        nc.vector.tensor_copy(out=tri[:], in_=id3)
        nc.vector.tensor_tensor(out=tri[:, :, 1:32], in0=tri[:, :, 1:32], in1=id3[:, :, 0:31], op=ALU.add)
        nc.vector.tensor_tensor(out=tri[:, :, 0:31], in0=tri[:, :, 0:31], in1=id3[:, :, 1:32], op=ALU.add)
        for dy in (-1, 0, 1):
            lo = P + 32 * dy
            nc.vector.tensor_tensor(
                out=band[:, lo:lo + P], in0=band[:, lo:lo + P],
                in1=tri[:].rearrange("p a z -> p (a z)"), op=ALU.add,
            )

        s_sum = keep.tile([P, B, 10], F32, name="s_sum")
        x2 = keep.tile([P, B, 8], F32, name="x2")
        w2 = keep.tile([P, 1], F32, name="w2")
        w_by_tap = [w_raw[u][:].rearrange("o (c a) -> o a c", a=TAPS) for u in range(2)]
        w_pairs = {}
        for u in range(2):
            for g in range(4):
                w_pairs[u, g] = keep.tile([P, 2 + g // 3, 256], BF16, name="w_pairs%d%d" % (u, g))
        w_grp = keep.tile([P, KD], BF16, name="w_grp", align_bytes=64)
        w_grp_words = w_grp[:].bitcast(F32).rearrange("p (a o u) -> p a o u", o=P, u=2)
        w_codes = keep.tile([P, TAPS * P], U32, name="w_codes", align_bytes=64)
        w_scales = keep.tile([P, TAPS * P], U8, name="w_scales", align_bytes=64)
        acc_whole = keep.tile([P, 2, 512], F32, name="acc0")
        acc_halves = [keep.tile([P, 2, 256], F32, name="acc1%d" % k) for k in range(2)]
        w2_parts = keep.tile([P, 3], F32, name="w2_parts")

        free_banks = list(range(8))
        held = {}

        def take_bank(key, shape, dtype):
            k = free_banks.pop(0)
            held[key] = (psum.tile(shape, dtype, name="ps_%s" % key, tag="bank%d" % k), k)
            return held[key][0]

        def bank_of(key):
            return held[key][0]

        def give_back(key):
            free_banks.append(held[key][1])

        def warm_up(n):
            junk = take_bank("warm", [P, P], F32)
            for i in range(n):
                nc.tensor.matmul(junk[:], lhsT=ident[:], rhs=ident[:], start=True, stop=True)
            give_back("warm")

        def square_weights(i):
            u, cols = W2_PIECES[i]
            junk = scrap.tile([P, KD // 2], BF16, name="junk_w")
            nc.scalar.activation(
                out=junk[:, 0:cols.stop - cols.start], in_=w_raw[u][:, cols], func=ACT.Square,
                accum_out=w2_parts[:, i:i + 1],
            )

        def pair_weights(u, g, on_scalar=False):
            dst = w_pairs[u, g][:].rearrange("o a c -> o c a")
            src = w_by_tap[u][:, TAP_GROUPS[g], :].rearrange("o a c -> o c a")
            if on_scalar:
                nc.scalar.copy(out=dst, in_=src)
            else:
                for a in range(0, 2 + g // 3, 2):
                    two = slice(a, min(a + 2, 2 + g // 3))
                    nc.vector.tensor_copy(out=dst[:, :, two], in_=src[:, :, two])

        def transpose_words(u, s0, s1):
            for s in range(s0, s1):
                g, n = GROUP_OF_SLOT[s]
                words = w_pairs[u, g][:].rearrange("o a c -> o (a c)").bitcast(F32)
                nc.tensor.transpose(bank_of("wT%d" % (s // 2))[:, s % 2, u, :], words[:, P * n:P * n + P], ident[:])

        def copy_words(g, on_scalar=True):
            n = min(2, TAPS - 2 * g)
            copy = nc.scalar.copy if on_scalar else nc.vector.tensor_copy
            copy(
                out=w_grp_words[:, 2 * g:2 * g + n],
                in_=bank_of("wT%d" % g)[:, 0:n].rearrange("p a u o -> p a o u"),
            )
            give_back("wT%d" % g)

        def quantise_weights(i):
            lo, n = W_QUANT[i]
            nc.vector.quantize_mx(
                out=w_codes[:, lo // 4:(lo + n) // 4].bitcast(FP8X4),
                scales=w_scales[:, lo // 4:(lo + n) // 4],
                in_=w_grp[:, lo:lo + n],
            )

        def group_x(b, half, e, on_scalar=False):
            for h in range(2):
                dst = grp[b][e][:].rearrange("p (r h n) -> p h r n", r=8, h=4)[:, 2 * half + h]
                src = raw[b][half][:].rearrange("p t (h r m e) -> p h e t r m", h=2, r=8, e=2)[:, h, e]
                copy = nc.scalar.copy if on_scalar else nc.vector.tensor_copy
                copy(
                    out=dst.rearrange("p r (c i t) -> p r c t i", i=4, t=4),
                    in_=src.rearrange("p t r (c i) -> p r c t i", i=4),
                )

        def quantise_x(b, e):
            c0 = PLANE * e + 64
            nc.vector.quantize_mx(
                out=x_codes[b][:, c0:c0 + 512].bitcast(FP8X4),
                scales=x_scales[b][:, c0:c0 + 512],
                in_=grp[b][e][:],
            )

        def copy_halo(b):
            for tile in (x_codes[b][:].bitcast(I32), x_scales[b][:]):
                rows = tile.rearrange("p (e r n) -> p e r n", e=2, r=10)
                nc.vector.tensor_copy(out=rows[:, :, 0, 16:64], in_=rows[:, :, 8, 0:48])
                nc.vector.tensor_copy(out=rows[:, :, 9, 0:48], in_=rows[:, :, 1, 16:64])

        def gram(b, ch):
            k, q = divmod(GRAM[b].index(ch), 4)
            if q == 0:
                take_bank("gram%d%d" % (b, k), [P, 4, P], F32)
            blocks = [raw[b][ch // 4][:, j, ch % 4 * P:(ch % 4 + 1) * P] for j in range(4)]
            for j in range(4):
                nc.tensor.matmul(bank_of("gram%d%d" % (b, k))[:, q, :], lhsT=blocks[j], rhs=blocks[j], start=(j == 0), stop=(j == 3))

        def flip(b, ch):
            k, n = divmod(FLIP[b].index(ch), 2)
            if n == 0:
                take_bank("flip%d%d" % (b, k), [P, 8, P], BF16)
            for j in range(4):
                nc.tensor.transpose(bank_of("flip%d%d" % (b, k))[:, 4 * n + j, :], raw[b][ch // 4][:, j, ch % 4 * P:(ch % 4 + 1) * P], ident_bf[:])

        def stats_on_tensor(b, chunks):
            for ch in chunks:
                if ch in GRAM[b]:
                    gram(b, ch)
                else:
                    flip(b, ch)

        def square_flipped(b, k):
            tp = bank_of("flip%d%d" % (b, k))
            for n in range(2):
                ch = FLIP[b][2 * k + n]
                junk = scrap.tile([P, 4 * P], BF16, name="junk_x")
                nc.scalar.activation(
                    out=junk[:], in_=tp[:, 4 * n:4 * n + 4, :].rearrange("p j c -> p (j c)"), func=ACT.Square,
                    accum_out=s_act[:, b, 1 + ch:2 + ch],
                )
            give_back("flip%d%d" % (b, k))

        def gram_diagonals(b, k, q0=0, q1=4):
            g = bank_of("gram%d%d" % (b, k))
            for q in range(q0, q1):
                ch = GRAM[b][4 * k + q]
                junk = scrap.tile([P, P], F32, name="junk_g")
                nc.vector.scalar_tensor_tensor(
                    out=junk[:], in0=g[:, q, :], scalar=1.0, in1=ident[:],
                    op0=ALU.mult, op1=ALU.mult, accum_out=s_dve[:, b, 1 + ch:2 + ch],
                )
            if q1 == 4:
                give_back("gram%d%d" % (b, k))

        def box_sum():
            f = take_bank("box", [P, B, 8], F32)
            for rel in range(3):
                nc.tensor.matmul(
                    f[:], lhsT=band[:, rel * P:(rel + 1) * P], rhs=s_sum[:, :, 2 - rel:10 - rel],
                    start=(rel == 0), stop=(rel == 2),
                )

        def spread_x2(b, k):
            xb = take_bank("x2_%d%d" % (b, k), [P, 512], F32)
            rows = xb[:].rearrange("p (r h z) -> p r h z", r=4, h=4)
            for h in range(4):
                ch = 2 * h + k
                nc.tensor.transpose(rows[:, :, h, :], x2[:, b, ch:ch + 1].to_broadcast([P, P]), ident[:])

        def spread_planes(b, k):
            return bank_of("x2_%d%d" % (b, k))[:].rearrange("p (n m e) -> p e n m", m=16, e=2)

        def acc_of(b, r0, r1):
            if b == 0:
                return acc_whole[:, :, 64 * r0:64 * r1]
            k = r0 // 4
            return acc_halves[k][:, :, 64 * (r0 - 4 * k):64 * (r1 - 4 * k)]

        def acc_planes(b, k):
            return acc_of(b, 4 * k, 4 * k + 4).rearrange("p e (n m) -> p e n m", m=16)

        def mx_taps(b, e, shifted):
            if shifted:
                return [(3 * i + 2 * e, 1 - e, i) for i in (1, 0, 2)]
            return [tap for i in (1, 0, 2) for tap in ((3 * i + 1, e, i), (3 * i + 2 - 2 * e, 1 - e, i))]

        def mx_group(b, e, shifted, r0=0, r1=8):
            ps = take_bank("mx%d%d%d%d" % (b, e, shifted, r0), [P, 512], F32)
            taps = mx_taps(b, e, shifted)
            for lo in (64 * r0,):
                n = 64 * (r1 - r0)
                for k, (tap, plane, i) in enumerate(taps):
                    w0 = P * TAP_ORDER.index(tap)
                    c0 = PLANE * plane + 64 * i + lo
                    nc.tensor.matmul_mx(
                        out=ps[:, 0:n],
                        lhsT=w_codes[:, w0:w0 + P].bitcast(FP8X4),
                        lhsT_scale=w_scales[:, w0:w0 + P],
                        rhs=x_codes[b][:, c0:c0 + n].bitcast(FP8X4),
                        rhs_scale=x_scales[b][:, c0:c0 + n],
                        start=(k == 0), stop=(k == len(taps) - 1),
                    )

        def take_main(b, e, r0=0, r1=8):
            key = "mx%d%d0%d" % (b, e, r0)
            nc.scalar.activation(
                out=acc_of(b, r0, r1)[:, e, :], in_=bank_of(key)[:, 0:64 * (r1 - r0)], func=ACT.Identity, scale=-2.0
            )
            give_back(key)

        def copy_x2(b, k):
            nc.scalar.copy(out=acc_planes(b, k), in_=spread_planes(b, k))
            give_back("x2_%d%d" % (b, k))

        def add_main(b, e, r0=0, r1=8):
            key = "mx%d%d0%d" % (b, e, r0)
            a = acc_of(b, r0, r1)[:, e, :]
            nc.vector.scalar_tensor_tensor(
                out=a, in0=bank_of(key)[:, 0:64 * (r1 - r0)], scalar=-2.0, in1=a, op0=ALU.mult, op1=ALU.add
            )
            give_back(key)

        def add_shifted(b, e, r0=0, r1=8):
            key = "mx%d%d1%d" % (b, e, r0)
            a3 = acc_of(b, r0, r1)[:, e, :].rearrange("p (s m) -> p s m", m=16)
            p3 = bank_of(key)[:, 0:64 * (r1 - r0)].rearrange("p (s m) -> p s m", m=16)
            dst, src = (a3[:, :, 0:15], p3[:, :, 1:16]) if e else (a3[:, :, 1:16], p3[:, :, 0:15])
            nc.vector.scalar_tensor_tensor(out=dst, in0=src, scalar=-2.0, in1=dst, op0=ALU.mult, op1=ALU.add)
            give_back(key)

        def add_x2(b, k):
            nc.vector.tensor_tensor(out=acc_planes(b, k), in0=spread_planes(b, k), in1=acc_planes(b, k), op=ALU.add)
            give_back("x2_%d%d" % (b, k))

        def finish(b, r0, r1, engine):
            n = r1 - r0
            src = acc_of(b, r0, r1).rearrange("p e (r h m) -> p r h m e", h=4, m=16)
            res = keep.tile([P, 4, n, 32], F32, name="res%d%d" % (b, r0))
            dst = res[:].rearrange("p h r (m e) -> p r h m e", e=2)
            if engine == "S":
                nc.scalar.activation(out=dst, in_=src, func=ACT.Relu, bias=w2[:, 0:1])
            else:
                eng = nc.gpsimd if engine == "G" else nc.vector
                eng.tensor_scalar(out=dst, in0=src, scalar1=w2[:, 0:1], scalar2=0.0, op0=ALU.add, op1=ALU.max)
            nc.sync.dma_start(out=out[b].rearrange("o (h r) z -> o h r z", h=4)[:, :, r0:r1, :], in_=res[:])

        warm_up(3)
        gram(0, 0)
        gram(0, 1)
        group_x(0, 0, 0)
        group_x(0, 0, 1, True)
        gram(0, 4)
        gram(0, 5)
        group_x(0, 1, 0)
        group_x(0, 1, 1)
        for g in range(5):
            take_bank("wT%d" % g, [P, 2, 2, P], F32)
        for g in range(4):
            pair_weights(0, g, True)
        gram(0, 2)
        quantise_x(0, 0)
        quantise_x(0, 1)
        for g in range(4):
            pair_weights(1, g)
        warm_up(2)
        gram(0, 3)
        for s in range(0, 9, 2):
            transpose_words(0, s, min(s + 2, 9))
            if s == 0:
                warm_up(2)
                gram(0, 6)
            transpose_words(1, s, min(s + 2, 9))
            if s == 4:
                gram(0, 7)
        copy_words(0)
        gram_diagonals(0, 0)
        quantise_weights(0)
        copy_words(1)
        copy_words(2)
        copy_halo(0)
        quantise_weights(1)
        copy_words(3)
        copy_words(4)
        quantise_weights(2)
        group_x(1, 0, 0)
        group_x(1, 0, 1)
        quantise_weights(3)
        quantise_weights(4)
        group_x(1, 1, 0)
        group_x(1, 1, 1)
        stats_on_tensor(1, range(8))
        mx_group(0, 0, 0)
        square_weights(0)
        square_flipped(1, 0)
        take_main(0, 0)
        mx_group(0, 1, 1)
        square_flipped(1, 1)
        square_weights(1)
        mx_group(0, 0, 1)
        mx_group(0, 1, 0)
        take_main(0, 1)
        quantise_x(1, 0)
        quantise_x(1, 1)
        gram_diagonals(0, 1, 0, 1)
        copy_halo(1)
        gram_diagonals(0, 1, 1, 4)
        gram_diagonals(1, 0)
        nc.vector.tensor_tensor(out=s_sum[:], in0=s_act[:], in1=s_dve[:], op=ALU.add)
        add_shifted(0, 0)
        add_shifted(0, 1)
        mx_group(1, 0, 0, 0, 4)
        take_main(1, 0, 0, 4)
        mx_group(1, 1, 0, 0, 4)
        mx_group(1, 0, 1, 0, 4)
        box_sum()
        nc.scalar.copy(out=x2[:], in_=bank_of("box")[:])
        give_back("box")
        take_main(1, 1, 0, 4)
        square_weights(2)
        mx_group(1, 1, 1, 0, 4)
        add_shifted(1, 0, 0, 4)
        add_shifted(1, 1, 0, 4)
        for b, k in ((0, 0), (0, 1), (1, 1), (1, 0)):
            spread_x2(b, k)
        mx_group(1, 0, 0, 4, 8)
        for k in range(2):
            add_x2(0, k)
        nc.vector.tensor_reduce(out=w2[:], in_=w2_parts[:], axis=AX.X, op=ALU.add)
        copy_x2(1, 1)
        finish(0, 0, 4, "S")
        finish(0, 4, 8, "S")
        add_x2(1, 0)
        finish(1, 0, 4, "S")
        mx_group(1, 1, 0, 4, 8)
        add_main(1, 0, 4, 8)
        mx_group(1, 0, 1, 4, 8)
        add_main(1, 1, 4, 8)
        mx_group(1, 1, 1, 4, 6)
        mx_group(1, 1, 1, 6, 8)
        add_shifted(1, 0, 4, 8)
        add_shifted(1, 1, 4, 6)
        finish(1, 4, 6, "S")
        add_shifted(1, 1, 6, 8)
        finish(1, 6, 8, "V")
